import numpy as np
import ml_dtypes


def mxq(x, axis, fmt="e4m3"):
    dtype, down = {"e4m3": (ml_dtypes.float8_e4m3fn, 7), "e5m2": (ml_dtypes.float8_e5m2, 14)}[fmt]
    v = np.moveaxis(np.asarray(x, np.float32).astype(ml_dtypes.bfloat16).astype(np.float64), axis, -1)
    blocks = v.reshape(v.shape[:-1] + (-1, 32))
    amax = np.abs(blocks).max(-1, keepdims=True)
    byte = np.maximum(np.where(amax > 0, np.frexp(amax)[1] - 1 + 127, 0) - down, 1)
    scale = np.exp2(byte - 127.0)
    codes = (blocks / scale).astype(np.float32).astype(dtype).astype(np.float64)
    return np.moveaxis((codes * scale).reshape(v.shape), -1, axis)


WIDE = False


def mx_kscale(k):
    if not WIDE:
        return np.ones(k)
    levels = np.array([10, -10, 5, -5, 0])
    a = np.random.permutation(np.resize(levels, k // 512 * 4)).reshape(k // 512, 4)
    idx = np.arange(k)
    return np.exp2(a[idx // 512, idx % 128 // 32])


BF16 = ml_dtypes.bfloat16


def bf(x):
    return np.asarray(x, np.float32).astype(BF16)


def f64(x):
    return np.asarray(x).astype(np.float64)


B, N, F, H = 128, 37, 1024, 1024
M = N - 1


def setup_inputs():
    s = mx_kscale(F)
    w1a = np.random.standard_normal((H, F)) / np.sqrt(F * M)
    w1b = np.random.standard_normal((H, F)) / np.sqrt(F)
    return {"x": bf(np.random.standard_normal((B, N, F)) * s),
            "W1": bf(np.concatenate([w1a / s, w1b / s], axis=1)),
            "W2": bf(np.random.standard_normal((F, H)) / np.sqrt(H * M)),
            "W0": bf(np.random.standard_normal((F, F)) / np.sqrt(F) / s)}


def reference(x, W1, W2, W0):
    x0 = f64(x)[:, 0, :]
    xi = f64(x)[:, 1:, :]
    W1a = f64(W1)[:, :F]
    W1b = f64(W1)[:, F:]
    h0 = x0 @ W1a.T
    hi = mxq(xi, 2, "e4m3") @ mxq(W1b, 1, "e4m3").T
    interact = np.tanh(h0[:, None, :] + hi)
    pooled = interact.sum(axis=1)
    summed = mxq(pooled, 1, "e4m3") @ mxq(f64(W2), 1, "e4m3").T
    return x0 @ f64(W0).T + summed

@@ -1,0 +1,250 @@
+from contextlib import ExitStack
+
+import concourse.mybir as mybir
+from concourse.masks import make_identity
+
+F32 = mybir.dt.float32
+BF16 = mybir.dt.bfloat16
+U32 = mybir.dt.uint32
+U8 = mybir.dt.uint8
+FP8X4 = mybir.dt.float8_e4m3fn_x4
+ADD = mybir.AluOpType.add
+TANH = mybir.ActivationFunctionType.Tanh
+
+P = 128
+NB = 36
+F = 1024
+CH = 4
+NCH = NB // CH
+FLOPS = 2 * 128 * 36 * 1024 * 1024 + 3 * 2 * 128 * 1024 * 1024
+
+SUM_ON_V = (3,)
+
+
+def tile_attention_pa_t_kernel(tc, x, W1, W2, W0, out):
+    nc = tc.nc
+    with ExitStack() as ctx:
+        const = ctx.enter_context(tc.tile_pool(name="const", bufs=1))
+        xin = ctx.enter_context(tc.tile_pool(name="xin", bufs=3))
+        win = ctx.enter_context(tc.tile_pool(name="win", bufs=3))
+        xq = ctx.enter_context(tc.tile_pool(name="xq", bufs=3))
+        zp = ctx.enter_context(tc.tile_pool(name="zp", bufs=6))
+        tp = ctx.enter_context(tc.psum_pool(name="tp", bufs=4))
+        mm = ctx.enter_context(tc.psum_pool(name="mm", bufs=4))
+
+        ident = const.tile([P, P], F32, name="ident")
+        make_identity(nc, ident[:])
+        ident_bf = const.tile([P, P], BF16, name="ident_bf")
+        make_identity(nc, ident_bf[:])
+        warm = const.tile([P, 1], F32, name="warm")
+        nc.vector.memset(warm[:], 0.0)
+        nc.scalar.activation(out=warm[:], in_=warm[:], func=TANH)
+        acc_v = const.tile([P, F], F32, name="acc_v")
+        acc_g = const.tile([P, F], F32, name="acc_g")
+        nc.vector.memset(acc_v[:], 0.0)
+        nc.vector.memset(acc_g[:], 0.0)
+
+        x0n = const.tile([P, F], BF16, name="x0n")
+        x0T = const.tile([P, F], BF16, name="x0T")
+        w1aT = const.tile([P, 4 * F], F32, name="w1aT")
+        w0T = const.tile([P, 4 * F], F32, name="w0T")
+        w1c = const.tile([P, 2 * F], U32, name="w1c", align_bytes=64)
+        w1s = const.tile([P, 2 * F], U8, name="w1s", align_bytes=64)
+        w2c = const.tile([P, 2 * F], U32, name="w2c", align_bytes=64)
+        w2s = const.tile([P, 2 * F], U8, name="w2s", align_bytes=64)
+        h0 = const.tile([P, F], F32, name="h0")
+        r0 = const.tile([P, F], F32, name="r0")
+
+        def copy(on_scalar, dst, src):
+            if on_scalar:
+                nc.scalar.copy(out=dst, in_=src)
+            else:
+                nc.vector.tensor_copy(out=dst, in_=src)
+
+        def load_x(q):
+            t = xin.tile([P, CH * F], BF16, name="xn", tag="xn")
+            nc.sync.dma_start(
+                out=t[:].rearrange("p (i f) -> p i f", i=CH),
+                in_=x[:, 1 + CH * q : 1 + CH * (q + 1), :],
+            )
+            return t
+
+        def load_w(W, t0, nt):
+            t = win.tile([P, 4 * F], BF16, name="wn", tag="wn")
+            nc.sync.dma_start(
+                out=t[:].rearrange("p (t c) -> p t c", t=nt),
+                in_=W.rearrange("(t p) c -> p t c", p=P)[:, t0 : t0 + nt, :],
+            )
+            return t
+
+        def transpose4(words):
+            bank = tp.tile([P, 512], F32, name="tb", tag="tb")
+            for c in range(4):
+                nc.tensor.transpose(bank[:, c * P : (c + 1) * P], words[:, c * P : (c + 1) * P], ident[:])
+            return bank
+
+        def to_plain(on_scalar, dstT, r, bank):
+            copy(
+                on_scalar,
+                dstT[:].rearrange("p (c r) -> p c r", c=4)[:, :, r : r + P],
+                bank[:].rearrange("p (c r) -> p c r", c=4),
+            )
+
+        def to_grouped(on_scalar, dst, bank):
+            copy(on_scalar, dst, bank[:].rearrange("p (g u r) -> p g r u", g=2, u=2))
+
+        def quantise_w(wg, wc, ws, half):
+            for g in range(2):
+                o = g * F + half * 512
+                nc.vector.quantize_mx(
+                    out=wc[:, o : o + 512].bitcast(FP8X4),
+                    scales=ws[:, o : o + 512],
+                    in_=wg[:, 4 * o : 4 * o + 2048],
+                )
+
+        def plain(wT, half, dst):
+            bank = mm.tile([P, 512], F32, name="hb", tag="hb")
+            v = wT[:].bitcast(BF16).rearrange("p (c r e) -> p c r e", c=4, e=2)
+            for n in range(8):
+                nc.tensor.matmul(
+                    out=bank[:],
+                    lhsT=x0T[:, n * P : (n + 1) * P],
+                    rhs=v[:, n // 2, half * 512 : (half + 1) * 512, n % 2],
+                    start=(n == 0),
+                    stop=(n == 7),
+                )
+            nc.scalar.copy(out=dst[:, half * 512 : (half + 1) * 512], in_=bank[:])
+
+        nc.sync.dma_start(out=x0n[:], in_=x[:, 0, :])
+        w1n = [load_w(W1, 0, 2), load_w(W1, 2, 2)]
+        xn = {0: load_x(0)}
+        w1n.append(load_w(W1, 4, 2))
+
+        bank = transpose4(x0n[:].bitcast(F32))
+        nc.vector.tensor_copy(
+            out=x0T[:].rearrange("p (c e b) -> p c e b", c=4, e=2),
+            in_=bank[:].bitcast(BF16).rearrange("p (c b e) -> p c e b", c=4, e=2),
+        )
+
+        w1g = const.tile([P, 8 * F], BF16, name="w1g", tag="wg", align_bytes=64)
+        w1gw = w1g[:].bitcast(F32).rearrange("p (g r u) -> p g r u", g=2, u=2)
+        for ht in range(8):
+            if ht == 4:
+                w1n.append(load_w(W1, 6, 2))
+            words = w1n[ht // 2][:].bitcast(F32)
+            o = (ht % 2) * 1024
+            ba = transpose4(words[:, o : o + 512])
+            bb = transpose4(words[:, o + 512 : o + 1024])
+            to_plain(True, w1aT, ht * P, ba)
+            to_grouped(False, w1gw[:, :, ht * P : (ht + 1) * P, :], bb)
+            if ht % 4 == 3:
+                quantise_w(w1g, w1c, w1s, ht // 4)
+                plain(w1aT, ht // 4, h0)
+
+        def prep_x(q):
+            words = xn[q][:].bitcast(F32)
+            xg = xq.tile([P, CH * F], BF16, name="xg", tag="xg", align_bytes=64)
+            xgw = xg[:].bitcast(F32)
+            for i in range(CH):
+                b = transpose4(words[:, i * 512 : (i + 1) * 512])
+                to_grouped(True, xgw[:, i * 512 : (i + 1) * 512].rearrange("p (g r u) -> p g r u", g=2, u=2), b)
+            xc = xq.tile([P, CH * 256], U32, name="xc", tag="xc", align_bytes=64)
+            xs = xq.tile([P, CH * 256], U8, name="xs", tag="xs", align_bytes=64)
+            nc.vector.quantize_mx(out=xc[:].bitcast(FP8X4), scales=xs[:], in_=xg[:])
+            return xc, xs
+
+        def main(q, xc, xs):
+            for i in range(CH):
+                z = zp.tile([P, F], F32, name="z", tag="z")
+                for hh in range(2):
+                    hb = mm.tile([P, 512], F32, name="hb", tag="hb")
+                    for g in range(2):
+                        o = (i * 2 + g) * P
+                        w = g * F + hh * 512
+                        nc.tensor.matmul_mx(
+                            out=hb[:],
+                            lhsT=xc[:, o : o + P].bitcast(FP8X4),
+                            lhsT_scale=xs[:, o : o + P],
+                            rhs=w1c[:, w : w + 512].bitcast(FP8X4),
+                            rhs_scale=w1s[:, w : w + 512],
+                            start=(g == 0),
+                            stop=(g == 1),
+                        )
+                    nc.vector.tensor_tensor(
+                        out=z[:, hh * 512 : (hh + 1) * 512],
+                        in0=hb[:],
+                        in1=h0[:, hh * 512 : (hh + 1) * 512],
+                        op=ADD,
+                    )
+                nc.scalar.activation(out=z[:], in_=z[:], func=TANH)
+                if i in SUM_ON_V:
+                    nc.vector.tensor_tensor(out=acc_v[:], in0=acc_v[:], in1=z[:], op=ADD)
+                else:
+                    nc.gpsimd.tensor_tensor(out=acc_g[:], in0=acc_g[:], in1=z[:], op=ADD)
+
+        xn[1] = load_x(1)
+        codes = {0: prep_x(0)}
+        w2g = None
+        w2gw = None
+        late = {}
+        for q in range(NCH):
+            if q + 2 < NCH:
+                xn[q + 2] = load_x(q + 2)
+            if q + 1 < NCH:
+                codes[q + 1] = prep_x(q + 1)
+            main(q, codes[q][0], codes[q][1])
+            if q < 8:
+                W = W0 if q < 4 else W2
+                if q % 2 == 0:
+                    late[q // 2] = load_w(W, (q % 4) * 2, 4)
+                if q == 4:
+                    w2g = const.tile([P, 8 * F], BF16, name="w2g", tag="wg", align_bytes=64)
+                    w2gw = w2g[:].bitcast(F32).rearrange("p (g r u) -> p g r u", g=2, u=2)
+                words = late[q // 2][:].bitcast(F32)
+                for k in range(2):
+                    ft = (q % 4) * 2 + k
+                    o = (ft % 4) * 512
+                    b = transpose4(words[:, o : o + 512])
+                    if q < 4:
+                        to_plain(k == 0, w0T, ft * P, b)
+                    else:
+                        to_grouped(k == 0, w2gw[:, :, ft * P : (ft + 1) * P, :], b)
+                if q == 1 or q == 3:
+                    plain(w0T, q // 2, r0)
+                if q == 5 or q == 7:
+                    quantise_w(w2g, w2c, w2s, (q - 4) // 2)
+
+        nc.vector.tensor_tensor(out=acc_v[:], in0=acc_v[:], in1=acc_g[:], op=ADD)
+        pb = const.tile([P, F], BF16, name="pb")
+        nc.vector.tensor_copy(
+            out=pb[:].rearrange("b (c e p) -> b c e p", c=4, e=2),
+            in_=acc_v[:].rearrange("b (c p e) -> b c e p", c=4, e=2),
+        )
+        pt = tp.tile([P, F], BF16, name="pt", tag="tb")
+        for n in range(8):
+            nc.tensor.transpose(pt[:, n * P : (n + 1) * P], pb[:, n * P : (n + 1) * P], ident_bf[:])
+        pg = const.tile([P, F], BF16, name="pg", align_bytes=64)
+        nc.vector.tensor_copy(
+            out=pg[:].rearrange("p (g b t) -> p g b t", g=2, t=4),
+            in_=pt[:].rearrange("p (g t b) -> p g b t", g=2, t=4),
+        )
+        pc = const.tile([P, 256], U32, name="pc", align_bytes=64)
+        ps = const.tile([P, 256], U8, name="ps", align_bytes=64)
+        nc.vector.quantize_mx(out=pc[:].bitcast(FP8X4), scales=ps[:], in_=pg[:])
+        res = const.tile([P, F], F32, name="res")
+        for fh in range(2):
+            ob = mm.tile([P, 512], F32, name="hb", tag="hb")
+            for g in range(2):
+                w = g * F + fh * 512
+                nc.tensor.matmul_mx(
+                    out=ob[:],
+                    lhsT=pc[:, g * P : (g + 1) * P].bitcast(FP8X4),
+                    lhsT_scale=ps[:, g * P : (g + 1) * P],
+                    rhs=w2c[:, w : w + 512].bitcast(FP8X4),
+                    rhs_scale=w2s[:, w : w + 512],
+                    start=(g == 0),
+                    stop=(g == 1),
+                )
+            s = slice(fh * 512, (fh + 1) * 512)
+            nc.vector.tensor_tensor(out=res[:, s], in0=ob[:], in1=r0[:, s], op=ADD)
+            nc.sync.dma_start(out=out[:, s], in_=res[:, s])

@@ -12,23 +12,33 @@ ADD = mybir.AluOpType.add
 TANH = mybir.ActivationFunctionType.Tanh
 
 P = 128
-NB = 36
 F = 1024
-CH = 4
-NCH = NB // CH
+HALF = 512
+NPAIR = 18
 FLOPS = 2 * 128 * 36 * 1024 * 1024 + 3 * 2 * 128 * 1024 * 1024
 
-SUM_ON_V = (3,)
+LAG = 4
+V_UNITS = {0: (), 1: (0, 1, 2, 3, 4, 6, 7, 8, 9, 10, 11, 13, 14, 16, 18, 19)}
+V_COPIES_EARLY = 2
+V_COPIES = 0
+G_WIDTH = 1024
+X_FIRST = 8
+PRO = 3
+FIN0 = 19
+LEAD = 2
 
 
 def tile_attention_pa_t_kernel(tc, x, W1, W2, W0, out):
     nc = tc.nc
     with ExitStack() as ctx:
+        ctx.enter_context(tc.manual_schedule())
         const = ctx.enter_context(tc.tile_pool(name="const", bufs=1))
         xin = ctx.enter_context(tc.tile_pool(name="xin", bufs=3))
         win = ctx.enter_context(tc.tile_pool(name="win", bufs=3))
-        xq = ctx.enter_context(tc.tile_pool(name="xq", bufs=3))
-        zp = ctx.enter_context(tc.tile_pool(name="zp", bufs=6))
+        wst = ctx.enter_context(tc.tile_pool(name="wst", bufs=2))
+        xgp = ctx.enter_context(tc.tile_pool(name="xgp", bufs=4))
+        xcp = ctx.enter_context(tc.tile_pool(name="xcp", bufs=LAG + LEAD + 5))
+        zp = ctx.enter_context(tc.tile_pool(name="zp", bufs=5))
         tp = ctx.enter_context(tc.psum_pool(name="tp", bufs=4))
         mm = ctx.enter_context(tc.psum_pool(name="mm", bufs=4))
 
@@ -39,21 +49,23 @@ def tile_attention_pa_t_kernel(tc, x, W1, W2, W0, out):
         warm = const.tile([P, 1], F32, name="warm")
         nc.vector.memset(warm[:], 0.0)
         nc.scalar.activation(out=warm[:], in_=warm[:], func=TANH)
-        acc_v = const.tile([P, F], F32, name="acc_v")
-        acc_g = const.tile([P, F], F32, name="acc_g")
-        nc.vector.memset(acc_v[:], 0.0)
-        nc.vector.memset(acc_g[:], 0.0)
 
         x0n = const.tile([P, F], BF16, name="x0n")
         x0T = const.tile([P, F], BF16, name="x0T")
-        w1aT = const.tile([P, 4 * F], F32, name="w1aT")
-        w0T = const.tile([P, 4 * F], F32, name="w0T")
-        w1c = const.tile([P, 2 * F], U32, name="w1c", align_bytes=64)
-        w1s = const.tile([P, 2 * F], U8, name="w1s", align_bytes=64)
-        w2c = const.tile([P, 2 * F], U32, name="w2c", align_bytes=64)
-        w2s = const.tile([P, 2 * F], U8, name="w2s", align_bytes=64)
-        h0 = const.tile([P, F], F32, name="h0")
-        r0 = const.tile([P, F], F32, name="r0")
+        wc = {}
+        ws = {}
+        bias = {}
+        for nm in ("w1", "w2"):
+            for hf in range(2):
+                wc[nm, hf] = const.tile([P, F], U32, name="c%s%d" % (nm, hf), align_bytes=64)
+                ws[nm, hf] = const.tile([P, F], U8, name="s%s%d" % (nm, hf), align_bytes=64)
+        for nm in ("w1", "w0"):
+            for hf in range(2):
+                bias[nm, hf] = const.tile([P, HALF], F32, name="b%s%d" % (nm, hf))
+        acc = {}
+        for e in ("g", "v"):
+            for hf in range(2):
+                acc[e, hf] = const.tile([P, F], F32, name="acc%s%d" % (e, hf))
 
         def copy(on_scalar, dst, src):
             if on_scalar:
@@ -61,190 +73,332 @@ def tile_attention_pa_t_kernel(tc, x, W1, W2, W0, out):
             else:
                 nc.vector.tensor_copy(out=dst, in_=src)
 
-        def load_x(q):
-            t = xin.tile([P, CH * F], BF16, name="xn", tag="xn")
-            nc.sync.dma_start(
-                out=t[:].rearrange("p (i f) -> p i f", i=CH),
-                in_=x[:, 1 + CH * q : 1 + CH * (q + 1), :],
-            )
-            return t
+        nat = {}
+        live = {"x": 0, "w": 0}
 
-        def load_w(W, t0, nt):
+        def load_x(q):
+            t = xin.tile([P, 4 * F], BF16, name="xn", tag="xn")
+            nc.sync.dma_start(out=t[:].rearrange("p (i f) -> p i f", i=4), in_=x[:, 1 + 4 * q : 5 + 4 * q, :])
+            nat["x", q] = t
+
+        def load_w(nm, W, j, nt):
             t = win.tile([P, 4 * F], BF16, name="wn", tag="wn")
             nc.sync.dma_start(
                 out=t[:].rearrange("p (t c) -> p t c", t=nt),
-                in_=W.rearrange("(t p) c -> p t c", p=P)[:, t0 : t0 + nt, :],
+                in_=W.rearrange("(t p) c -> p t c", p=P)[:, j * nt : (j + 1) * nt, :],
             )
-            return t
+            nat[nm, j] = t
 
-        def transpose4(words):
-            bank = tp.tile([P, 512], F32, name="tb", tag="tb")
-            for c in range(4):
-                nc.tensor.transpose(bank[:, c * P : (c + 1) * P], words[:, c * P : (c + 1) * P], ident[:])
-            return bank
+        plan = []
 
-        def to_plain(on_scalar, dstT, r, bank):
-            copy(
-                on_scalar,
-                dstT[:].rearrange("p (c r) -> p c r", c=4)[:, :, r : r + P],
-                bank[:].rearrange("p (c r) -> p c r", c=4),
-            )
-
-        def to_grouped(on_scalar, dst, bank):
-            copy(on_scalar, dst, bank[:].rearrange("p (g u r) -> p g r u", g=2, u=2))
-
-        def quantise_w(wg, wc, ws, half):
-            for g in range(2):
-                o = g * F + half * 512
-                nc.vector.quantize_mx(
-                    out=wc[:, o : o + 512].bitcast(FP8X4),
-                    scales=ws[:, o : o + 512],
-                    in_=wg[:, 4 * o : 4 * o + 2048],
-                )
-
-        def plain(wT, half, dst):
-            bank = mm.tile([P, 512], F32, name="hb", tag="hb")
-            v = wT[:].bitcast(BF16).rearrange("p (c r e) -> p c r e", c=4, e=2)
-            for n in range(8):
-                nc.tensor.matmul(
-                    out=bank[:],
-                    lhsT=x0T[:, n * P : (n + 1) * P],
-                    rhs=v[:, n // 2, half * 512 : (half + 1) * 512, n % 2],
-                    start=(n == 0),
-                    stop=(n == 7),
-                )
-            nc.scalar.copy(out=dst[:, half * 512 : (half + 1) * 512], in_=bank[:])
-
-        nc.sync.dma_start(out=x0n[:], in_=x[:, 0, :])
-        w1n = [load_w(W1, 0, 2), load_w(W1, 2, 2)]
-        xn = {0: load_x(0)}
-        w1n.append(load_w(W1, 4, 2))
-
-        bank = transpose4(x0n[:].bitcast(F32))
-        nc.vector.tensor_copy(
-            out=x0T[:].rearrange("p (c e b) -> p c e b", c=4, e=2),
-            in_=bank[:].bitcast(BF16).rearrange("p (c b e) -> p c e b", c=4, e=2),
-        )
-
-        w1g = const.tile([P, 8 * F], BF16, name="w1g", tag="wg", align_bytes=64)
-        w1gw = w1g[:].bitcast(F32).rearrange("p (g r u) -> p g r u", g=2, u=2)
-        for ht in range(8):
-            if ht == 4:
-                w1n.append(load_w(W1, 6, 2))
-            words = w1n[ht // 2][:].bitcast(F32)
-            o = (ht % 2) * 1024
-            ba = transpose4(words[:, o : o + 512])
-            bb = transpose4(words[:, o + 512 : o + 1024])
-            to_plain(True, w1aT, ht * P, ba)
-            to_grouped(False, w1gw[:, :, ht * P : (ht + 1) * P, :], bb)
-            if ht % 4 == 3:
-                quantise_w(w1g, w1c, w1s, ht // 4)
-                plain(w1aT, ht // 4, h0)
-
-        def prep_x(q):
-            words = xn[q][:].bitcast(F32)
-            xg = xq.tile([P, CH * F], BF16, name="xg", tag="xg", align_bytes=64)
-            xgw = xg[:].bitcast(F32)
-            for i in range(CH):
-                b = transpose4(words[:, i * 512 : (i + 1) * 512])
-                to_grouped(True, xgw[:, i * 512 : (i + 1) * 512].rearrange("p (g r u) -> p g r u", g=2, u=2), b)
-            xc = xq.tile([P, CH * 256], U32, name="xc", tag="xc", align_bytes=64)
-            xs = xq.tile([P, CH * 256], U8, name="xs", tag="xs", align_bytes=64)
-            nc.vector.quantize_mx(out=xc[:].bitcast(FP8X4), scales=xs[:], in_=xg[:])
-            return xc, xs
-
-        def main(q, xc, xs):
-            for i in range(CH):
-                z = zp.tile([P, F], F32, name="z", tag="z")
-                for hh in range(2):
-                    hb = mm.tile([P, 512], F32, name="hb", tag="hb")
-                    for g in range(2):
-                        o = (i * 2 + g) * P
-                        w = g * F + hh * 512
-                        nc.tensor.matmul_mx(
-                            out=hb[:],
-                            lhsT=xc[:, o : o + P].bitcast(FP8X4),
-                            lhsT_scale=xs[:, o : o + P],
-                            rhs=w1c[:, w : w + 512].bitcast(FP8X4),
-                            rhs_scale=w1s[:, w : w + 512],
-                            start=(g == 0),
-                            stop=(g == 1),
-                        )
-                    nc.vector.tensor_tensor(
-                        out=z[:, hh * 512 : (hh + 1) * 512],
-                        in0=hb[:],
-                        in1=h0[:, hh * 512 : (hh + 1) * 512],
-                        op=ADD,
-                    )
-                nc.scalar.activation(out=z[:], in_=z[:], func=TANH)
-                if i in SUM_ON_V:
-                    nc.vector.tensor_tensor(out=acc_v[:], in0=acc_v[:], in1=z[:], op=ADD)
+        def pump():
+            while plan and live[plan[0][0]] < 3:
+                kind, nm, j = plan.pop(0)
+                live[kind] += 1
+                if kind == "x":
+                    load_x(j)
+                elif nm == "w1":
+                    load_w(nm, W1, j, 2)
                 else:
-                    nc.gpsimd.tensor_tensor(out=acc_g[:], in0=acc_g[:], in1=z[:], op=ADD)
+                    load_w(nm, W0 if nm == "w0" else W2, j, 4)
 
-        xn[1] = load_x(1)
-        codes = {0: prep_x(0)}
-        w2g = None
-        w2gw = None
-        late = {}
-        for q in range(NCH):
-            if q + 2 < NCH:
-                xn[q + 2] = load_x(q + 2)
-            if q + 1 < NCH:
-                codes[q + 1] = prep_x(q + 1)
-            main(q, codes[q][0], codes[q][1])
-            if q < 8:
-                W = W0 if q < 4 else W2
-                if q % 2 == 0:
-                    late[q // 2] = load_w(W, (q % 4) * 2, 4)
-                if q == 4:
-                    w2g = const.tile([P, 8 * F], BF16, name="w2g", tag="wg", align_bytes=64)
-                    w2gw = w2g[:].bitcast(F32).rearrange("p (g r u) -> p g r u", g=2, u=2)
-                words = late[q // 2][:].bitcast(F32)
-                for k in range(2):
-                    ft = (q % 4) * 2 + k
-                    o = (ft % 4) * 512
-                    b = transpose4(words[:, o : o + 512])
-                    if q < 4:
-                        to_plain(k == 0, w0T, ft * P, b)
-                    else:
-                        to_grouped(k == 0, w2gw[:, :, ft * P : (ft + 1) * P, :], b)
-                if q == 1 or q == 3:
-                    plain(w0T, q // 2, r0)
-                if q == 5 or q == 7:
-                    quantise_w(w2g, w2c, w2s, (q - 4) // 2)
+        stage = {}
 
-        nc.vector.tensor_tensor(out=acc_v[:], in0=acc_v[:], in1=acc_g[:], op=ADD)
-        pb = const.tile([P, F], BF16, name="pb")
-        nc.vector.tensor_copy(
-            out=pb[:].rearrange("b (c e p) -> b c e p", c=4, e=2),
-            in_=acc_v[:].rearrange("b (c p e) -> b c e p", c=4, e=2),
-        )
-        pt = tp.tile([P, F], BF16, name="pt", tag="tb")
-        for n in range(8):
-            nc.tensor.transpose(pt[:, n * P : (n + 1) * P], pb[:, n * P : (n + 1) * P], ident_bf[:])
-        pg = const.tile([P, F], BF16, name="pg", align_bytes=64)
-        nc.vector.tensor_copy(
-            out=pg[:].rearrange("p (g b t) -> p g b t", g=2, t=4),
-            in_=pt[:].rearrange("p (g t b) -> p g b t", g=2, t=4),
-        )
-        pc = const.tile([P, 256], U32, name="pc", align_bytes=64)
-        ps = const.tile([P, 256], U8, name="ps", align_bytes=64)
-        nc.vector.quantize_mx(out=pc[:].bitcast(FP8X4), scales=ps[:], in_=pg[:])
-        res = const.tile([P, F], F32, name="res")
-        for fh in range(2):
-            ob = mm.tile([P, 512], F32, name="hb", tag="hb")
+        def words_of(item):
+            kind, n = item
+            if kind == "x0":
+                return x0n[:].bitcast(F32)
+            if kind == "x":
+                return nat["x", n // 4][:].bitcast(F32)[:, (n % 4) * HALF : (n % 4 + 1) * HALF]
+            if kind == "w1a" or kind == "w1b":
+                o = (n % 2) * F + (HALF if kind == "w1b" else 0)
+                return nat["w1", n // 2][:].bitcast(F32)[:, o : o + HALF]
+            return nat[kind, n // 4][:].bitcast(F32)[:, (n % 4) * HALF : (n % 4 + 1) * HALF]
+
+        def transposes(items):
+            banks = []
+            for item in items:
+                words = words_of(item)
+                bank = tp.tile([P, HALF], F32, name="tb", tag="tb")
+                for c in range(4):
+                    nc.tensor.transpose(bank[:, c * P : (c + 1) * P], words[:, c * P : (c + 1) * P], ident[:])
+                banks.append(bank)
+                kind, n = item
+                if kind == "x" and n % 4 == 3:
+                    live["x"] -= 1
+                if kind == "w1b" and n % 2 == 1:
+                    live["w"] -= 1
+                if (kind == "w0" or kind == "w2") and n % 4 == 3:
+                    live["w"] -= 1
+            pump()
+            return banks
+
+        def empty(item, bank, on_scalar):
+            kind, n = item
+            if kind == "x0":
+                nc.vector.tensor_copy(
+                    out=x0T[:].rearrange("p (c e b) -> p c e b", c=4, e=2),
+                    in_=bank[:].bitcast(BF16).rearrange("p (c b e) -> p c e b", c=4, e=2),
+                )
+            elif kind == "x":
+                if n % 2 == 0:
+                    stage["xg"] = xgp.tile([P, 2 * F], BF16, name="xg", tag="xg", align_bytes=64)
+                dst = stage["xg"][:].bitcast(F32)[:, (n % 2) * HALF : (n % 2 + 1) * HALF]
+                copy(on_scalar, dst.rearrange("p (g r u) -> p g r u", g=2, u=2),
+                     bank[:].rearrange("p (g u r) -> p g r u", g=2, u=2))
+            elif kind == "w1a" or kind == "w0":
+                if n % 4 == 0:
+                    stage[kind] = wst.tile([P, 4 * HALF], F32, name="pT", tag="pT")
+                r = (n % 4) * P
+                copy(on_scalar, stage[kind][:].rearrange("p (c r) -> p c r", c=4)[:, :, r : r + P],
+                     bank[:].rearrange("p (c r) -> p c r", c=4))
+            else:
+                if n % 4 == 0:
+                    stage[kind] = wst.tile([P, 4 * F], BF16, name="wg", tag="wg", align_bytes=64)
+                r = (n % 4) * P
+                dst = stage[kind][:].bitcast(F32).rearrange("p (g r u) -> p g r u", g=2, u=2)
+                copy(on_scalar, dst[:, :, r : r + P, :], bank[:].rearrange("p (g u r) -> p g r u", g=2, u=2))
+
+        def quantise_w(nm, wg, hf):
             for g in range(2):
-                w = g * F + fh * 512
+                nc.vector.quantize_mx(
+                    out=wc[nm, hf][:, g * HALF : (g + 1) * HALF].bitcast(FP8X4),
+                    scales=ws[nm, hf][:, g * HALF : (g + 1) * HALF],
+                    in_=wg[:, g * 2048 : (g + 1) * 2048],
+                )
+
+        codes = {}
+
+        def quantise_x(j, xg):
+            xc = xcp.tile([P, HALF], U32, name="xc", tag="xc", align_bytes=64)
+            xs = xcp.tile([P, HALF], U8, name="xs", tag="xs", align_bytes=64)
+            nc.vector.quantize_mx(out=xc[:].bitcast(FP8X4), scales=xs[:], in_=xg[:])
+            codes[j] = (xc, xs)
+
+        def plain(kind, n, wT):
+            if n % 4 == 0:
+                stage["bank", kind] = mm.tile([P, HALF], F32, name="hb", tag="hb")
+            bank = stage["bank", kind]
+            r = (n % 4) * P
+            v = wT[:].bitcast(BF16).rearrange("p (c r e) -> p c r e", c=4, e=2)
+            for k in range(8):
+                nc.tensor.matmul(out=bank[:, r : r + P], lhsT=x0T[:, k * P : (k + 1) * P],
+                                 rhs=v[:, k // 2, r : r + P, k % 2], start=(k == 0), stop=(k == 7))
+            if n % 4 == 3:
+                nc.scalar.copy(out=bias["w1" if kind == "w1a" else "w0", n // 4][:], in_=bank[:])
+
+        def mx_group(lc, ls, lo, nm, hf):
+            bank = mm.tile([P, HALF], F32, name="hb", tag="hb")
+            for g in range(2):
                 nc.tensor.matmul_mx(
-                    out=ob[:],
-                    lhsT=pc[:, g * P : (g + 1) * P].bitcast(FP8X4),
-                    lhsT_scale=ps[:, g * P : (g + 1) * P],
-                    rhs=w2c[:, w : w + 512].bitcast(FP8X4),
-                    rhs_scale=w2s[:, w : w + 512],
+                    out=bank[:],
+                    lhsT=lc[:, lo + g * P : lo + (g + 1) * P].bitcast(FP8X4),
+                    lhsT_scale=ls[:, lo + g * P : lo + (g + 1) * P],
+                    rhs=wc[nm, hf][:, g * HALF : (g + 1) * HALF].bitcast(FP8X4),
+                    rhs_scale=ws[nm, hf][:, g * HALF : (g + 1) * HALF],
                     start=(g == 0),
                     stop=(g == 1),
                 )
-            s = slice(fh * 512, (fh + 1) * 512)
-            nc.vector.tensor_tensor(out=res[:, s], in0=ob[:], in1=r0[:, s], op=ADD)
-            nc.sync.dma_start(out=out[:, s], in_=res[:, s])
+            return bank
+
+        started = set()
+        pc = const.tile([P, 2 * P], U32, name="pc", align_bytes=64)
+        ps = const.tile([P, 2 * P], U8, name="ps", align_bytes=64)
+        pre = {}
+
+        def tanh(unit, owed):
+            hf, n, z, width = unit
+            e = "v" if n in V_UNITS[hf] else "g"
+            if width == F and (e, hf) not in started:
+                started.add((e, hf))
+                nc.scalar.activation(out=acc[e, hf][:], in_=z[:], func=TANH)
+                return
+            nc.scalar.activation(out=z[:], in_=z[:], func=TANH)
+            if e == "g":
+                for o in range(0, F, G_WIDTH):
+                    nc.gpsimd.tensor_tensor(out=acc[e, hf][:, o : o + G_WIDTH], in0=acc[e, hf][:, o : o + G_WIDTH],
+                                            in1=z[:, o : o + G_WIDTH], op=ADD)
+            else:
+                owed.append(unit)
+
+        def v_sum(unit):
+            hf, n, z, width = unit
+            if width == F:
+                nc.vector.tensor_tensor(out=acc["v", hf][:], in0=acc["v", hf][:], in1=z[:], op=ADD)
+                if hf == 1 and n == NPAIR - 2:
+                    merge(1)
+                    fold(1)
+            elif n == NPAIR:
+                nc.vector.tensor_tensor(out=pre[hf][:], in0=pre[hf][:], in1=z[:], op=ADD)
+            else:
+                round_pooled(hf, pre[hf][:], z[:])
+
+        def merge(hf):
+            if ("v", hf) in started and ("g", hf) in started:
+                a = acc["v", hf]
+                nc.vector.tensor_tensor(out=a[:], in0=a[:], in1=acc["g", hf][:], op=ADD)
+            elif ("g", hf) in started:
+                acc["v", hf] = acc["g", hf]
+
+        def fold(hf):
+            a = acc["v", hf]
+            pre[hf] = const.tile([P, HALF], F32, name="pre%d" % hf)
+            nc.vector.tensor_tensor(out=pre[hf][:], in0=a[:, 0:HALF], in1=a[:, HALF:F], op=ADD)
+
+        def round_pooled(hf, one, other):
+            pb = const.tile([P, HALF], BF16, name="pb%d" % hf)
+            nc.vector.tensor_tensor(
+                out=pb[:].rearrange("b (u e p) -> b u e p", u=2, e=2),
+                in0=one.rearrange("b (u p e) -> b u e p", u=2, e=2),
+                in1=other.rearrange("b (u p e) -> b u e p", u=2, e=2),
+                op=ADD,
+            )
+            pt = tp.tile([P, HALF], BF16, name="pt", tag="tb")
+            for n in range(4):
+                nc.tensor.transpose(pt[:, n * P : (n + 1) * P], pb[:, n * P : (n + 1) * P], ident_bf[:])
+            pg = const.tile([P, HALF], BF16, name="pg%d" % hf, align_bytes=64)
+            nc.scalar.copy(out=pg[:].rearrange("p (b t) -> p b t", t=4), in_=pt[:].rearrange("p (t b) -> p b t", t=4))
+            nc.vector.quantize_mx(out=pc[:, hf * P : (hf + 1) * P].bitcast(FP8X4),
+                                  scales=ps[:, hf * P : (hf + 1) * P], in_=pg[:])
+
+        banks = [("x0", 0)]
+        for n in range(4):
+            banks += [("w1a", n), ("w1b", n)]
+        banks += [("x", n) for n in range(X_FIRST)]
+        for n in range(4, 8):
+            banks += [("w1a", n), ("w1b", n)]
+        wq = [("w0", n) for n in range(8)] + [("w2", n) for n in range(8)]
+        nx = X_FIRST
+        while nx < 2 * NPAIR or wq:
+            rnd = len(banks) // 4 - PRO
+            if nx < 2 * NPAIR and (not wq or nx // 2 <= rnd + LEAD):
+                banks.append(("x", nx))
+                nx += 1
+            else:
+                banks.append(wq.pop(0))
+        bunch = [banks[k : k + 4] for k in range(0, len(banks), 4)]
+        seen = set()
+        for kind, n in banks:
+            if kind == "x":
+                key = ("x", "x", n // 4)
+            elif kind == "w1a" or kind == "w1b":
+                key = ("w", "w1", n // 2)
+            elif kind == "x0":
+                continue
+            else:
+                key = ("w", kind, n // 4)
+            if key not in seen:
+                seen.add(key)
+                plan.append(key)
+
+        nc.sync.dma_start(out=x0n[:], in_=x[:, 0, :])
+        pump()
+
+        def empty_bunch(k, n_v):
+            ready = []
+            for i in range(len(bunch[k])):
+                item = bunch[k][i]
+                empty(item, tb[k][i], i >= n_v)
+                if item[0] == "x" and item[1] % 2 == 1:
+                    ready.append(("qx", item[1] // 2, stage["xg"]))
+                if item[0] == "w1b" and item[1] % 4 == 3:
+                    ready.append(("qw", "w1", stage["w1b"], item[1] // 4))
+                if item[0] == "w2" and item[1] % 4 == 3:
+                    ready.append(("qw", "w2", stage["w2"], item[1] // 4))
+                if item[0] == "w1a" or item[0] == "w0":
+                    ready.append(("mm", item[0], item[1], stage[item[0]]))
+            return ready
+
+        def quantise_ready(ready):
+            for t in ready:
+                if t[0] == "qx":
+                    quantise_x(t[1], t[2])
+                if t[0] == "qw":
+                    quantise_w(t[1], t[2], t[3])
+
+        def multiply_ready(ready):
+            for t in ready:
+                if t[0] == "mm":
+                    plain(t[1], t[2], t[3])
+
+        tb = {0: transposes(bunch[0])}
+        for k in range(PRO):
+            ready = empty_bunch(k, 2)
+            quantise_ready(ready)
+            tb[k + 1] = transposes(bunch[k + 1])
+            multiply_ready(ready)
+
+        second = list(range(NPAIR))
+        owed = []
+        r = 0
+        while r < NPAIR or second:
+            todo = []
+            if r < NPAIR:
+                todo.append((0, r))
+            if r >= LAG:
+                todo.append((1, second.pop(0)))
+                if r >= NPAIR and second:
+                    todo.append((1, second.pop(0)))
+            groups = []
+            for hf, j in todo:
+                for i in range(2):
+                    groups.append((hf, j, mx_group(codes[j][0], codes[j][1], i * 2 * P, "w1", hf)))
+            k = r + PRO
+            ready = empty_bunch(k, V_COPIES_EARLY if r < LAG else V_COPIES) if k < len(bunch) else []
+            now_owed = owed
+            owed = []
+            for n in range(len(groups)):
+                hf, j, bank = groups[n]
+                single = hf == 1 and j == NPAIR - 1
+                if single:
+                    z = zp.tile([P, HALF], F32, name="z1", tag="z1")
+                    unit = (hf, NPAIR + n % 2, z, HALF)
+                    dst = z[:]
+                else:
+                    if n % 2 == 0:
+                        z = zp.tile([P, F], F32, name="z", tag="z")
+                        unit = (hf, j, z, F)
+                    dst = z[:, (n % 2) * HALF : (n % 2 + 1) * HALF]
+                nc.vector.tensor_tensor(out=dst, in0=bank[:], in1=bias["w1", hf][:], op=ADD)
+                if single or n % 2 == 1:
+                    tanh(unit, owed)
+            quantise_ready(ready)
+            for unit in now_owed:
+                v_sum(unit)
+            if r == FIN0:
+                merge(0)
+                round_pooled(0, acc["v", 0][:, 0:HALF], acc["v", 0][:, HALF:F])
+            multiply_ready(ready)
+            if k + 1 < len(bunch):
+                tb[k + 1] = transposes(bunch[k + 1])
+            r += 1
+
+        obs = []
+        for fh in range(2):
+            ob = mm.tile([P, HALF], F32, name="hb", tag="hb")
+            obs.append(ob)
+
+        def second_pass(g):
+            for fh in range(2):
+                nc.tensor.matmul_mx(
+                    out=obs[fh][:],
+                    lhsT=pc[:, g * P : (g + 1) * P].bitcast(FP8X4),
+                    lhsT_scale=ps[:, g * P : (g + 1) * P],
+                    rhs=wc["w2", fh][:, g * HALF : (g + 1) * HALF].bitcast(FP8X4),
+                    rhs_scale=ws["w2", fh][:, g * HALF : (g + 1) * HALF],
+                    start=(g == 0),
+                    stop=(g == 1),
+                )
+
+        second_pass(0)
+        for unit in owed:
+            v_sum(unit)
+        second_pass(1)
+        res = const.tile([P, F], F32, name="res")
+        for fh in range(2):
+            s = slice(fh * HALF, (fh + 1) * HALF)
+            nc.vector.tensor_tensor(out=res[:, s], in0=obs[fh][:], in1=bias["w0", fh][:], op=ADD)
+            if fh == 0:
+                nc.sync.dma_start(out=out[:, s], in_=res[:, s])
+            else:
+                nc.scalar.dma_start(out=out[:, s], in_=res[:, s])

@@ -18,14 +18,14 @@ NPAIR = 18
 FLOPS = 2 * 128 * 36 * 1024 * 1024 + 3 * 2 * 128 * 1024 * 1024
 
 LAG = 4
-V_UNITS = {0: (), 1: (0, 1, 2, 3, 4, 6, 7, 8, 9, 10, 11, 13, 14, 16, 18, 19)}
-V_COPIES_EARLY = 2
-V_COPIES = 0
-G_WIDTH = 1024
-X_FIRST = 8
-PRO = 3
-FIN0 = 19
-LEAD = 2
+ENG = {0: "gggggggggggggpgggg", 1: "vvvvvgpppgpppppppppp"}
+FLUSH1 = 18
+V_COPIES = "30201110101000000000000"
+G_WIDTH = 512
+X_FIRST = 10
+PRO = 4
+FIN0 = 18
+LEAD = 4
 
 
 def tile_attention_pa_t_kernel(tc, x, W1, W2, W0, out):
@@ -37,15 +37,14 @@ def tile_attention_pa_t_kernel(tc, x, W1, W2, W0, out):
         win = ctx.enter_context(tc.tile_pool(name="win", bufs=3))
         wst = ctx.enter_context(tc.tile_pool(name="wst", bufs=2))
         xgp = ctx.enter_context(tc.tile_pool(name="xgp", bufs=4))
-        xcp = ctx.enter_context(tc.tile_pool(name="xcp", bufs=LAG + LEAD + 5))
-        zp = ctx.enter_context(tc.tile_pool(name="zp", bufs=5))
+        xcp = ctx.enter_context(tc.tile_pool(name="xcp", bufs=LAG + LEAD + 3))
+        zp = ctx.enter_context(tc.tile_pool(name="zp", bufs=7))
         tp = ctx.enter_context(tc.psum_pool(name="tp", bufs=4))
-        mm = ctx.enter_context(tc.psum_pool(name="mm", bufs=4))
+        mm = ctx.enter_context(tc.psum_pool(name="mm", bufs=3))
+        atp = ctx.enter_context(tc.psum_pool(name="at", bufs=1))
 
         ident = const.tile([P, P], F32, name="ident")
         make_identity(nc, ident[:])
-        ident_bf = const.tile([P, P], BF16, name="ident_bf")
-        make_identity(nc, ident_bf[:])
         warm = const.tile([P, 1], F32, name="warm")
         nc.vector.memset(warm[:], 0.0)
         nc.scalar.activation(out=warm[:], in_=warm[:], func=TANH)
@@ -78,14 +77,20 @@ def tile_attention_pa_t_kernel(tc, x, W1, W2, W0, out):
 
         def load_x(q):
             t = xin.tile([P, 4 * F], BF16, name="xn", tag="xn")
-            nc.sync.dma_start(out=t[:].rearrange("p (i f) -> p i f", i=4), in_=x[:, 1 + 4 * q : 5 + 4 * q, :])
+            v = t[:].rearrange("p (i f) -> p i f", i=4)
+            if q == 0:
+                nc.sync.dma_start(out=v[:, 0:2, :], in_=x[:, 1:3, :])
+                nc.sync.dma_start(out=v[:, 2:4, :], in_=x[:, 3:5, :])
+            else:
+                nc.sync.dma_start(out=v, in_=x[:, 1 + 4 * q : 5 + 4 * q, :])
             nat["x", q] = t
 
         def load_w(nm, W, j, nt):
             t = win.tile([P, 4 * F], BF16, name="wn", tag="wn")
             nc.sync.dma_start(
                 out=t[:].rearrange("p (t c) -> p t c", t=nt),
-                in_=W.rearrange("(t p) c -> p t c", p=P)[:, j * nt : (j + 1) * nt, :],
+                in_=W1.rearrange("(j p e) c -> j p e c", p=P, e=2)[j] if nm == "w1"
+                else W.rearrange("(t p) c -> p t c", p=P)[:, j * nt : (j + 1) * nt, :],
             )
             nat[nm, j] = t
 
@@ -159,12 +164,13 @@ def tile_attention_pa_t_kernel(tc, x, W1, W2, W0, out):
                 dst = stage[kind][:].bitcast(F32).rearrange("p (g r u) -> p g r u", g=2, u=2)
                 copy(on_scalar, dst[:, :, r : r + P, :], bank[:].rearrange("p (g u r) -> p g r u", g=2, u=2))
 
-        def quantise_w(nm, wg, hf):
+        def quantise_w(nm, wg, n):
+            r = (n % 4) * P
             for g in range(2):
                 nc.vector.quantize_mx(
-                    out=wc[nm, hf][:, g * HALF : (g + 1) * HALF].bitcast(FP8X4),
-                    scales=ws[nm, hf][:, g * HALF : (g + 1) * HALF],
-                    in_=wg[:, g * 2048 : (g + 1) * 2048],
+                    out=wc[nm, n // 4][:, g * HALF + r : g * HALF + r + P].bitcast(FP8X4),
+                    scales=ws[nm, n // 4][:, g * HALF + r : g * HALF + r + P],
+                    in_=wg[:, g * 2048 + 4 * r : g * 2048 + 4 * r + HALF],
                 )
 
         codes = {}
@@ -176,16 +182,13 @@ def tile_attention_pa_t_kernel(tc, x, W1, W2, W0, out):
             codes[j] = (xc, xs)
 
         def plain(kind, n, wT):
-            if n % 4 == 0:
-                stage["bank", kind] = mm.tile([P, HALF], F32, name="hb", tag="hb")
-            bank = stage["bank", kind]
+            bank = mm.tile([P, P], F32, name="hq", tag="hb")
             r = (n % 4) * P
             v = wT[:].bitcast(BF16).rearrange("p (c r e) -> p c r e", c=4, e=2)
             for k in range(8):
-                nc.tensor.matmul(out=bank[:, r : r + P], lhsT=x0T[:, k * P : (k + 1) * P],
+                nc.tensor.matmul(out=bank[:], lhsT=x0T[:, k * P : (k + 1) * P],
                                  rhs=v[:, k // 2, r : r + P, k % 2], start=(k == 0), stop=(k == 7))
-            if n % 4 == 3:
-                nc.scalar.copy(out=bias["w1" if kind == "w1a" else "w0", n // 4][:], in_=bank[:])
+            nc.scalar.copy(out=bias["w1" if kind == "w1a" else "w0", n // 4][:, r : r + P], in_=bank[:])
 
         def mx_group(lc, ls, lo, nm, hf):
             bank = mm.tile([P, HALF], F32, name="hb", tag="hb")
@@ -204,60 +207,56 @@ def tile_attention_pa_t_kernel(tc, x, W1, W2, W0, out):
         started = set()
         pc = const.tile([P, 2 * P], U32, name="pc", align_bytes=64)
         ps = const.tile([P, 2 * P], U8, name="ps", align_bytes=64)
-        pre = {}
+        accT = {}
+        holds = {("p", 0): [], ("p", 1): []}
 
-        def tanh(unit, owed):
+        def tanh(unit, v_owed, p_owed):
             hf, n, z, width = unit
-            e = "v" if n in V_UNITS[hf] else "g"
-            if width == F and (e, hf) not in started:
+            e = ENG[hf][n]
+            assert e == "p" or hf not in flushed
+            if e != "p" and (e, hf) not in started:
                 started.add((e, hf))
                 nc.scalar.activation(out=acc[e, hf][:], in_=z[:], func=TANH)
+                holds[e, hf] = [n]
                 return
             nc.scalar.activation(out=z[:], in_=z[:], func=TANH)
             if e == "g":
                 for o in range(0, F, G_WIDTH):
                     nc.gpsimd.tensor_tensor(out=acc[e, hf][:, o : o + G_WIDTH], in0=acc[e, hf][:, o : o + G_WIDTH],
                                             in1=z[:, o : o + G_WIDTH], op=ADD)
+                holds[e, hf].append(n)
+            elif e == "v":
+                v_owed.append(unit)
             else:
-                owed.append(unit)
+                p_owed.append(unit)
 
         def v_sum(unit):
             hf, n, z, width = unit
-            if width == F:
-                nc.vector.tensor_tensor(out=acc["v", hf][:], in0=acc["v", hf][:], in1=z[:], op=ADD)
-                if hf == 1 and n == NPAIR - 2:
-                    merge(1)
-                    fold(1)
-            elif n == NPAIR:
-                nc.vector.tensor_tensor(out=pre[hf][:], in0=pre[hf][:], in1=z[:], op=ADD)
-            else:
-                round_pooled(hf, pre[hf][:], z[:])
+            nc.vector.tensor_tensor(out=acc["v", hf][:], in0=acc["v", hf][:], in1=z[:], op=ADD)
+            holds["v", hf].append(n)
 
-        def merge(hf):
-            if ("v", hf) in started and ("g", hf) in started:
-                a = acc["v", hf]
-                nc.vector.tensor_tensor(out=a[:], in0=a[:], in1=acc["g", hf][:], op=ADD)
-            elif ("g", hf) in started:
-                acc["v", hf] = acc["g", hf]
+        def pe_sum(hf, src, width, last):
+            first = hf not in accT
+            if first:
+                accT[hf] = atp.tile([P, HALF], F32, name="at") if hf == 1 else tp.tile([P, HALF], F32, name="at0", tag="tb")
+            nblk = width // P
+            for k in range(nblk):
+                t = k % 4
+                nc.tensor.matmul(out=accT[hf][:, t * P : (t + 1) * P], lhsT=src[:, k * P : (k + 1) * P], rhs=ident[:],
+                                 is_transpose=True, start=(first and k == 0), stop=(last and k == nblk - 1))
 
-        def fold(hf):
-            a = acc["v", hf]
-            pre[hf] = const.tile([P, HALF], F32, name="pre%d" % hf)
-            nc.vector.tensor_tensor(out=pre[hf][:], in0=a[:, 0:HALF], in1=a[:, HALF:F], op=ADD)
+        flushed = set()
 
-        def round_pooled(hf, one, other):
-            pb = const.tile([P, HALF], BF16, name="pb%d" % hf)
-            nc.vector.tensor_tensor(
-                out=pb[:].rearrange("b (u e p) -> b u e p", u=2, e=2),
-                in0=one.rearrange("b (u p e) -> b u e p", u=2, e=2),
-                in1=other.rearrange("b (u p e) -> b u e p", u=2, e=2),
-                op=ADD,
-            )
-            pt = tp.tile([P, HALF], BF16, name="pt", tag="tb")
-            for n in range(4):
-                nc.tensor.transpose(pt[:, n * P : (n + 1) * P], pb[:, n * P : (n + 1) * P], ident_bf[:])
+        def flush(hf, last):
+            flushed.add(hf)
+            todo = [e for e in ("g", "v") if (e, hf) in started]
+            for e in todo:
+                pe_sum(hf, acc[e, hf], F, last and e == todo[-1])
+                holds["p", hf] += holds[e, hf]
+
+        def quantise_pooled(hf):
             pg = const.tile([P, HALF], BF16, name="pg%d" % hf, align_bytes=64)
-            nc.scalar.copy(out=pg[:].rearrange("p (b t) -> p b t", t=4), in_=pt[:].rearrange("p (t b) -> p b t", t=4))
+            nc.scalar.copy(out=pg[:].rearrange("p (b t) -> p b t", t=4), in_=accT[hf][:].rearrange("p (t b) -> p b t", t=4))
             nc.vector.quantize_mx(out=pc[:, hf * P : (hf + 1) * P].bitcast(FP8X4),
                                   scales=ps[:, hf * P : (hf + 1) * P], in_=pg[:])
 
@@ -270,13 +269,13 @@ def tile_attention_pa_t_kernel(tc, x, W1, W2, W0, out):
         wq = [("w0", n) for n in range(8)] + [("w2", n) for n in range(8)]
         nx = X_FIRST
         while nx < 2 * NPAIR or wq:
-            rnd = len(banks) // 4 - PRO
+            rnd = (len(banks) + 3) // 4 - PRO
             if nx < 2 * NPAIR and (not wq or nx // 2 <= rnd + LEAD):
                 banks.append(("x", nx))
                 nx += 1
             else:
                 banks.append(wq.pop(0))
-        bunch = [banks[k : k + 4] for k in range(0, len(banks), 4)]
+        bunch = [banks[0:1]] + [banks[k : k + 4] for k in range(1, len(banks), 4)]
         seen = set()
         for kind, n in banks:
             if kind == "x":
@@ -301,10 +300,8 @@ def tile_attention_pa_t_kernel(tc, x, W1, W2, W0, out):
                 empty(item, tb[k][i], i >= n_v)
                 if item[0] == "x" and item[1] % 2 == 1:
                     ready.append(("qx", item[1] // 2, stage["xg"]))
-                if item[0] == "w1b" and item[1] % 4 == 3:
-                    ready.append(("qw", "w1", stage["w1b"], item[1] // 4))
-                if item[0] == "w2" and item[1] % 4 == 3:
-                    ready.append(("qw", "w2", stage["w2"], item[1] // 4))
+                if item[0] == "w1b" or item[0] == "w2":
+                    ready.append(("qw", item[0][0:2], stage[item[0]], item[1]))
                 if item[0] == "w1a" or item[0] == "w0":
                     ready.append(("mm", item[0], item[1], stage[item[0]]))
             return ready
@@ -325,11 +322,16 @@ def tile_attention_pa_t_kernel(tc, x, W1, W2, W0, out):
         for k in range(PRO):
             ready = empty_bunch(k, 2)
             quantise_ready(ready)
-            tb[k + 1] = transposes(bunch[k + 1])
-            multiply_ready(ready)
+            if k == 1:
+                multiply_ready(ready)
+            if k + 1 < PRO:
+                tb[k + 1] = transposes(bunch[k + 1])
+            if k != 1:
+                multiply_ready(ready)
 
         second = list(range(NPAIR))
-        owed = []
+        v_owed = []
+        p_owed = []
         r = 0
         while r < NPAIR or second:
             todo = []
@@ -343,15 +345,29 @@ def tile_attention_pa_t_kernel(tc, x, W1, W2, W0, out):
             for hf, j in todo:
                 for i in range(2):
                     groups.append((hf, j, mx_group(codes[j][0], codes[j][1], i * 2 * P, "w1", hf)))
+            for hf, n, z, width in p_owed:
+                pe_sum(hf, z, width, False)
+                holds["p", hf].append(n)
+            p_owed = []
+            if r == FIN0:
+                assert not [u for u in v_owed if u[0] == 0] and r >= NPAIR
+                flush(0, True)
+            if r == FLUSH1:
+                assert not [u for u in v_owed if u[0] == 1]
+                flush(1, False)
             k = r + PRO
-            ready = empty_bunch(k, V_COPIES_EARLY if r < LAG else V_COPIES) if k < len(bunch) else []
-            now_owed = owed
-            owed = []
+            ready = []
+            if r == 0:
+                tb[k] = transposes(bunch[k])
+            elif k < len(bunch):
+                ready = empty_bunch(k, int(V_COPIES[r]))
+            now_owed = v_owed
+            v_owed = []
             for n in range(len(groups)):
                 hf, j, bank = groups[n]
                 single = hf == 1 and j == NPAIR - 1
                 if single:
-                    z = zp.tile([P, HALF], F32, name="z1", tag="z1")
+                    z = zp.tile([P, HALF], F32, name="z1", tag="z1", bufs=2)
                     unit = (hf, NPAIR + n % 2, z, HALF)
                     dst = z[:]
                 else:
@@ -361,13 +377,14 @@ def tile_attention_pa_t_kernel(tc, x, W1, W2, W0, out):
                     dst = z[:, (n % 2) * HALF : (n % 2 + 1) * HALF]
                 nc.vector.tensor_tensor(out=dst, in0=bank[:], in1=bias["w1", hf][:], op=ADD)
                 if single or n % 2 == 1:
-                    tanh(unit, owed)
+                    tanh(unit, v_owed, p_owed)
+            if r == 0:
+                ready = empty_bunch(k, int(V_COPIES[r]))
             quantise_ready(ready)
             for unit in now_owed:
                 v_sum(unit)
             if r == FIN0:
-                merge(0)
-                round_pooled(0, acc["v", 0][:, 0:HALF], acc["v", 0][:, HALF:F])
+                quantise_pooled(0)
             multiply_ready(ready)
             if k + 1 < len(bunch):
                 tb[k + 1] = transposes(bunch[k + 1])
@@ -391,8 +408,13 @@ def tile_attention_pa_t_kernel(tc, x, W1, W2, W0, out):
                 )
 
         second_pass(0)
-        for unit in owed:
-            v_sum(unit)
+        for i in range(len(p_owed)):
+            hf, n, z, width = p_owed[i]
+            pe_sum(hf, z, width, i == len(p_owed) - 1)
+            holds["p", hf].append(n)
+        assert sorted(holds["p", 0]) == list(range(NPAIR))
+        assert sorted(holds["p", 1]) == list(range(NPAIR - 1)) + [NPAIR, NPAIR + 1]
+        quantise_pooled(1)
         second_pass(1)
         res = const.tile([P, F], F32, name="res")
         for fh in range(2):

@@ -17,15 +17,16 @@ HALF = 512
 NPAIR = 18
 FLOPS = 2 * 128 * 36 * 1024 * 1024 + 3 * 2 * 128 * 1024 * 1024
 
-LAG = 4
-ENG = {0: "gggggggggggggpgggg", 1: "vvvvvgpppgpppppppppp"}
-FLUSH1 = 18
-V_COPIES = "30201110101000000000000"
+LAG = 5
+ENG = {0: "gggvggggvgvggpgggg", 1: "vgpgggvgpgpppppppppp"}
+FLUSH1 = 17
+V_COPIES = "30211110110000000000000"
 G_WIDTH = 512
 X_FIRST = 10
-PRO = 4
-FIN0 = 18
-LEAD = 4
+FIRST_SIZES = (1, 2, 2, 2, 2, 2, 2)
+PRO = 6
+FIN0 = 19
+LEAD = 5
 
 
 def tile_attention_pa_t_kernel(tc, x, W1, W2, W0, out):
@@ -35,7 +36,7 @@ def tile_attention_pa_t_kernel(tc, x, W1, W2, W0, out):
         const = ctx.enter_context(tc.tile_pool(name="const", bufs=1))
         xin = ctx.enter_context(tc.tile_pool(name="xin", bufs=3))
         win = ctx.enter_context(tc.tile_pool(name="win", bufs=3))
-        wst = ctx.enter_context(tc.tile_pool(name="wst", bufs=2))
+        wst = ctx.enter_context(tc.tile_pool(name="wst", bufs=6))
         xgp = ctx.enter_context(tc.tile_pool(name="xgp", bufs=4))
         xcp = ctx.enter_context(tc.tile_pool(name="xcp", bufs=LAG + LEAD + 3))
         zp = ctx.enter_context(tc.tile_pool(name="zp", bufs=7))
@@ -87,6 +88,12 @@ def tile_attention_pa_t_kernel(tc, x, W1, W2, W0, out):
 
         def load_w(nm, W, j, nt):
             t = win.tile([P, 4 * F], BF16, name="wn", tag="wn")
+            nat[nm, j] = t
+            if nm == "w1" and j < 2:
+                for e in range(2):
+                    nc.sync.dma_start(out=t[:, e * 2 * F : (e + 1) * 2 * F],
+                                      in_=W1.rearrange("(j p e) c -> j e p c", p=P, e=2)[j, e])
+                return
             nc.sync.dma_start(
                 out=t[:].rearrange("p (t c) -> p t c", t=nt),
                 in_=W1.rearrange("(j p e) c -> j p e c", p=P, e=2)[j] if nm == "w1"
@@ -152,17 +159,12 @@ def tile_attention_pa_t_kernel(tc, x, W1, W2, W0, out):
                 copy(on_scalar, dst.rearrange("p (g r u) -> p g r u", g=2, u=2),
                      bank[:].rearrange("p (g u r) -> p g r u", g=2, u=2))
             elif kind == "w1a" or kind == "w0":
-                if n % 4 == 0:
-                    stage[kind] = wst.tile([P, 4 * HALF], F32, name="pT", tag="pT")
-                r = (n % 4) * P
-                copy(on_scalar, stage[kind][:].rearrange("p (c r) -> p c r", c=4)[:, :, r : r + P],
-                     bank[:].rearrange("p (c r) -> p c r", c=4))
+                stage[kind] = wst.tile([P, HALF], F32, name="pT", tag="pT")
+                copy(on_scalar, stage[kind][:], bank[:])
             else:
-                if n % 4 == 0:
-                    stage[kind] = wst.tile([P, 4 * F], BF16, name="wg", tag="wg", align_bytes=64)
-                r = (n % 4) * P
-                dst = stage[kind][:].bitcast(F32).rearrange("p (g r u) -> p g r u", g=2, u=2)
-                copy(on_scalar, dst[:, :, r : r + P, :], bank[:].rearrange("p (g u r) -> p g r u", g=2, u=2))
+                stage[kind] = wst.tile([P, F], BF16, name="wg", tag="wg", align_bytes=64)
+                copy(on_scalar, stage[kind][:].bitcast(F32).rearrange("p (g r u) -> p g r u", g=2, u=2),
+                     bank[:].rearrange("p (g u r) -> p g r u", g=2, u=2))
 
         def quantise_w(nm, wg, n):
             r = (n % 4) * P
@@ -170,7 +172,7 @@ def tile_attention_pa_t_kernel(tc, x, W1, W2, W0, out):
                 nc.vector.quantize_mx(
                     out=wc[nm, n // 4][:, g * HALF + r : g * HALF + r + P].bitcast(FP8X4),
                     scales=ws[nm, n // 4][:, g * HALF + r : g * HALF + r + P],
-                    in_=wg[:, g * 2048 + 4 * r : g * 2048 + 4 * r + HALF],
+                    in_=wg[:, g * HALF : (g + 1) * HALF],
                 )
 
         codes = {}
@@ -181,14 +183,21 @@ def tile_attention_pa_t_kernel(tc, x, W1, W2, W0, out):
             nc.vector.quantize_mx(out=xc[:].bitcast(FP8X4), scales=xs[:], in_=xg[:])
             codes[j] = (xc, xs)
 
+        unpaid = []
+
+        def pay():
+            while unpaid:
+                dst, bank = unpaid.pop(0)
+                nc.scalar.copy(out=dst, in_=bank[:])
+
         def plain(kind, n, wT):
             bank = mm.tile([P, P], F32, name="hq", tag="hb")
             r = (n % 4) * P
             v = wT[:].bitcast(BF16).rearrange("p (c r e) -> p c r e", c=4, e=2)
             for k in range(8):
                 nc.tensor.matmul(out=bank[:], lhsT=x0T[:, k * P : (k + 1) * P],
-                                 rhs=v[:, k // 2, r : r + P, k % 2], start=(k == 0), stop=(k == 7))
-            nc.scalar.copy(out=bias["w1" if kind == "w1a" else "w0", n // 4][:, r : r + P], in_=bank[:])
+                                 rhs=v[:, k // 2, :, k % 2], start=(k == 0), stop=(k == 7))
+            unpaid.append((bias["w1" if kind == "w1a" else "w0", n // 4][:, r : r + P], bank))
 
         def mx_group(lc, ls, lo, nm, hf):
             bank = mm.tile([P, HALF], F32, name="hb", tag="hb")
@@ -260,22 +269,28 @@ def tile_attention_pa_t_kernel(tc, x, W1, W2, W0, out):
             nc.vector.quantize_mx(out=pc[:, hf * P : (hf + 1) * P].bitcast(FP8X4),
                                   scales=ps[:, hf * P : (hf + 1) * P], in_=pg[:])
 
-        banks = [("x0", 0)]
+        first = [("x0", 0)]
         for n in range(4):
-            banks += [("w1a", n), ("w1b", n)]
-        banks += [("x", n) for n in range(X_FIRST)]
+            first += [("w1a", n), ("w1b", n)]
+        first += [("x", n) for n in range(X_FIRST)]
         for n in range(4, 8):
-            banks += [("w1a", n), ("w1b", n)]
+            first += [("w1a", n), ("w1b", n)]
         wq = [("w0", n) for n in range(8)] + [("w2", n) for n in range(8)]
         nx = X_FIRST
-        while nx < 2 * NPAIR or wq:
-            rnd = (len(banks) + 3) // 4 - PRO
-            if nx < 2 * NPAIR and (not wq or nx // 2 <= rnd + LEAD):
-                banks.append(("x", nx))
-                nx += 1
-            else:
-                banks.append(wq.pop(0))
-        bunch = [banks[0:1]] + [banks[k : k + 4] for k in range(1, len(banks), 4)]
+        bunch = []
+        while first or nx < 2 * NPAIR or wq:
+            size = FIRST_SIZES[len(bunch)] if len(bunch) < len(FIRST_SIZES) else 4
+            items = []
+            while len(items) < size and (first or nx < 2 * NPAIR or wq):
+                if first:
+                    items.append(first.pop(0))
+                elif nx < 2 * NPAIR and (not wq or nx // 2 <= len(bunch) - PRO + LEAD):
+                    items.append(("x", nx))
+                    nx += 1
+                else:
+                    items.append(wq.pop(0))
+            bunch.append(items)
+        banks = [item for items in bunch for item in items]
         seen = set()
         for kind, n in banks:
             if kind == "x":
@@ -304,6 +319,7 @@ def tile_attention_pa_t_kernel(tc, x, W1, W2, W0, out):
                     ready.append(("qw", item[0][0:2], stage[item[0]], item[1]))
                 if item[0] == "w1a" or item[0] == "w0":
                     ready.append(("mm", item[0], item[1], stage[item[0]]))
+            pay()
             return ready
 
         def quantise_ready(ready):
@@ -320,14 +336,11 @@ def tile_attention_pa_t_kernel(tc, x, W1, W2, W0, out):
 
         tb = {0: transposes(bunch[0])}
         for k in range(PRO):
-            ready = empty_bunch(k, 2)
+            ready = empty_bunch(k, 1)
             quantise_ready(ready)
-            if k == 1:
-                multiply_ready(ready)
             if k + 1 < PRO:
                 tb[k + 1] = transposes(bunch[k + 1])
-            if k != 1:
-                multiply_ready(ready)
+            multiply_ready(ready)
 
         second = list(range(NPAIR))
         v_owed = []
@@ -359,6 +372,7 @@ def tile_attention_pa_t_kernel(tc, x, W1, W2, W0, out):
             ready = []
             if r == 0:
                 tb[k] = transposes(bunch[k])
+                pay()
             elif k < len(bunch):
                 ready = empty_bunch(k, int(V_COPIES[r]))
             now_owed = v_owed
@@ -386,6 +400,7 @@ def tile_attention_pa_t_kernel(tc, x, W1, W2, W0, out):
             if r == FIN0:
                 quantise_pooled(0)
             multiply_ready(ready)
+            pay()
             if k + 1 < len(bunch):
                 tb[k + 1] = transposes(bunch[k + 1])
             r += 1

@@ -18,7 +18,7 @@ NPAIR = 18
 FLOPS = 2 * 128 * 36 * 1024 * 1024 + 3 * 2 * 128 * 1024 * 1024
 
 LAG = 5
-ENG = {0: "gggvggggvgvggpgggg", 1: "vgpgggvgpgpppppppppp"}
+ENG = {0: "gggvggggvgvggpgpvg", 1: "vgpvggvgpghphphpfppp"}
 FLUSH1 = 17
 V_COPIES = "30211110110000000000000"
 G_WIDTH = 512
@@ -222,8 +222,8 @@ def tile_attention_pa_t_kernel(tc, x, W1, W2, W0, out):
         def tanh(unit, v_owed, p_owed):
             hf, n, z, width = unit
             e = ENG[hf][n]
-            assert e == "p" or hf not in flushed
-            if e != "p" and (e, hf) not in started:
+            assert e in "pfh" or hf not in folded
+            if e in "gv" and (e, hf) not in started:
                 started.add((e, hf))
                 nc.scalar.activation(out=acc[e, hf][:], in_=z[:], func=TANH)
                 holds[e, hf] = [n]
@@ -234,13 +234,20 @@ def tile_attention_pa_t_kernel(tc, x, W1, W2, W0, out):
                     nc.gpsimd.tensor_tensor(out=acc[e, hf][:, o : o + G_WIDTH], in0=acc[e, hf][:, o : o + G_WIDTH],
                                             in1=z[:, o : o + G_WIDTH], op=ADD)
                 holds[e, hf].append(n)
-            elif e == "v":
+            elif e == "v" or (e == "h" and width == F):
                 v_owed.append(unit)
+            elif e == "f" and width == F:
+                nc.gpsimd.tensor_tensor(out=z[:, 0:HALF], in0=z[:, 0:HALF], in1=z[:, HALF:F], op=ADD)
+                p_owed.append((hf, n, z, HALF))
             else:
                 p_owed.append(unit)
 
         def v_sum(unit):
             hf, n, z, width = unit
+            if ENG[hf][n] == "h":
+                nc.vector.tensor_tensor(out=z[:, 0:HALF], in0=z[:, 0:HALF], in1=z[:, HALF:F], op=ADD)
+                p_late.append((hf, n, z, HALF))
+                return
             nc.vector.tensor_tensor(out=acc["v", hf][:], in0=acc["v", hf][:], in1=z[:], op=ADD)
             holds["v", hf].append(n)
 
@@ -254,13 +261,21 @@ def tile_attention_pa_t_kernel(tc, x, W1, W2, W0, out):
                 nc.tensor.matmul(out=accT[hf][:, t * P : (t + 1) * P], lhsT=src[:, k * P : (k + 1) * P], rhs=ident[:],
                                  is_transpose=True, start=(first and k == 0), stop=(last and k == nblk - 1))
 
-        flushed = set()
+        folded = set()
+        p_late = []
+
+        def fold(hf):
+            folded.add(hf)
+            for e in ("g", "v"):
+                if (e, hf) in started:
+                    a = acc[e, hf]
+                    nc.gpsimd.tensor_tensor(out=a[:, 0:HALF], in0=a[:, 0:HALF], in1=a[:, HALF:F], op=ADD)
 
         def flush(hf, last):
-            flushed.add(hf)
+            assert hf in folded
             todo = [e for e in ("g", "v") if (e, hf) in started]
             for e in todo:
-                pe_sum(hf, acc[e, hf], F, last and e == todo[-1])
+                pe_sum(hf, acc[e, hf], HALF, last and e == todo[-1])
                 holds["p", hf] += holds[e, hf]
 
         def quantise_pooled(hf):
@@ -363,11 +378,15 @@ def tile_attention_pa_t_kernel(tc, x, W1, W2, W0, out):
                 holds["p", hf].append(n)
             p_owed = []
             if r == FIN0:
-                assert not [u for u in v_owed if u[0] == 0] and r >= NPAIR
                 flush(0, True)
             if r == FLUSH1:
-                assert not [u for u in v_owed if u[0] == 1]
                 flush(1, False)
+            if r == FIN0 - 1:
+                assert not [u for u in v_owed if u[0] == 0 and ENG[0][u[1]] == "v"] and r >= NPAIR
+                fold(0)
+            if r == FLUSH1 - 1:
+                assert not [u for u in v_owed if u[0] == 1 and ENG[1][u[1]] == "v"]
+                fold(1)
             k = r + PRO
             ready = []
             if r == 0:
@@ -397,6 +416,9 @@ def tile_attention_pa_t_kernel(tc, x, W1, W2, W0, out):
             quantise_ready(ready)
             for unit in now_owed:
                 v_sum(unit)
+            p_owed += p_late
+            while p_late:
+                p_late.pop()
             if r == FIN0:
                 quantise_pooled(0)
             multiply_ready(ready)
@@ -423,6 +445,7 @@ def tile_attention_pa_t_kernel(tc, x, W1, W2, W0, out):
                 )
 
         second_pass(0)
+        assert not v_owed
         for i in range(len(p_owed)):
             hf, n, z, width = p_owed[i]
             pe_sum(hf, z, width, i == len(p_owed) - 1)

@@ -10,23 +10,29 @@ U8 = mybir.dt.uint8
 FP8X4 = mybir.dt.float8_e4m3fn_x4
 ADD = mybir.AluOpType.add
 TANH = mybir.ActivationFunctionType.Tanh
+AX = mybir.AxisListType.X
 
 P = 128
 F = 1024
-HALF = 512
-NPAIR = 18
+BANK = 512
+NQ = 9
+NJ = 4
+NHT = 8
 FLOPS = 2 * 128 * 36 * 1024 * 1024 + 3 * 2 * 128 * 1024 * 1024
 
-LAG = 5
-ENG = {0: "gggvggggvgvggpgpvg", 1: "vgpvggvgpghphphpfppp"}
-FLUSH1 = 17
-V_COPIES = "30211110110000000000000"
-G_WIDTH = 512
-X_FIRST = 10
-FIRST_SIZES = (1, 2, 2, 2, 2, 2, 2)
-PRO = 6
-FIN0 = 19
-LEAD = 5
+TABLE = ("dddddddd", "gggggggg", "gggggggg", "gpgpgggg", "pgpggggg", "gpgpgggg", "pgpggggg", "ppppvvvv", "ffffffff")
+LAST_ORDER = (4, 5, 6, 7, 0, 1, 2, 3)
+SUMS_AT = 1
+BACK_AT = 4
+V_LAG = 1
+Q_AT = 2
+EXTRA_AT = (4,)
+PLAN_Q = (3, 4, 5, 6, 7, 8)
+PAT_LONG = "sssv"
+PAT_SHORT = "svsv"
+ZB = 12
+G_W = 512
+NS = 6
 
 
 def tile_attention_pa_t_kernel(tc, x, W1, W2, W0, out):
@@ -35,14 +41,13 @@ def tile_attention_pa_t_kernel(tc, x, W1, W2, W0, out):
         ctx.enter_context(tc.manual_schedule())
         const = ctx.enter_context(tc.tile_pool(name="const", bufs=1))
         xin = ctx.enter_context(tc.tile_pool(name="xin", bufs=3))
-        win = ctx.enter_context(tc.tile_pool(name="win", bufs=3))
-        wst = ctx.enter_context(tc.tile_pool(name="wst", bufs=6))
-        xgp = ctx.enter_context(tc.tile_pool(name="xgp", bufs=4))
-        xcp = ctx.enter_context(tc.tile_pool(name="xcp", bufs=LAG + LEAD + 3))
-        zp = ctx.enter_context(tc.tile_pool(name="zp", bufs=7))
-        tp = ctx.enter_context(tc.psum_pool(name="tp", bufs=4))
-        mm = ctx.enter_context(tc.psum_pool(name="mm", bufs=3))
-        atp = ctx.enter_context(tc.psum_pool(name="at", bufs=1))
+        win = ctx.enter_context(tc.tile_pool(name="win", bufs=2))
+        stg = ctx.enter_context(tc.tile_pool(name="stg", bufs=2))
+        wst = ctx.enter_context(tc.tile_pool(name="wst", bufs=2))
+        xcp = ctx.enter_context(tc.tile_pool(name="xcp", bufs=5))
+        zp = ctx.enter_context(tc.tile_pool(name="zp", bufs=ZB))
+        ps = ctx.enter_context(tc.psum_pool(name="ps", bufs=7))
+        pbp = ctx.enter_context(tc.psum_pool(name="pbp", bufs=1))
 
         ident = const.tile([P, P], F32, name="ident")
         make_identity(nc, ident[:])
@@ -52,413 +57,334 @@ def tile_attention_pa_t_kernel(tc, x, W1, W2, W0, out):
 
         x0n = const.tile([P, F], BF16, name="x0n")
         x0T = const.tile([P, F], BF16, name="x0T")
-        wc = {}
-        ws = {}
-        bias = {}
-        for nm in ("w1", "w2"):
-            for hf in range(2):
-                wc[nm, hf] = const.tile([P, F], U32, name="c%s%d" % (nm, hf), align_bytes=64)
-                ws[nm, hf] = const.tile([P, F], U8, name="s%s%d" % (nm, hf), align_bytes=64)
-        for nm in ("w1", "w0"):
-            for hf in range(2):
-                bias[nm, hf] = const.tile([P, HALF], F32, name="b%s%d" % (nm, hf))
-        acc = {}
-        for e in ("g", "v"):
-            for hf in range(2):
-                acc[e, hf] = const.tile([P, F], F32, name="acc%s%d" % (e, hf))
-
-        def copy(on_scalar, dst, src):
-            if on_scalar:
-                nc.scalar.copy(out=dst, in_=src)
-            else:
-                nc.vector.tensor_copy(out=dst, in_=src)
+        w1c = [const.tile([P, 512], U32, name="w1c%d" % j, align_bytes=64) for j in range(NJ)]
+        w1s = [const.tile([P, 512], U8, name="w1s%d" % j, align_bytes=64) for j in range(NJ)]
+        h0T = [const.tile([P, 256], F32, name="h0T%d" % j) for j in range(NJ)]
+        w2c = [const.tile([P, F], U32, name="w2c%d" % o, align_bytes=64) for o in range(2)]
+        w2s = [const.tile([P, F], U8, name="w2s%d" % o, align_bytes=64) for o in range(2)]
+        w0T = [const.tile([P, 4 * BANK], F32, name="w0T%d" % o) for o in range(2)]
+        r0 = const.tile([P, F], F32, name="r0")
+        acc = [const.tile([P, BANK], F32, name="acc%d" % h) for h in range(NHT)]
+        finh = [const.tile([P, 4 * NS * P], F32, name="fin%d" % g) for g in range(2)]
+        fin = [finh[h // 4][:, (h % 4) * NS * P : (h % 4 + 1) * NS * P] for h in range(NHT)]
+        pbs = const.tile([P, BANK], F32, name="pbs")
+        pT = [const.tile([P, BANK], F32, name="pT%d" % g) for g in range(2)]
+        pg = [const.tile([P, BANK], BF16, name="pg%d" % g, align_bytes=64) for g in range(2)]
+        pc = const.tile([P, 2 * P], U32, name="pc", align_bytes=64)
+        pscale = const.tile([P, 2 * P], U8, name="pscale", align_bytes=64)
+        res = const.tile([P, F], F32, name="res")
 
         nat = {}
-        live = {"x": 0, "w": 0}
+        state = {"on_v": False, "back": False}
 
-        def load_x(q):
-            t = xin.tile([P, 4 * F], BF16, name="xn", tag="xn")
-            v = t[:].rearrange("p (i f) -> p i f", i=4)
-            if q == 0:
-                nc.sync.dma_start(out=v[:, 0:2, :], in_=x[:, 1:3, :])
-                nc.sync.dma_start(out=v[:, 2:4, :], in_=x[:, 3:5, :])
+        def copy(dst, src):
+            if state["on_v"]:
+                nc.vector.tensor_copy(out=dst, in_=src)
             else:
-                nc.sync.dma_start(out=v, in_=x[:, 1 + 4 * q : 5 + 4 * q, :])
-            nat["x", q] = t
+                nc.scalar.copy(out=dst, in_=src)
 
-        def load_w(nm, W, j, nt):
-            t = win.tile([P, 4 * F], BF16, name="wn", tag="wn")
-            nat[nm, j] = t
-            if nm == "w1" and j < 2:
-                for e in range(2):
-                    nc.sync.dma_start(out=t[:, e * 2 * F : (e + 1) * 2 * F],
-                                      in_=W1.rearrange("(j p e) c -> j e p c", p=P, e=2)[j, e])
-                return
-            nc.sync.dma_start(
-                out=t[:].rearrange("p (t c) -> p t c", t=nt),
-                in_=W1.rearrange("(j p e) c -> j p e c", p=P, e=2)[j] if nm == "w1"
-                else W.rearrange("(t p) c -> p t c", p=P)[:, j * nt : (j + 1) * nt, :],
-            )
-            nat[nm, j] = t
-
-        plan = []
-
-        def pump():
-            while plan and live[plan[0][0]] < 3:
-                kind, nm, j = plan.pop(0)
-                live[kind] += 1
-                if kind == "x":
-                    load_x(j)
-                elif nm == "w1":
-                    load_w(nm, W1, j, 2)
-                else:
-                    load_w(nm, W0 if nm == "w0" else W2, j, 4)
-
-        stage = {}
-
-        def words_of(item):
+        def load(item):
             kind, n = item
-            if kind == "x0":
-                return x0n[:].bitcast(F32)
             if kind == "x":
-                return nat["x", n // 4][:].bitcast(F32)[:, (n % 4) * HALF : (n % 4 + 1) * HALF]
-            if kind == "w1a" or kind == "w1b":
-                o = (n % 2) * F + (HALF if kind == "w1b" else 0)
-                return nat["w1", n // 2][:].bitcast(F32)[:, o : o + HALF]
-            return nat[kind, n // 4][:].bitcast(F32)[:, (n % 4) * HALF : (n % 4 + 1) * HALF]
-
-        def transposes(items):
-            banks = []
-            for item in items:
-                words = words_of(item)
-                bank = tp.tile([P, HALF], F32, name="tb", tag="tb")
-                for c in range(4):
-                    nc.tensor.transpose(bank[:, c * P : (c + 1) * P], words[:, c * P : (c + 1) * P], ident[:])
-                banks.append(bank)
-                kind, n = item
-                if kind == "x" and n % 4 == 3:
-                    live["x"] -= 1
-                if kind == "w1b" and n % 2 == 1:
-                    live["w"] -= 1
-                if (kind == "w0" or kind == "w2") and n % 4 == 3:
-                    live["w"] -= 1
-            pump()
-            return banks
-
-        def empty(item, bank, on_scalar):
-            kind, n = item
-            if kind == "x0":
-                nc.vector.tensor_copy(
-                    out=x0T[:].rearrange("p (c e b) -> p c e b", c=4, e=2),
-                    in_=bank[:].bitcast(BF16).rearrange("p (c b e) -> p c e b", c=4, e=2),
-                )
-            elif kind == "x":
-                if n % 2 == 0:
-                    stage["xg"] = xgp.tile([P, 2 * F], BF16, name="xg", tag="xg", align_bytes=64)
-                dst = stage["xg"][:].bitcast(F32)[:, (n % 2) * HALF : (n % 2 + 1) * HALF]
-                copy(on_scalar, dst.rearrange("p (g r u) -> p g r u", g=2, u=2),
-                     bank[:].rearrange("p (g u r) -> p g r u", g=2, u=2))
-            elif kind == "w1a" or kind == "w0":
-                stage[kind] = wst.tile([P, HALF], F32, name="pT", tag="pT")
-                copy(on_scalar, stage[kind][:], bank[:])
+                t = xin.tile([P, 4 * F], BF16, name="xn", tag="xn")
+                v = t[:].rearrange("p (i f) -> p i f", i=4)
+                if n == 0:
+                    nc.sync.dma_start(out=v[:, 0:2, :], in_=x[:, 1:3, :])
+                    nc.sync.dma_start(out=v[:, 2:4, :], in_=x[:, 3:5, :])
+                else:
+                    nc.sync.dma_start(out=v, in_=x[:, 1 + 4 * n : 5 + 4 * n, :])
+            elif kind == "w1":
+                t = win.tile([P, 4 * F], BF16, name="wn", tag="wn")
+                v = t[:].rearrange("p (e c) -> p e c", e=2)
+                if n == 0:
+                    for e in range(2):
+                        nc.sync.dma_start(out=v[:, e, :], in_=W1.rearrange("(j p e) c -> j e p c", p=P, e=2)[n, e])
+                else:
+                    nc.sync.dma_start(out=v, in_=W1.rearrange("(j p e) c -> j p e c", p=P, e=2)[n])
             else:
-                stage[kind] = wst.tile([P, F], BF16, name="wg", tag="wg", align_bytes=64)
-                copy(on_scalar, stage[kind][:].bitcast(F32).rearrange("p (g r u) -> p g r u", g=2, u=2),
-                     bank[:].rearrange("p (g u r) -> p g r u", g=2, u=2))
+                t = win.tile([P, 4 * F], BF16, name="wn", tag="wn")
+                W = W0 if kind == "w0" else W2
+                nc.sync.dma_start(out=t[:].rearrange("p (t c) -> p t c", t=4),
+                                  in_=W.rearrange("(t p) c -> p t c", p=P)[:, 4 * n : 4 * n + 4, :])
+            nat[item] = t
 
-        def quantise_w(nm, wg, n):
-            r = (n % 4) * P
-            for g in range(2):
-                nc.vector.quantize_mx(
-                    out=wc[nm, n // 4][:, g * HALF + r : g * HALF + r + P].bitcast(FP8X4),
-                    scales=ws[nm, n // 4][:, g * HALF + r : g * HALF + r + P],
-                    in_=wg[:, g * HALF : (g + 1) * HALF],
-                )
-
-        codes = {}
-
-        def quantise_x(j, xg):
-            xc = xcp.tile([P, HALF], U32, name="xc", tag="xc", align_bytes=64)
-            xs = xcp.tile([P, HALF], U8, name="xs", tag="xs", align_bytes=64)
-            nc.vector.quantize_mx(out=xc[:].bitcast(FP8X4), scales=xs[:], in_=xg[:])
-            codes[j] = (xc, xs)
-
-        unpaid = []
-
-        def pay():
-            while unpaid:
-                dst, bank = unpaid.pop(0)
-                nc.scalar.copy(out=dst, in_=bank[:])
-
-        def plain(kind, n, wT):
-            bank = mm.tile([P, P], F32, name="hq", tag="hb")
-            r = (n % 4) * P
-            v = wT[:].bitcast(BF16).rearrange("p (c r e) -> p c r e", c=4, e=2)
-            for k in range(8):
-                nc.tensor.matmul(out=bank[:], lhsT=x0T[:, k * P : (k + 1) * P],
-                                 rhs=v[:, k // 2, :, k % 2], start=(k == 0), stop=(k == 7))
-            unpaid.append((bias["w1" if kind == "w1a" else "w0", n // 4][:, r : r + P], bank))
-
-        def mx_group(lc, ls, lo, nm, hf):
-            bank = mm.tile([P, HALF], F32, name="hb", tag="hb")
-            for g in range(2):
-                nc.tensor.matmul_mx(
-                    out=bank[:],
-                    lhsT=lc[:, lo + g * P : lo + (g + 1) * P].bitcast(FP8X4),
-                    lhsT_scale=ls[:, lo + g * P : lo + (g + 1) * P],
-                    rhs=wc[nm, hf][:, g * HALF : (g + 1) * HALF].bitcast(FP8X4),
-                    rhs_scale=ws[nm, hf][:, g * HALF : (g + 1) * HALF],
-                    start=(g == 0),
-                    stop=(g == 1),
-                )
+        def transposes(words):
+            bank = ps.tile([P, BANK], F32, name="bank", tag="bank")
+            for c in range(4):
+                nc.tensor.transpose(bank[:, c * P : (c + 1) * P], words[:, c * P : (c + 1) * P], ident[:])
             return bank
 
-        started = set()
-        pc = const.tile([P, 2 * P], U32, name="pc", align_bytes=64)
-        ps = const.tile([P, 2 * P], U8, name="ps", align_bytes=64)
-        accT = {}
-        holds = {("p", 0): [], ("p", 1): []}
+        side = []
+        codes = {}
+        stage = {}
 
-        def tanh(unit, v_owed, p_owed):
-            hf, n, z, width = unit
-            e = ENG[hf][n]
-            assert e in "pfh" or hf not in folded
-            if e in "gv" and (e, hf) not in started:
-                started.add((e, hf))
-                nc.scalar.activation(out=acc[e, hf][:], in_=z[:], func=TANH)
-                holds[e, hf] = [n]
-                return
-            nc.scalar.activation(out=z[:], in_=z[:], func=TANH)
-            if e == "g":
-                for o in range(0, F, G_WIDTH):
-                    nc.gpsimd.tensor_tensor(out=acc[e, hf][:, o : o + G_WIDTH], in0=acc[e, hf][:, o : o + G_WIDTH],
-                                            in1=z[:, o : o + G_WIDTH], op=ADD)
-                holds[e, hf].append(n)
-            elif e == "v" or (e == "h" and width == F):
-                v_owed.append(unit)
-            elif e == "f" and width == F:
-                nc.gpsimd.tensor_tensor(out=z[:, 0:HALF], in0=z[:, 0:HALF], in1=z[:, HALF:F], op=ADD)
-                p_owed.append((hf, n, z, HALF))
+        def prep(item):
+            kind, n = item
+            words = nat[item][:].bitcast(F32)
+            banks = []
+            if kind == "w1":
+                order = (BANK, 3 * BANK, 0, 2 * BANK)
             else:
-                p_owed.append(unit)
+                order = (0, BANK, 2 * BANK, 3 * BANK)
+            for o in order:
+                banks.append(transposes(words[:, o : o + BANK]))
+            if state["back"]:
+                state["back"] = False
+                pe_back()
+            pe_sums()
+            if kind == "x" or kind == "w2":
+                xg = stg.tile([P, 4 * F], BF16, name="xg", tag="xg", align_bytes=64)
+                dst = xg[:].bitcast(F32).rearrange("p (g i r u) -> p g i r u", g=2, i=4, u=2)
+                for i in range(4):
+                    side.append((item, "e", dst[:, :, i], banks[i][:].rearrange("p (g u r) -> p g r u", g=2, u=2)))
+                side.append((item, "q", xg, None))
+            elif kind == "w1":
+                wg = wst.tile([P, 2 * F], BF16, name="wg", tag="wg", align_bytes=64)
+                wa = wst.tile([P, F], F32, name="wa", tag="wa")
+                dst = wg[:].bitcast(F32).rearrange("p (e g r u) -> p e g r u", e=2, g=2, u=2)
+                for e in range(2):
+                    side.append((item, "e", dst[:, e], banks[e][:].rearrange("p (g u r) -> p g r u", g=2, u=2)))
+                side.append((item, "q", wg, None))
+                for e in range(2):
+                    side.append((item, "e", wa[:, e * BANK : (e + 1) * BANK], banks[2 + e][:]))
+                stage[item] = wa
+            else:
+                dst = w0T[n][:].rearrange("p (c t r) -> p c t r", c=4, t=4)
+                for i in range(4):
+                    side.append((item, "e", dst[:, :, i], banks[i][:].rearrange("p (c r) -> p c r", c=4)))
 
-        def v_sum(unit):
-            hf, n, z, width = unit
-            if ENG[hf][n] == "h":
-                nc.vector.tensor_tensor(out=z[:, 0:HALF], in0=z[:, 0:HALF], in1=z[:, HALF:F], op=ADD)
-                p_late.append((hf, n, z, HALF))
-                return
-            nc.vector.tensor_tensor(out=acc["v", hf][:], in0=acc["v", hf][:], in1=z[:], op=ADD)
-            holds["v", hf].append(n)
+        def do_side(at=0):
+            item, what, a, b = side.pop(at)
+            kind, n = item
+            if what == "e":
+                copy(a, b)
+            elif kind == "x":
+                xc = xcp.tile([P, F], U32, name="xc", tag="xc", align_bytes=64)
+                xs = xcp.tile([P, F], U8, name="xs", tag="xs", align_bytes=64)
+                nc.vector.quantize_mx(out=xc[:].bitcast(FP8X4), scales=xs[:], in_=a[:])
+                codes[n] = (xc, xs)
+            elif kind == "w2":
+                nc.vector.quantize_mx(out=w2c[n][:].bitcast(FP8X4), scales=w2s[n][:], in_=a[:])
+            else:
+                nc.vector.quantize_mx(out=w1c[n][:].bitcast(FP8X4), scales=w1s[n][:], in_=a[:])
 
-        def pe_sum(hf, src, width, last):
-            first = hf not in accT
-            if first:
-                accT[hf] = atp.tile([P, HALF], F32, name="at") if hf == 1 else tp.tile([P, HALF], F32, name="at0", tag="tb")
-            nblk = width // P
-            for k in range(nblk):
-                t = k % 4
-                nc.tensor.matmul(out=accT[hf][:, t * P : (t + 1) * P], lhsT=src[:, k * P : (k + 1) * P], rhs=ident[:],
-                                 is_transpose=True, start=(first and k == 0), stop=(last and k == nblk - 1))
+        def flush(item):
+            while [s for s in side if s[0] == item]:
+                do_side()
 
-        folded = set()
-        p_late = []
+        def anchors_h(j):
+            bank = ps.tile([P, BANK], F32, name="bank", tag="bank")
+            v = stage["w1", j][:].bitcast(BF16).rearrange("p (e c r s) -> p e c r s", e=2, c=4, s=2)
+            for e in range(2):
+                for k in range(8):
+                    nc.tensor.matmul(out=bank[:, e * P : (e + 1) * P], lhsT=v[:, e, k // 2, :, k % 2],
+                                     rhs=x0T[:, k * P : (k + 1) * P], start=(k == 0), stop=(k == 7))
+            return bank
 
-        def fold(hf):
-            folded.add(hf)
-            for e in ("g", "v"):
-                if (e, hf) in started:
-                    a = acc[e, hf]
-                    nc.gpsimd.tensor_tensor(out=a[:, 0:HALF], in0=a[:, 0:HALF], in1=a[:, HALF:F], op=ADD)
+        def anchors_w0(o):
+            bank = ps.tile([P, BANK], F32, name="bank", tag="bank")
+            v = w0T[o][:].bitcast(BF16).rearrange("p (c r s) -> p c r s", c=4, s=2)
+            for k in range(8):
+                nc.tensor.matmul(out=bank[:], lhsT=x0T[:, k * P : (k + 1) * P], rhs=v[:, k // 2, :, k % 2],
+                                 start=(k == 0), stop=(k == 7))
+            nc.scalar.copy(out=r0[:, o * BANK : (o + 1) * BANK], in_=bank[:])
 
-        def flush(hf, last):
-            assert hf in folded
-            todo = [e for e in ("g", "v") if (e, hf) in started]
-            for e in todo:
-                pe_sum(hf, acc[e, hf], HALF, last and e == todo[-1])
-                holds["p", hf] += holds[e, hf]
+        count = [0] * NHT
 
-        def quantise_pooled(hf):
-            pg = const.tile([P, HALF], BF16, name="pg%d" % hf, align_bytes=64)
-            nc.scalar.copy(out=pg[:].rearrange("p (b t) -> p b t", t=4), in_=accT[hf][:].rearrange("p (t b) -> p b t", t=4))
-            nc.vector.quantize_mx(out=pc[:, hf * P : (hf + 1) * P].bitcast(FP8X4),
-                                  scales=ps[:, hf * P : (hf + 1) * P], in_=pg[:])
+        def cls(ht, q):
+            if q == 0:
+                return "d"
+            if q == NQ - 1:
+                return "f"
+            return TABLE[q][ht]
 
-        first = [("x0", 0)]
-        for n in range(4):
-            first += [("w1a", n), ("w1b", n)]
-        first += [("x", n) for n in range(X_FIRST)]
-        for n in range(4, 8):
-            first += [("w1a", n), ("w1b", n)]
-        wq = [("w0", n) for n in range(8)] + [("w2", n) for n in range(8)]
-        nx = X_FIRST
-        bunch = []
-        while first or nx < 2 * NPAIR or wq:
-            size = FIRST_SIZES[len(bunch)] if len(bunch) < len(FIRST_SIZES) else 4
-            items = []
-            while len(items) < size and (first or nx < 2 * NPAIR or wq):
+        def kinds(ht):
+            return [cls(ht, q) for q in range(NQ)]
+
+        def nslot(ht):
+            return 5 + len([c for c in kinds(ht) if c == "v"]) + (1 if "p" in kinds(ht) else 0)
+
+        assert max([nslot(ht) for ht in range(NHT)]) <= NS
+        last_p = max([(q, ht) for ht in range(4) for q in range(NQ) if cls(ht, q) == "p"] + [(-1, -1)])
+
+        owed = []
+        pb = {}
+
+        def pe_sums():
+            while owed:
+                ht, z, last = owed.pop(0)
+                first = "t" not in pb
                 if first:
-                    items.append(first.pop(0))
-                elif nx < 2 * NPAIR and (not wq or nx // 2 <= len(bunch) - PRO + LEAD):
-                    items.append(("x", nx))
-                    nx += 1
-                else:
-                    items.append(wq.pop(0))
-            bunch.append(items)
-        banks = [item for items in bunch for item in items]
-        seen = set()
-        for kind, n in banks:
-            if kind == "x":
-                key = ("x", "x", n // 4)
-            elif kind == "w1a" or kind == "w1b":
-                key = ("w", "w1", n // 2)
-            elif kind == "x0":
-                continue
+                    pb["t"] = pbp.tile([P, BANK], F32, name="pb")
+                for i in range(4):
+                    nc.tensor.matmul(out=pb["t"][:, ht * P : (ht + 1) * P], lhsT=z[:, i * P : (i + 1) * P], rhs=ident[:],
+                                     is_transpose=True, start=(first and i == 0), stop=(last and i == 3))
+                if last:
+                    nc.scalar.copy(out=pbs[:], in_=pb["t"][:])
+                    state["back"] = True
+
+        def pe_back():
+            bank = transposes(pbs[:])
+            for ht in range(4):
+                if "p" in kinds(ht):
+                    s = nslot(ht) - 1
+                    nc.scalar.copy(out=fin[ht][:, s * P : (s + 1) * P], in_=bank[:, ht * P : (ht + 1) * P])
+
+        def quantise_pooled(g):
+            nc.scalar.copy(out=pg[g][:].rearrange("p (b t) -> p b t", t=4), in_=pT[g][:].rearrange("p (t b) -> p b t", t=4))
+            nc.vector.quantize_mx(out=pc[:, g * P : (g + 1) * P].bitcast(FP8X4), scales=pscale[:, g * P : (g + 1) * P], in_=pg[g][:])
+
+        def unit(ht, q):
+            j, e = ht // 2, ht % 2
+            xc, xs = codes[q]
+            bank = ps.tile([P, BANK], F32, name="bank", tag="bank")
+            for g in range(2):
+                lo = e * 2 * P + g * P
+                nc.tensor.matmul_mx(out=bank[:], lhsT=w1c[j][:, lo : lo + P].bitcast(FP8X4), lhsT_scale=w1s[j][:, lo : lo + P],
+                                    rhs=xc[:, g * BANK : (g + 1) * BANK].bitcast(FP8X4), rhs_scale=xs[:, g * BANK : (g + 1) * BANK],
+                                    start=(g == 0), stop=(g == 1))
+            z = zp.tile([P, BANK], F32, name="z", tag="z")
+            nc.vector.tensor_tensor(out=z[:].rearrange("p (i b) -> p i b", i=4), in0=bank[:].rearrange("p (i b) -> p i b", i=4),
+                                    in1=h0T[j][:, e * P : (e + 1) * P].unsqueeze(1).to_broadcast([P, 4, P]), op=ADD)
+            return z
+
+        vlate = []
+
+        done = []
+        ready2 = []
+
+        def late_reduce():
+            ht, z, s = vlate.pop(0)
+            if z is not None:
+                nc.vector.tensor_reduce(out=fin[ht][:, s * P : (s + 1) * P], in_=z[:].rearrange("p (i b) -> p b i", i=4), axis=AX, op=ADD)
+                return
+            nc.vector.tensor_reduce(out=pT[ht // 4][:, (ht % 4) * P : (ht % 4 + 1) * P],
+                                    in_=fin[ht][:, 0 : nslot(ht) * P].rearrange("p (s b) -> p b s", s=nslot(ht)), axis=AX, op=ADD)
+            done.append(ht)
+            g = ht // 4
+            if len([d for d in done if d // 4 == g]) == 4:
+                quantise_pooled(g)
+                ready2.append(g)
+
+        obs = []
+
+        def second(g, first, last):
+            for o in range(2):
+                if first:
+                    ob = ps.tile([P, BANK], F32, name="bank", tag="bank")
+                    obs.append(ob)
+                nc.tensor.matmul_mx(out=obs[o][:], lhsT=pc[:, g * P : (g + 1) * P].bitcast(FP8X4), lhsT_scale=pscale[:, g * P : (g + 1) * P],
+                                    rhs=w2c[o][:, g * BANK : (g + 1) * BANK].bitcast(FP8X4), rhs_scale=w2s[o][:, g * BANK : (g + 1) * BANK],
+                                    start=first, stop=last)
+
+        def finish(ht, z):
+            k = count[ht]
+            count[ht] += 1
+            c = cls(ht, k)
+            if c == "d":
+                nc.scalar.activation(out=acc[ht][:], in_=z[:], func=TANH)
+            elif c == "f":
+                nc.scalar.activation(out=fin[ht][:, 0:BANK], in_=z[:], func=TANH)
+                vlate.append((ht, None, 0))
+            elif c == "p":
+                nc.scalar.activation(out=z[:], in_=z[:], func=TANH)
+                owed.append((ht, z, (k, ht) == last_p))
+            elif c == "v":
+                nc.scalar.activation(out=z[:], in_=z[:], func=TANH)
+                vlate.append((ht, z, 5 + len([c for c in kinds(ht)[0:k] if c == "v"])))
             else:
-                key = ("w", kind, n // 4)
-            if key not in seen:
-                seen.add(key)
-                plan.append(key)
+                nc.scalar.activation(out=z[:], in_=z[:], func=TANH)
+                for o in range(0, BANK, G_W):
+                    nc.gpsimd.tensor_tensor(out=acc[ht][:, o : o + G_W], in0=acc[ht][:, o : o + G_W], in1=z[:, o : o + G_W], op=ADD)
+            if k == max([q for q in range(NQ) if cls(ht, q) in "dg"]):
+                a = acc[ht]
+                nc.gpsimd.tensor_tensor(out=a[:, 0 : 2 * P], in0=a[:, 0 : 2 * P], in1=a[:, 2 * P : 4 * P], op=ADD)
+                nc.gpsimd.tensor_tensor(out=fin[ht][:, 4 * P : 5 * P], in0=a[:, 0:P], in1=a[:, P : 2 * P], op=ADD)
+
+        arrivals = []
+        for n in range(NJ):
+            arrivals += [("w1", n), ("x", n)]
+        arrivals += [("x", n) for n in range(NJ, NQ)]
+        extras = [("w0", 0), ("w0", 1), ("w2", 0), ("w2", 1)]
+        loads = arrivals[0:9] + [("w0", 0), ("x", 5), ("w0", 1), ("x", 6), ("w2", 0), ("x", 7), ("w2", 1), ("x", 8)]
+        live = {"x": 0, "w": 0}
+
+        def pump():
+            while loads and live["x" if loads[0][0] == "x" else "w"] < (3 if loads[0][0] == "x" else 2):
+                live["x" if loads[0][0] == "x" else "w"] += 1
+                load(loads.pop(0))
+
+        def prep_and_pump(item):
+            prep(item)
+            live["x" if item[0] == "x" else "w"] -= 1
+            pump()
 
         nc.sync.dma_start(out=x0n[:], in_=x[:, 0, :])
         pump()
-
-        def empty_bunch(k, n_v):
-            ready = []
-            for i in range(len(bunch[k])):
-                item = bunch[k][i]
-                empty(item, tb[k][i], i >= n_v)
-                if item[0] == "x" and item[1] % 2 == 1:
-                    ready.append(("qx", item[1] // 2, stage["xg"]))
-                if item[0] == "w1b" or item[0] == "w2":
-                    ready.append(("qw", item[0][0:2], stage[item[0]], item[1]))
-                if item[0] == "w1a" or item[0] == "w0":
-                    ready.append(("mm", item[0], item[1], stage[item[0]]))
-            pay()
-            return ready
-
-        def quantise_ready(ready):
-            for t in ready:
-                if t[0] == "qx":
-                    quantise_x(t[1], t[2])
-                if t[0] == "qw":
-                    quantise_w(t[1], t[2], t[3])
-
-        def multiply_ready(ready):
-            for t in ready:
-                if t[0] == "mm":
-                    plain(t[1], t[2], t[3])
-
-        tb = {0: transposes(bunch[0])}
-        for k in range(PRO):
-            ready = empty_bunch(k, 1)
-            quantise_ready(ready)
-            if k + 1 < PRO:
-                tb[k + 1] = transposes(bunch[k + 1])
-            multiply_ready(ready)
-
-        second = list(range(NPAIR))
-        v_owed = []
-        p_owed = []
-        r = 0
-        while r < NPAIR or second:
-            todo = []
-            if r < NPAIR:
-                todo.append((0, r))
-            if r >= LAG:
-                todo.append((1, second.pop(0)))
-                if r >= NPAIR and second:
-                    todo.append((1, second.pop(0)))
-            groups = []
-            for hf, j in todo:
-                for i in range(2):
-                    groups.append((hf, j, mx_group(codes[j][0], codes[j][1], i * 2 * P, "w1", hf)))
-            for hf, n, z, width in p_owed:
-                pe_sum(hf, z, width, False)
-                holds["p", hf].append(n)
-            p_owed = []
-            if r == FIN0:
-                flush(0, True)
-            if r == FLUSH1:
-                flush(1, False)
-            if r == FIN0 - 1:
-                assert not [u for u in v_owed if u[0] == 0 and ENG[0][u[1]] == "v"] and r >= NPAIR
-                fold(0)
-            if r == FLUSH1 - 1:
-                assert not [u for u in v_owed if u[0] == 1 and ENG[1][u[1]] == "v"]
-                fold(1)
-            k = r + PRO
-            ready = []
-            if r == 0:
-                tb[k] = transposes(bunch[k])
-                pay()
-            elif k < len(bunch):
-                ready = empty_bunch(k, int(V_COPIES[r]))
-            now_owed = v_owed
-            v_owed = []
-            for n in range(len(groups)):
-                hf, j, bank = groups[n]
-                single = hf == 1 and j == NPAIR - 1
-                if single:
-                    z = zp.tile([P, HALF], F32, name="z1", tag="z1", bufs=2)
-                    unit = (hf, NPAIR + n % 2, z, HALF)
-                    dst = z[:]
-                else:
-                    if n % 2 == 0:
-                        z = zp.tile([P, F], F32, name="z", tag="z")
-                        unit = (hf, j, z, F)
-                    dst = z[:, (n % 2) * HALF : (n % 2 + 1) * HALF]
-                nc.vector.tensor_tensor(out=dst, in0=bank[:], in1=bias["w1", hf][:], op=ADD)
-                if single or n % 2 == 1:
-                    tanh(unit, v_owed, p_owed)
-            if r == 0:
-                ready = empty_bunch(k, int(V_COPIES[r]))
-            quantise_ready(ready)
-            for unit in now_owed:
-                v_sum(unit)
-            p_owed += p_late
-            while p_late:
-                p_late.pop()
-            if r == FIN0:
-                quantise_pooled(0)
-            multiply_ready(ready)
-            pay()
-            if k + 1 < len(bunch):
-                tb[k + 1] = transposes(bunch[k + 1])
-            r += 1
-
+        bank0 = transposes(x0n[:].bitcast(F32))
+        nc.vector.tensor_copy(out=x0T[:].rearrange("p (c s b) -> p c s b", c=4, s=2),
+                              in_=bank0[:].bitcast(BF16).rearrange("p (c b s) -> p c s b", c=4, s=2))
+        prep_and_pump(arrivals[0])
+        have = {"w1": [], "x": []}
+        plan = [(PLAN_Q[i], (extras + [("p", 0), ("p", 1)])[i]) for i in range(6)]
         obs = []
-        for fh in range(2):
-            ob = mm.tile([P, HALF], F32, name="hb", tag="hb")
-            obs.append(ob)
+        def evacuate(pattern):
+            n_e = len([s for s in side if s[1] == "e"])
+            for i in range(n_e):
+                state["on_v"] = pattern[i % len(pattern)] == "v"
+                do_side([s[1] for s in side].index("e"))
 
-        def second_pass(g):
-            for fh in range(2):
-                nc.tensor.matmul_mx(
-                    out=obs[fh][:],
-                    lhsT=pc[:, g * P : (g + 1) * P].bitcast(FP8X4),
-                    lhsT_scale=ps[:, g * P : (g + 1) * P],
-                    rhs=wc["w2", fh][:, g * HALF : (g + 1) * HALF].bitcast(FP8X4),
-                    rhs_scale=ws["w2", fh][:, g * HALF : (g + 1) * HALF],
-                    start=(g == 0),
-                    stop=(g == 1),
-                )
-
-        second_pass(0)
-        assert not v_owed
-        for i in range(len(p_owed)):
-            hf, n, z, width = p_owed[i]
-            pe_sum(hf, z, width, i == len(p_owed) - 1)
-            holds["p", hf].append(n)
-        assert sorted(holds["p", 0]) == list(range(NPAIR))
-        assert sorted(holds["p", 1]) == list(range(NPAIR - 1)) + [NPAIR, NPAIR + 1]
-        quantise_pooled(1)
-        second_pass(1)
-        res = const.tile([P, F], F32, name="res")
-        for fh in range(2):
-            s = slice(fh * HALF, (fh + 1) * HALF)
-            nc.vector.tensor_tensor(out=res[:, s], in0=obs[fh][:], in1=bias["w0", fh][:], op=ADD)
-            if fh == 0:
+        for n in range(len(arrivals)):
+            item = arrivals[n]
+            flush(item)
+            hb = None
+            if item[0] == "w1":
+                units = [(2 * item[1] + e, q) for q in have["x"] for e in range(2)]
+            else:
+                units = [(ht, item[1]) for j in have["w1"] for ht in (2 * j, 2 * j + 1)]
+            long_event = len(units) == NHT
+            if item == ("x", NQ - 1):
+                units = [(ht, item[1]) for ht in LAST_ORDER]
+            if n + 1 < len(arrivals):
+                prep_and_pump(arrivals[n + 1])
+            if item[0] == "w1":
+                hb = anchors_h(item[1])
+            have[item[0]].append(item[1])
+            evacuate(PAT_LONG if long_event else PAT_SHORT)
+            if not long_event:
+                while side:
+                    do_side()
+            if hb is not None:
+                nc.scalar.copy(out=h0T[item[1]][:], in_=hb[:, 0 : 2 * P])
+            for k in range(len(units)):
+                if long_event and k in EXTRA_AT and plan and plan[0][0] <= item[1]:
+                    what = plan.pop(0)[1]
+                    if what[0] == "p":
+                        anchors_w0(what[1])
+                    else:
+                        prep_and_pump(what)
+                        evacuate(PAT_LONG)
+                if item == ("x", NQ - 1) and k == SUMS_AT:
+                    pe_sums()
+                if item == ("x", NQ - 1) and k == BACK_AT and state["back"]:
+                    state["back"] = False
+                    pe_back()
+                z = unit(units[k][0], units[k][1])
+                while len(vlate) > V_LAG:
+                    late_reduce()
+                if side and k % 4 == Q_AT:
+                    do_side()
+                finish(units[k][0], z)
+        while vlate:
+            late_reduce()
+            if len(ready2) == 1:
+                second(ready2[0], True, False)
+                ready2.append(-1)
+        second(ready2[2], False, True)
+        for o in range(2):
+            s = slice(o * BANK, (o + 1) * BANK)
+            nc.vector.tensor_tensor(out=res[:, s], in0=obs[o][:], in1=r0[:, s], op=ADD)
+            if o == 0:
                 nc.sync.dma_start(out=out[:, s], in_=res[:, s])
             else:
                 nc.scalar.dma_start(out=out[:, s], in_=res[:, s])

@@ -10,29 +10,26 @@ U8 = mybir.dt.uint8
 FP8X4 = mybir.dt.float8_e4m3fn_x4
 ADD = mybir.AluOpType.add
 TANH = mybir.ActivationFunctionType.Tanh
-AX = mybir.AxisListType.X
 
 P = 128
 F = 1024
 BANK = 512
 NQ = 9
-NJ = 4
-NHT = 8
 FLOPS = 2 * 128 * 36 * 1024 * 1024 + 3 * 2 * 128 * 1024 * 1024
 
-TABLE = ("dddddddd", "gggggggg", "gggggggg", "gpgpgggg", "pgpggggg", "gpgpgggg", "pgpggggg", "ppppvvvv", "ffffffff")
-LAST_ORDER = (4, 5, 6, 7, 0, 1, 2, 3)
-SUMS_AT = 1
-BACK_AT = 4
-V_LAG = 1
-Q_AT = 2
-EXTRA_AT = (4,)
-PLAN_Q = (3, 4, 5, 6, 7, 8)
+TABLE = ("dggg....", "gggg....", "gpgpgpgv", "gpgpgpgv", "gpgpgpgv", "gpgpgpgv", "gpgpgpgv", "gpgpgpgv", "pppppppp")
+FIRST1 = "dpgpgpgv"
 PAT_LONG = "sssv"
 PAT_SHORT = "svsv"
 ZB = 12
-G_W = 512
-NS = 6
+Q_AT = 3
+EXTRA_AT = (4,)
+PLAN_Q = (2, 3, 4, 5, 6, 7)
+V_LAG = 1
+P_LAG = 2
+FLUSH_EARLY = False
+LAST_RUN_AT = 6
+NBANK = 7
 
 
 def tile_attention_pa_t_kernel(tc, x, W1, W2, W0, out):
@@ -43,11 +40,10 @@ def tile_attention_pa_t_kernel(tc, x, W1, W2, W0, out):
         xin = ctx.enter_context(tc.tile_pool(name="xin", bufs=3))
         win = ctx.enter_context(tc.tile_pool(name="win", bufs=2))
         stg = ctx.enter_context(tc.tile_pool(name="stg", bufs=2))
-        wst = ctx.enter_context(tc.tile_pool(name="wst", bufs=2))
-        xcp = ctx.enter_context(tc.tile_pool(name="xcp", bufs=5))
+        xcp = ctx.enter_context(tc.tile_pool(name="xcp", bufs=4))
         zp = ctx.enter_context(tc.tile_pool(name="zp", bufs=ZB))
-        ps = ctx.enter_context(tc.psum_pool(name="ps", bufs=7))
-        pbp = ctx.enter_context(tc.psum_pool(name="pbp", bufs=1))
+        ps = ctx.enter_context(tc.psum_pool(name="ps", bufs=NBANK))
+        atp = ctx.enter_context(tc.psum_pool(name="atp", bufs=1))
 
         ident = const.tile([P, P], F32, name="ident")
         make_identity(nc, ident[:])
@@ -57,25 +53,29 @@ def tile_attention_pa_t_kernel(tc, x, W1, W2, W0, out):
 
         x0n = const.tile([P, F], BF16, name="x0n")
         x0T = const.tile([P, F], BF16, name="x0T")
-        w1c = [const.tile([P, 512], U32, name="w1c%d" % j, align_bytes=64) for j in range(NJ)]
-        w1s = [const.tile([P, 512], U8, name="w1s%d" % j, align_bytes=64) for j in range(NJ)]
-        h0T = [const.tile([P, 256], F32, name="h0T%d" % j) for j in range(NJ)]
-        w2c = [const.tile([P, F], U32, name="w2c%d" % o, align_bytes=64) for o in range(2)]
-        w2s = [const.tile([P, F], U8, name="w2s%d" % o, align_bytes=64) for o in range(2)]
-        w0T = [const.tile([P, 4 * BANK], F32, name="w0T%d" % o) for o in range(2)]
-        r0 = const.tile([P, F], F32, name="r0")
-        acc = [const.tile([P, BANK], F32, name="acc%d" % h) for h in range(NHT)]
-        finh = [const.tile([P, 4 * NS * P], F32, name="fin%d" % g) for g in range(2)]
-        fin = [finh[h // 4][:, (h % 4) * NS * P : (h % 4 + 1) * NS * P] for h in range(NHT)]
-        pbs = const.tile([P, BANK], F32, name="pbs")
-        pT = [const.tile([P, BANK], F32, name="pT%d" % g) for g in range(2)]
+        wc = {}
+        ws = {}
+        for nm in ("w1", "w2"):
+            for hf in range(2):
+                wc[nm, hf] = const.tile([P, F], U32, name="c%s%d" % (nm, hf), align_bytes=64)
+                ws[nm, hf] = const.tile([P, F], U8, name="s%s%d" % (nm, hf), align_bytes=64)
+        wT = {}
+        prod = {}
+        for nm in ("w1", "w0"):
+            for hf in range(2):
+                wT[nm, hf] = const.tile([P, 4 * BANK], F32, name="t%s%d" % (nm, hf))
+                prod[nm, hf] = const.tile([P, BANK], F32, name="b%s%d" % (nm, hf))
+        acc = {}
+        for e in ("g", "v"):
+            for hf in range(2):
+                acc[e, hf] = const.tile([P, BANK], F32, name="acc%s%d" % (e, hf))
         pg = [const.tile([P, BANK], BF16, name="pg%d" % g, align_bytes=64) for g in range(2)]
         pc = const.tile([P, 2 * P], U32, name="pc", align_bytes=64)
         pscale = const.tile([P, 2 * P], U8, name="pscale", align_bytes=64)
         res = const.tile([P, F], F32, name="res")
 
         nat = {}
-        state = {"on_v": False, "back": False}
+        state = {"on_v": False, "units": 0}
 
         def copy(dst, src):
             if state["on_v"]:
@@ -117,6 +117,29 @@ def tile_attention_pa_t_kernel(tc, x, W1, W2, W0, out):
         side = []
         codes = {}
         stage = {}
+        owed = []
+        accT = {}
+        left = {0: 0, 1: 0}
+
+        def pe_sum(hf, src):
+            first = hf not in accT
+            if first:
+                if hf == 1:
+                    accT[hf] = atp.tile([P, BANK], F32, name="at1")
+                else:
+                    accT[hf] = ps.tile([P, BANK], F32, name="bank", tag="bank")
+            left[hf] -= 1
+            for t in range(4):
+                nc.tensor.matmul(out=accT[hf][:, t * P : (t + 1) * P], lhsT=src[:, t * P : (t + 1) * P], rhs=ident[:],
+                                 is_transpose=True, start=(first and t == 0), stop=(left[hf] == 0 and t == 3))
+
+        def pe_sums():
+            while owed and owed[0][2] <= state["units"] - P_LAG:
+                hf, z, seq = owed.pop(0)
+                pe_sum(hf, z)
+
+        def quant_view(t):
+            return t[:].bitcast(F32).rearrange("p (g i r u) -> p g i r u", g=2, i=4, u=2)
 
         def prep(item):
             kind, n = item
@@ -128,28 +151,25 @@ def tile_attention_pa_t_kernel(tc, x, W1, W2, W0, out):
                 order = (0, BANK, 2 * BANK, 3 * BANK)
             for o in order:
                 banks.append(transposes(words[:, o : o + BANK]))
-            if state["back"]:
-                state["back"] = False
-                pe_back()
             pe_sums()
             if kind == "x" or kind == "w2":
                 xg = stg.tile([P, 4 * F], BF16, name="xg", tag="xg", align_bytes=64)
-                dst = xg[:].bitcast(F32).rearrange("p (g i r u) -> p g i r u", g=2, i=4, u=2)
                 for i in range(4):
-                    side.append((item, "e", dst[:, :, i], banks[i][:].rearrange("p (g u r) -> p g r u", g=2, u=2)))
+                    side.append((item, "e", quant_view(xg)[:, :, i], banks[i][:].rearrange("p (g u r) -> p g r u", g=2, u=2)))
                 side.append((item, "q", xg, None))
             elif kind == "w1":
-                wg = wst.tile([P, 2 * F], BF16, name="wg", tag="wg", align_bytes=64)
-                wa = wst.tile([P, F], F32, name="wa", tag="wa")
-                dst = wg[:].bitcast(F32).rearrange("p (e g r u) -> p e g r u", e=2, g=2, u=2)
+                hf = n // 2
+                if n % 2 == 0:
+                    stage[hf] = stg.tile([P, 4 * F], BF16, name="xg", tag="xg", align_bytes=64)
                 for e in range(2):
-                    side.append((item, "e", dst[:, e], banks[e][:].rearrange("p (g u r) -> p g r u", g=2, u=2)))
-                side.append((item, "q", wg, None))
+                    side.append((item, "e", quant_view(stage[hf])[:, :, 2 * (n % 2) + e], banks[e][:].rearrange("p (g u r) -> p g r u", g=2, u=2)))
+                if n % 2 == 1:
+                    side.append((item, "q", stage[hf], None))
+                dst = wT["w1", hf][:].rearrange("p (c t r) -> p c t r", c=4, t=4)
                 for e in range(2):
-                    side.append((item, "e", wa[:, e * BANK : (e + 1) * BANK], banks[2 + e][:]))
-                stage[item] = wa
+                    side.append((item, "e", dst[:, :, 2 * (n % 2) + e], banks[2 + e][:].rearrange("p (c r) -> p c r", c=4)))
             else:
-                dst = w0T[n][:].rearrange("p (c t r) -> p c t r", c=4, t=4)
+                dst = wT["w0", n][:].rearrange("p (c t r) -> p c t r", c=4, t=4)
                 for i in range(4):
                     side.append((item, "e", dst[:, :, i], banks[i][:].rearrange("p (c r) -> p c r", c=4)))
 
@@ -164,107 +184,63 @@ def tile_attention_pa_t_kernel(tc, x, W1, W2, W0, out):
                 nc.vector.quantize_mx(out=xc[:].bitcast(FP8X4), scales=xs[:], in_=a[:])
                 codes[n] = (xc, xs)
             elif kind == "w2":
-                nc.vector.quantize_mx(out=w2c[n][:].bitcast(FP8X4), scales=w2s[n][:], in_=a[:])
+                nc.vector.quantize_mx(out=wc["w2", n][:].bitcast(FP8X4), scales=ws["w2", n][:], in_=a[:])
             else:
-                nc.vector.quantize_mx(out=w1c[n][:].bitcast(FP8X4), scales=w1s[n][:], in_=a[:])
+                nc.vector.quantize_mx(out=wc["w1", n // 2][:].bitcast(FP8X4), scales=ws["w1", n // 2][:], in_=a[:])
 
         def flush(item):
             while [s for s in side if s[0] == item]:
                 do_side()
 
-        def anchors_h(j):
-            bank = ps.tile([P, BANK], F32, name="bank", tag="bank")
-            v = stage["w1", j][:].bitcast(BF16).rearrange("p (e c r s) -> p e c r s", e=2, c=4, s=2)
-            for e in range(2):
-                for k in range(8):
-                    nc.tensor.matmul(out=bank[:, e * P : (e + 1) * P], lhsT=v[:, e, k // 2, :, k % 2],
-                                     rhs=x0T[:, k * P : (k + 1) * P], start=(k == 0), stop=(k == 7))
-            return bank
+        def evacuate(pattern):
+            n_e = len([s for s in side if s[1] == "e"])
+            for i in range(n_e):
+                state["on_v"] = pattern[i % len(pattern)] == "v"
+                do_side([s[1] for s in side].index("e"))
 
-        def anchors_w0(o):
+        def anchors(nm, hf):
             bank = ps.tile([P, BANK], F32, name="bank", tag="bank")
-            v = w0T[o][:].bitcast(BF16).rearrange("p (c r s) -> p c r s", c=4, s=2)
+            v = wT[nm, hf][:].bitcast(BF16).rearrange("p (c r s) -> p c r s", c=4, s=2)
             for k in range(8):
                 nc.tensor.matmul(out=bank[:], lhsT=x0T[:, k * P : (k + 1) * P], rhs=v[:, k // 2, :, k % 2],
                                  start=(k == 0), stop=(k == 7))
-            nc.scalar.copy(out=r0[:, o * BANK : (o + 1) * BANK], in_=bank[:])
+            return bank
 
-        count = [0] * NHT
-
-        def cls(ht, q):
-            if q == 0:
-                return "d"
-            if q == NQ - 1:
-                return "f"
-            return TABLE[q][ht]
-
-        def kinds(ht):
-            return [cls(ht, q) for q in range(NQ)]
-
-        def nslot(ht):
-            return 5 + len([c for c in kinds(ht) if c == "v"]) + (1 if "p" in kinds(ht) else 0)
-
-        assert max([nslot(ht) for ht in range(NHT)]) <= NS
-        last_p = max([(q, ht) for ht in range(4) for q in range(NQ) if cls(ht, q) == "p"] + [(-1, -1)])
-
-        owed = []
-        pb = {}
-
-        def pe_sums():
-            while owed:
-                ht, z, last = owed.pop(0)
-                first = "t" not in pb
-                if first:
-                    pb["t"] = pbp.tile([P, BANK], F32, name="pb")
-                for i in range(4):
-                    nc.tensor.matmul(out=pb["t"][:, ht * P : (ht + 1) * P], lhsT=z[:, i * P : (i + 1) * P], rhs=ident[:],
-                                     is_transpose=True, start=(first and i == 0), stop=(last and i == 3))
-                if last:
-                    nc.scalar.copy(out=pbs[:], in_=pb["t"][:])
-                    state["back"] = True
-
-        def pe_back():
-            bank = transposes(pbs[:])
-            for ht in range(4):
-                if "p" in kinds(ht):
-                    s = nslot(ht) - 1
-                    nc.scalar.copy(out=fin[ht][:, s * P : (s + 1) * P], in_=bank[:, ht * P : (ht + 1) * P])
-
-        def quantise_pooled(g):
-            nc.scalar.copy(out=pg[g][:].rearrange("p (b t) -> p b t", t=4), in_=pT[g][:].rearrange("p (t b) -> p b t", t=4))
-            nc.vector.quantize_mx(out=pc[:, g * P : (g + 1) * P].bitcast(FP8X4), scales=pscale[:, g * P : (g + 1) * P], in_=pg[g][:])
-
-        def unit(ht, q):
-            j, e = ht // 2, ht % 2
-            xc, xs = codes[q]
+        def unit(n, hf):
+            xc, xs = codes[n // 4]
             bank = ps.tile([P, BANK], F32, name="bank", tag="bank")
             for g in range(2):
-                lo = e * 2 * P + g * P
-                nc.tensor.matmul_mx(out=bank[:], lhsT=w1c[j][:, lo : lo + P].bitcast(FP8X4), lhsT_scale=w1s[j][:, lo : lo + P],
-                                    rhs=xc[:, g * BANK : (g + 1) * BANK].bitcast(FP8X4), rhs_scale=xs[:, g * BANK : (g + 1) * BANK],
-                                    start=(g == 0), stop=(g == 1))
+                lo = g * BANK + (n % 4) * P
+                nc.tensor.matmul_mx(out=bank[:], lhsT=xc[:, lo : lo + P].bitcast(FP8X4), lhsT_scale=xs[:, lo : lo + P],
+                                    rhs=wc["w1", hf][:, g * BANK : (g + 1) * BANK].bitcast(FP8X4),
+                                    rhs_scale=ws["w1", hf][:, g * BANK : (g + 1) * BANK], start=(g == 0), stop=(g == 1))
             z = zp.tile([P, BANK], F32, name="z", tag="z")
-            nc.vector.tensor_tensor(out=z[:].rearrange("p (i b) -> p i b", i=4), in0=bank[:].rearrange("p (i b) -> p i b", i=4),
-                                    in1=h0T[j][:, e * P : (e + 1) * P].unsqueeze(1).to_broadcast([P, 4, P]), op=ADD)
+            nc.vector.tensor_tensor(out=z[:], in0=bank[:], in1=prod["w1", hf][:], op=ADD)
             return z
 
         vlate = []
+        started = []
 
-        done = []
-        ready2 = []
+        def late_add():
+            hf, z = vlate.pop(0)
+            nc.vector.tensor_tensor(out=acc["v", hf][:], in0=acc["v", hf][:], in1=z[:], op=ADD)
 
-        def late_reduce():
-            ht, z, s = vlate.pop(0)
-            if z is not None:
-                nc.vector.tensor_reduce(out=fin[ht][:, s * P : (s + 1) * P], in_=z[:].rearrange("p (i b) -> p b i", i=4), axis=AX, op=ADD)
+        def finish(c, hf, z):
+            if c in "gv" and (c, hf) not in started:
+                started.append((c, hf))
+                nc.scalar.activation(out=acc[c, hf][:], in_=z[:], func=TANH)
                 return
-            nc.vector.tensor_reduce(out=pT[ht // 4][:, (ht % 4) * P : (ht % 4 + 1) * P],
-                                    in_=fin[ht][:, 0 : nslot(ht) * P].rearrange("p (s b) -> p b s", s=nslot(ht)), axis=AX, op=ADD)
-            done.append(ht)
-            g = ht // 4
-            if len([d for d in done if d // 4 == g]) == 4:
-                quantise_pooled(g)
-                ready2.append(g)
+            nc.scalar.activation(out=z[:], in_=z[:], func=TANH)
+            if c == "g":
+                nc.gpsimd.tensor_tensor(out=acc["g", hf][:], in0=acc["g", hf][:], in1=z[:], op=ADD)
+            elif c == "v":
+                vlate.append((hf, z))
+            else:
+                owed.append((hf, z, state["units"]))
+
+        def quantise_pooled(g):
+            nc.scalar.copy(out=pg[g][:].rearrange("p (b t) -> p b t", t=4), in_=accT[g][:].rearrange("p (t b) -> p b t", t=4))
+            nc.vector.quantize_mx(out=pc[:, g * P : (g + 1) * P].bitcast(FP8X4), scales=pscale[:, g * P : (g + 1) * P], in_=pg[g][:])
 
         obs = []
 
@@ -274,39 +250,13 @@ def tile_attention_pa_t_kernel(tc, x, W1, W2, W0, out):
                     ob = ps.tile([P, BANK], F32, name="bank", tag="bank")
                     obs.append(ob)
                 nc.tensor.matmul_mx(out=obs[o][:], lhsT=pc[:, g * P : (g + 1) * P].bitcast(FP8X4), lhsT_scale=pscale[:, g * P : (g + 1) * P],
-                                    rhs=w2c[o][:, g * BANK : (g + 1) * BANK].bitcast(FP8X4), rhs_scale=w2s[o][:, g * BANK : (g + 1) * BANK],
+                                    rhs=wc["w2", o][:, g * BANK : (g + 1) * BANK].bitcast(FP8X4), rhs_scale=ws["w2", o][:, g * BANK : (g + 1) * BANK],
                                     start=first, stop=last)
 
-        def finish(ht, z):
-            k = count[ht]
-            count[ht] += 1
-            c = cls(ht, k)
-            if c == "d":
-                nc.scalar.activation(out=acc[ht][:], in_=z[:], func=TANH)
-            elif c == "f":
-                nc.scalar.activation(out=fin[ht][:, 0:BANK], in_=z[:], func=TANH)
-                vlate.append((ht, None, 0))
-            elif c == "p":
-                nc.scalar.activation(out=z[:], in_=z[:], func=TANH)
-                owed.append((ht, z, (k, ht) == last_p))
-            elif c == "v":
-                nc.scalar.activation(out=z[:], in_=z[:], func=TANH)
-                vlate.append((ht, z, 5 + len([c for c in kinds(ht)[0:k] if c == "v"])))
-            else:
-                nc.scalar.activation(out=z[:], in_=z[:], func=TANH)
-                for o in range(0, BANK, G_W):
-                    nc.gpsimd.tensor_tensor(out=acc[ht][:, o : o + G_W], in0=acc[ht][:, o : o + G_W], in1=z[:, o : o + G_W], op=ADD)
-            if k == max([q for q in range(NQ) if cls(ht, q) in "dg"]):
-                a = acc[ht]
-                nc.gpsimd.tensor_tensor(out=a[:, 0 : 2 * P], in0=a[:, 0 : 2 * P], in1=a[:, 2 * P : 4 * P], op=ADD)
-                nc.gpsimd.tensor_tensor(out=fin[ht][:, 4 * P : 5 * P], in0=a[:, 0:P], in1=a[:, P : 2 * P], op=ADD)
-
-        arrivals = []
-        for n in range(NJ):
-            arrivals += [("w1", n), ("x", n)]
-        arrivals += [("x", n) for n in range(NJ, NQ)]
-        extras = [("w0", 0), ("w0", 1), ("w2", 0), ("w2", 1)]
-        loads = arrivals[0:9] + [("w0", 0), ("x", 5), ("w0", 1), ("x", 6), ("w2", 0), ("x", 7), ("w2", 1), ("x", 8)]
+        arrivals = [("w1", 0), ("w1", 1), ("x", 0), ("x", 1), ("w1", 2), ("w1", 3)] + [("x", n) for n in range(2, NQ)]
+        extras = [("w0", 0), ("w0", 1), ("w2", 0), ("w2", 1), ("p", 0), ("p", 1)]
+        plan = [(PLAN_Q[i], extras[i]) for i in range(6)]
+        loads = arrivals[0:8] + [("w0", 0), ("x", 4), ("w0", 1), ("x", 5), ("w2", 0), ("x", 6), ("w2", 1), ("x", 7), ("x", 8)]
         live = {"x": 0, "w": 0}
 
         def pump():
@@ -319,71 +269,87 @@ def tile_attention_pa_t_kernel(tc, x, W1, W2, W0, out):
             live["x" if item[0] == "x" else "w"] -= 1
             pump()
 
+        events = []
+        for item in arrivals:
+            units = []
+            if item == ("w1", 3):
+                units = [(n, 1, FIRST1[n]) for n in range(8)]
+            elif item[0] == "x":
+                q = item[1]
+                for i in range(4):
+                    for hf in range(2):
+                        c = TABLE[q][2 * i + hf] if q >= 2 else (TABLE[q][i] if hf == 0 else ".")
+                        if c != ".":
+                            units.append((4 * q + i, hf, c))
+            if item == ("x", NQ - 1):
+                units = [u for u in units if u[1] == 0] + [u for u in units if u[1] == 1]
+            events.append(units)
+        for units in events:
+            for n, hf, c in units:
+                if c == "p":
+                    left[hf] += 1
+        used = sorted(set([(c if c != "d" else "g", hf) for units in events for n, hf, c in units if c in "dgv"]))
+        for c, hf in used:
+            left[hf] += 1
+
         nc.sync.dma_start(out=x0n[:], in_=x[:, 0, :])
         pump()
         bank0 = transposes(x0n[:].bitcast(F32))
         nc.vector.tensor_copy(out=x0T[:].rearrange("p (c s b) -> p c s b", c=4, s=2),
                               in_=bank0[:].bitcast(BF16).rearrange("p (c b s) -> p c s b", c=4, s=2))
         prep_and_pump(arrivals[0])
-        have = {"w1": [], "x": []}
-        plan = [(PLAN_Q[i], (extras + [("p", 0), ("p", 1)])[i]) for i in range(6)]
-        obs = []
-        def evacuate(pattern):
-            n_e = len([s for s in side if s[1] == "e"])
-            for i in range(n_e):
-                state["on_v"] = pattern[i % len(pattern)] == "v"
-                do_side([s[1] for s in side].index("e"))
-
         for n in range(len(arrivals)):
             item = arrivals[n]
+            units = events[n]
             flush(item)
-            hb = None
-            if item[0] == "w1":
-                units = [(2 * item[1] + e, q) for q in have["x"] for e in range(2)]
-            else:
-                units = [(ht, item[1]) for j in have["w1"] for ht in (2 * j, 2 * j + 1)]
-            long_event = len(units) == NHT
-            if item == ("x", NQ - 1):
-                units = [(ht, item[1]) for ht in LAST_ORDER]
+            long_event = len(units) == 8
             if n + 1 < len(arrivals):
                 prep_and_pump(arrivals[n + 1])
-            if item[0] == "w1":
-                hb = anchors_h(item[1])
-            have[item[0]].append(item[1])
+            hb = None
+            if item[0] == "w1" and item[1] % 2 == 1:
+                hb = anchors("w1", item[1] // 2)
             evacuate(PAT_LONG if long_event else PAT_SHORT)
             if not long_event:
-                while side:
+                while side and side[0][1] == "q":
                     do_side()
             if hb is not None:
-                nc.scalar.copy(out=h0T[item[1]][:], in_=hb[:, 0 : 2 * P])
+                nc.scalar.copy(out=prod["w1", item[1] // 2][:], in_=hb[:])
             for k in range(len(units)):
-                if long_event and k in EXTRA_AT and plan and plan[0][0] <= item[1]:
+                if long_event and k in EXTRA_AT and plan and item[0] == "x" and plan[0][0] <= item[1]:
                     what = plan.pop(0)[1]
                     if what[0] == "p":
-                        anchors_w0(what[1])
+                        wb = anchors("w0", what[1])
+                        nc.scalar.copy(out=prod["w0", what[1]][:], in_=wb[:])
                     else:
                         prep_and_pump(what)
                         evacuate(PAT_LONG)
-                if item == ("x", NQ - 1) and k == SUMS_AT:
+                if n == len(arrivals) - 1 and k == LAST_RUN_AT:
+                    while vlate:
+                        late_add()
+                    for c2, h2 in used:
+                        if h2 == 0 or FLUSH_EARLY:
+                            pe_sum(h2, acc[c2, h2])
                     pe_sums()
-                if item == ("x", NQ - 1) and k == BACK_AT and state["back"]:
-                    state["back"] = False
-                    pe_back()
-                z = unit(units[k][0], units[k][1])
+                    quantise_pooled(0)
+                nn, hf, c = units[k]
+                z = unit(nn, hf)
+                state["units"] += 1
                 while len(vlate) > V_LAG:
-                    late_reduce()
+                    late_add()
                 if side and k % 4 == Q_AT:
                     do_side()
-                finish(units[k][0], z)
-        while vlate:
-            late_reduce()
-            if len(ready2) == 1:
-                second(ready2[0], True, False)
-                ready2.append(-1)
-        second(ready2[2], False, True)
+                finish("g" if c == "d" else c, hf, z)
+        second(0, True, False)
+        state["units"] += P_LAG
+        for c2, h2 in used:
+            if h2 == 1 and not FLUSH_EARLY:
+                pe_sum(h2, acc[c2, h2])
+        pe_sums()
+        quantise_pooled(1)
+        second(1, False, True)
         for o in range(2):
             s = slice(o * BANK, (o + 1) * BANK)
-            nc.vector.tensor_tensor(out=res[:, s], in0=obs[o][:], in1=r0[:, s], op=ADD)
+            nc.vector.tensor_tensor(out=res[:, s], in0=obs[o][:], in1=prod["w0", o][:], op=ADD)
             if o == 0:
                 nc.sync.dma_start(out=out[:, s], in_=res[:, s])
             else:

@@ -17,17 +17,21 @@ BANK = 512
 NQ = 9
 FLOPS = 2 * 128 * 36 * 1024 * 1024 + 3 * 2 * 128 * 1024 * 1024
 
-TABLE = ("dggg....", "gggg....", "gpgpgpgv", "gpgpgpgv", "gpgpgpgv", "gpgpgpgv", "gpgpgpgv", "gpgpgpgv", "pppppppp")
+TABLE = ("dggg....", "gggg....", "gpgpgpgv", "gpgpgpgv", "gpgpgpgv", "gpgpgpgv", "gpgpgpgv", "gpgpgpgp", "pppppppp")
 FIRST1 = "dpgpgpgv"
 PAT_LONG = "sssv"
 PAT_SHORT = "svsv"
 ZB = 12
 Q_AT = 3
+Q_MOD = 4
+HF_MAJOR = 0
+G_W = 512
 EXTRA_AT = (4,)
 PLAN_Q = (2, 3, 4, 5, 6, 7)
-V_LAG = 1
+V_LAG = 2
 P_LAG = 2
-FLUSH_EARLY = False
+G_LAG = 5
+N_WARM = 6
 LAST_RUN_AT = 6
 NBANK = 7
 
@@ -50,6 +54,13 @@ def tile_attention_pa_t_kernel(tc, x, W1, W2, W0, out):
         warm = const.tile([P, 1], F32, name="warm")
         nc.vector.memset(warm[:], 0.0)
         nc.scalar.activation(out=warm[:], in_=warm[:], func=TANH)
+
+        if N_WARM:
+            zeros = const.tile([P, BANK], BF16, name="zeros")
+            nc.vector.memset(zeros[:], 0.0)
+            wbank = ps.tile([P, BANK], F32, name="bank", tag="bank")
+            for i in range(N_WARM):
+                nc.tensor.matmul(out=wbank[:], lhsT=zeros[:, 0:P], rhs=zeros[:], start=True, stop=True)
 
         x0n = const.tile([P, F], BF16, name="x0n")
         x0T = const.tile([P, F], BF16, name="x0T")
@@ -117,6 +128,7 @@ def tile_attention_pa_t_kernel(tc, x, W1, W2, W0, out):
         side = []
         codes = {}
         stage = {}
+        last_seq = {}
         owed = []
         accT = {}
         left = {0: 0, 1: 0}
@@ -137,6 +149,10 @@ def tile_attention_pa_t_kernel(tc, x, W1, W2, W0, out):
             while owed and owed[0][2] <= state["units"] - P_LAG:
                 hf, z, seq = owed.pop(0)
                 pe_sum(hf, z)
+            for key in sorted(last_seq):
+                if last_seq[key] <= state["units"] - (G_LAG if key[0] == "g" else V_LAG + P_LAG):
+                    last_seq.pop(key)
+                    pe_sum(key[1], acc[key])
 
         def quant_view(t):
             return t[:].bitcast(F32).rearrange("p (g i r u) -> p g i r u", g=2, i=4, u=2)
@@ -145,7 +161,9 @@ def tile_attention_pa_t_kernel(tc, x, W1, W2, W0, out):
             kind, n = item
             words = nat[item][:].bitcast(F32)
             banks = []
-            if kind == "w1":
+            if item == ("w1", 0):
+                order = (BANK, 0, 3 * BANK, 2 * BANK)
+            elif kind == "w1":
                 order = (BANK, 3 * BANK, 0, 2 * BANK)
             else:
                 order = (0, BANK, 2 * BANK, 3 * BANK)
@@ -161,13 +179,16 @@ def tile_attention_pa_t_kernel(tc, x, W1, W2, W0, out):
                 hf = n // 2
                 if n % 2 == 0:
                     stage[hf] = stg.tile([P, 4 * F], BF16, name="xg", tag="xg", align_bytes=64)
-                for e in range(2):
-                    side.append((item, "e", quant_view(stage[hf])[:, :, 2 * (n % 2) + e], banks[e][:].rearrange("p (g u r) -> p g r u", g=2, u=2)))
+                dst = wT["w1", hf][:].rearrange("p (c t r) -> p c t r", c=4, t=4)
+                for o in order:
+                    e = o // (2 * BANK)
+                    bank = banks[order.index(o)]
+                    if o % (2 * BANK) == BANK:
+                        side.append((item, "e", quant_view(stage[hf])[:, :, 2 * (n % 2) + e], bank[:].rearrange("p (g u r) -> p g r u", g=2, u=2)))
+                    else:
+                        side.append((item, "e", dst[:, :, 2 * (n % 2) + e], bank[:].rearrange("p (c r) -> p c r", c=4)))
                 if n % 2 == 1:
                     side.append((item, "q", stage[hf], None))
-                dst = wT["w1", hf][:].rearrange("p (c t r) -> p c t r", c=4, t=4)
-                for e in range(2):
-                    side.append((item, "e", dst[:, :, 2 * (n % 2) + e], banks[2 + e][:].rearrange("p (c r) -> p c r", c=4)))
             else:
                 dst = wT["w0", n][:].rearrange("p (c t r) -> p c t r", c=4, t=4)
                 for i in range(4):
@@ -198,11 +219,11 @@ def tile_attention_pa_t_kernel(tc, x, W1, W2, W0, out):
                 state["on_v"] = pattern[i % len(pattern)] == "v"
                 do_side([s[1] for s in side].index("e"))
 
-        def anchors(nm, hf):
+        def anchors(nm, hf, lo=0, width=BANK):
             bank = ps.tile([P, BANK], F32, name="bank", tag="bank")
             v = wT[nm, hf][:].bitcast(BF16).rearrange("p (c r s) -> p c r s", c=4, s=2)
             for k in range(8):
-                nc.tensor.matmul(out=bank[:], lhsT=x0T[:, k * P : (k + 1) * P], rhs=v[:, k // 2, :, k % 2],
+                nc.tensor.matmul(out=bank[:, 0:width], lhsT=x0T[:, k * P : (k + 1) * P], rhs=v[:, k // 2, lo : lo + width, k % 2],
                                  start=(k == 0), stop=(k == 7))
             return bank
 
@@ -222,7 +243,7 @@ def tile_attention_pa_t_kernel(tc, x, W1, W2, W0, out):
         started = []
 
         def late_add():
-            hf, z = vlate.pop(0)
+            hf, z, seq = vlate.pop(0)
             nc.vector.tensor_tensor(out=acc["v", hf][:], in0=acc["v", hf][:], in1=z[:], op=ADD)
 
         def finish(c, hf, z):
@@ -232,9 +253,10 @@ def tile_attention_pa_t_kernel(tc, x, W1, W2, W0, out):
                 return
             nc.scalar.activation(out=z[:], in_=z[:], func=TANH)
             if c == "g":
-                nc.gpsimd.tensor_tensor(out=acc["g", hf][:], in0=acc["g", hf][:], in1=z[:], op=ADD)
+                for o in range(0, BANK, G_W):
+                    nc.gpsimd.tensor_tensor(out=acc["g", hf][:, o : o + G_W], in0=acc["g", hf][:, o : o + G_W], in1=z[:, o : o + G_W], op=ADD)
             elif c == "v":
-                vlate.append((hf, z))
+                vlate.append((hf, z, state["units"]))
             else:
                 owed.append((hf, z, state["units"]))
 
@@ -281,8 +303,10 @@ def tile_attention_pa_t_kernel(tc, x, W1, W2, W0, out):
                         c = TABLE[q][2 * i + hf] if q >= 2 else (TABLE[q][i] if hf == 0 else ".")
                         if c != ".":
                             units.append((4 * q + i, hf, c))
-            if item == ("x", NQ - 1):
+            if item == ("x", NQ - 1) or (HF_MAJOR == 1 and len(units) == 8 and item[0] == "x"):
                 units = [u for u in units if u[1] == 0] + [u for u in units if u[1] == 1]
+            elif HF_MAJOR == 2 and len(units) == 8 and item[0] == "x":
+                units = [u for u in units if u[1] == 1] + [u for u in units if u[1] == 0]
             events.append(units)
         for units in events:
             for n, hf, c in units:
@@ -291,6 +315,12 @@ def tile_attention_pa_t_kernel(tc, x, W1, W2, W0, out):
         used = sorted(set([(c if c != "d" else "g", hf) for units in events for n, hf, c in units if c in "dgv"]))
         for c, hf in used:
             left[hf] += 1
+        seq = 0
+        for units in events:
+            for n, hf, c in units:
+                seq += 1
+                if c in "dgv":
+                    last_seq["g" if c == "d" else c, hf] = seq
 
         nc.sync.dma_start(out=x0n[:], in_=x[:, 0, :])
         pump()
@@ -298,22 +328,26 @@ def tile_attention_pa_t_kernel(tc, x, W1, W2, W0, out):
         nc.vector.tensor_copy(out=x0T[:].rearrange("p (c s b) -> p c s b", c=4, s=2),
                               in_=bank0[:].bitcast(BF16).rearrange("p (c b s) -> p c s b", c=4, s=2))
         prep_and_pump(arrivals[0])
+        evacuate(PAT_SHORT)
         for n in range(len(arrivals)):
             item = arrivals[n]
             units = events[n]
             flush(item)
             long_event = len(units) == 8
+            hb = None
+            if n == 0:
+                hb = anchors("w1", 0, 0, 2 * P)
             if n + 1 < len(arrivals):
                 prep_and_pump(arrivals[n + 1])
-            hb = None
-            if item[0] == "w1" and item[1] % 2 == 1:
-                hb = anchors("w1", item[1] // 2)
+            if item[0] == "w1" and n > 0:
+                hb = anchors("w1", item[1] // 2, (item[1] % 2) * 2 * P, 2 * P)
             evacuate(PAT_LONG if long_event else PAT_SHORT)
             if not long_event:
                 while side and side[0][1] == "q":
                     do_side()
             if hb is not None:
-                nc.scalar.copy(out=prod["w1", item[1] // 2][:], in_=hb[:])
+                lo = (item[1] % 2) * 2 * P
+                nc.scalar.copy(out=prod["w1", item[1] // 2][:, lo : lo + 2 * P], in_=hb[:, 0 : 2 * P])
             for k in range(len(units)):
                 if long_event and k in EXTRA_AT and plan and item[0] == "x" and plan[0][0] <= item[1]:
                     what = plan.pop(0)[1]
@@ -324,27 +358,21 @@ def tile_attention_pa_t_kernel(tc, x, W1, W2, W0, out):
                         prep_and_pump(what)
                         evacuate(PAT_LONG)
                 if n == len(arrivals) - 1 and k == LAST_RUN_AT:
-                    while vlate:
-                        late_add()
-                    for c2, h2 in used:
-                        if h2 == 0 or FLUSH_EARLY:
-                            pe_sum(h2, acc[c2, h2])
                     pe_sums()
+                    assert left[0] == 0
                     quantise_pooled(0)
                 nn, hf, c = units[k]
                 z = unit(nn, hf)
                 state["units"] += 1
-                while len(vlate) > V_LAG:
+                while vlate and vlate[0][2] <= state["units"] - V_LAG:
                     late_add()
-                if side and k % 4 == Q_AT:
+                if side and k % Q_MOD == Q_AT:
                     do_side()
                 finish("g" if c == "d" else c, hf, z)
         second(0, True, False)
         state["units"] += P_LAG
-        for c2, h2 in used:
-            if h2 == 1 and not FLUSH_EARLY:
-                pe_sum(h2, acc[c2, h2])
         pe_sums()
+        assert left[1] == 0
         quantise_pooled(1)
         second(1, False, True)
         for o in range(2):

@@ -17,9 +17,9 @@ BANK = 512
 NQ = 9
 FLOPS = 2 * 128 * 36 * 1024 * 1024 + 3 * 2 * 128 * 1024 * 1024
 
-TABLE = ("dggg....", "gggg....", "gpgpgpgv", "gpgpgpgv", "gpgpgpgv", "gpgpgpgv", "gpgpgpgv", "gpgpgpgp", "pppppppp")
+TABLE = ("dggg....", "gggg....", "gvgpgvgp", "gvgpgvgp", "gvgpgvgp", "gvgpgvgp", "gvgpgvgp", "gvgpgpgv", "pppppppp")
 FIRST1 = "dpgpgpgv"
-PAT_LONG = "sssv"
+PAT_LONG = "ssss"
 PAT_SHORT = "svsv"
 ZB = 12
 Q_AT = 3
@@ -28,11 +28,11 @@ HF_MAJOR = 0
 G_W = 512
 EXTRA_AT = (4,)
 PLAN_Q = (2, 3, 4, 5, 6, 7)
-V_LAG = 2
+V_LAG = 4
 P_LAG = 2
 G_LAG = 5
 N_WARM = 6
-LAST_RUN_AT = 6
+LAST_RUN_AT = 5
 NBANK = 7
 
 
@@ -264,6 +264,14 @@ def tile_attention_pa_t_kernel(tc, x, W1, W2, W0, out):
             nc.scalar.copy(out=pg[g][:].rearrange("p (b t) -> p b t", t=4), in_=accT[g][:].rearrange("p (t b) -> p b t", t=4))
             nc.vector.quantize_mx(out=pc[:, g * P : (g + 1) * P].bitcast(FP8X4), scales=pscale[:, g * P : (g + 1) * P], in_=pg[g][:])
 
+        pooled = []
+
+        def try_pool():
+            for g in range(2):
+                if left[g] == 0 and g not in pooled:
+                    pooled.append(g)
+                    quantise_pooled(g)
+
         obs = []
 
         def second(g, first, last):
@@ -359,8 +367,7 @@ def tile_attention_pa_t_kernel(tc, x, W1, W2, W0, out):
                         evacuate(PAT_LONG)
                 if n == len(arrivals) - 1 and k == LAST_RUN_AT:
                     pe_sums()
-                    assert left[0] == 0
-                    quantise_pooled(0)
+                    try_pool()
                 nn, hf, c = units[k]
                 z = unit(nn, hf)
                 state["units"] += 1
@@ -369,12 +376,19 @@ def tile_attention_pa_t_kernel(tc, x, W1, W2, W0, out):
                 if side and k % Q_MOD == Q_AT:
                     do_side()
                 finish("g" if c == "d" else c, hf, z)
-        second(0, True, False)
+        if pooled:
+            second(pooled[0], True, False)
+        while vlate:
+            late_add()
         state["units"] += P_LAG
         pe_sums()
-        assert left[1] == 0
-        quantise_pooled(1)
-        second(1, False, True)
+        state["units"] += 100
+        pe_sums()
+        n_before = len(pooled)
+        try_pool()
+        assert len(pooled) == 2
+        for g in pooled[n_before:]:
+            second(g, g == pooled[0], g == pooled[1])
         for o in range(2):
             s = slice(o * BANK, (o + 1) * BANK)
             nc.vector.tensor_tensor(out=res[:, s], in0=obs[o][:], in1=prod["w0", o][:], op=ADD)

@@ -68,8 +68,8 @@ def tile_attention_pa_t_kernel(tc, x, W1, W2, W0, out):
         ws = {}
         for nm in ("w1", "w2"):
             for hf in range(2):
-                wc[nm, hf] = const.tile([P, F], U32, name="c%s%d" % (nm, hf), align_bytes=64)
-                ws[nm, hf] = const.tile([P, F], U8, name="s%s%d" % (nm, hf), align_bytes=64)
+                wc[nm, hf] = const.tile([P, F], U32, name="c%s%d" % (nm, hf), align_bytes=256)
+                ws[nm, hf] = const.tile([P, F], U8, name="s%s%d" % (nm, hf), align_bytes=256)
         wT = {}
         prod = {}
         for nm in ("w1", "w0"):
@@ -80,9 +80,9 @@ def tile_attention_pa_t_kernel(tc, x, W1, W2, W0, out):
         for e in ("g", "v"):
             for hf in range(2):
                 acc[e, hf] = const.tile([P, BANK], F32, name="acc%s%d" % (e, hf))
-        pg = [const.tile([P, BANK], BF16, name="pg%d" % g, align_bytes=64) for g in range(2)]
-        pc = const.tile([P, 2 * P], U32, name="pc", align_bytes=64)
-        pscale = const.tile([P, 2 * P], U8, name="pscale", align_bytes=64)
+        pg = [const.tile([P, BANK], BF16, name="pg%d" % g, align_bytes=256) for g in range(2)]
+        pc = const.tile([P, 2 * P], U32, name="pc", align_bytes=256)
+        pscale = const.tile([P, 2 * P], U8, name="pscale", align_bytes=256)
         res = const.tile([P, F], F32, name="res")
 
         nat = {}
@@ -171,14 +171,14 @@ def tile_attention_pa_t_kernel(tc, x, W1, W2, W0, out):
                 banks.append(transposes(words[:, o : o + BANK]))
             pe_sums()
             if kind == "x" or kind == "w2":
-                xg = stg.tile([P, 4 * F], BF16, name="xg", tag="xg", align_bytes=64)
+                xg = stg.tile([P, 4 * F], BF16, name="xg", tag="xg", align_bytes=256)
                 for i in range(4):
                     side.append((item, "e", quant_view(xg)[:, :, i], banks[i][:].rearrange("p (g u r) -> p g r u", g=2, u=2)))
                 side.append((item, "q", xg, None))
             elif kind == "w1":
                 hf = n // 2
                 if n % 2 == 0:
-                    stage[hf] = stg.tile([P, 4 * F], BF16, name="xg", tag="xg", align_bytes=64)
+                    stage[hf] = stg.tile([P, 4 * F], BF16, name="xg", tag="xg", align_bytes=256)
                 dst = wT["w1", hf][:].rearrange("p (c t r) -> p c t r", c=4, t=4)
                 for o in order:
                     e = o // (2 * BANK)
@@ -200,8 +200,8 @@ def tile_attention_pa_t_kernel(tc, x, W1, W2, W0, out):
             if what == "e":
                 copy(a, b)
             elif kind == "x":
-                xc = xcp.tile([P, F], U32, name="xc", tag="xc", align_bytes=64)
-                xs = xcp.tile([P, F], U8, name="xs", tag="xs", align_bytes=64)
+                xc = xcp.tile([P, F], U32, name="xc", tag="xc", align_bytes=256)
+                xs = xcp.tile([P, F], U8, name="xs", tag="xs", align_bytes=256)
                 nc.vector.quantize_mx(out=xc[:].bitcast(FP8X4), scales=xs[:], in_=a[:])
                 codes[n] = (xc, xs)
             elif kind == "w2":

@@ -27,7 +27,12 @@ Q_MOD = 4
 HF_MAJOR = 0
 G_W = 512
 EXTRA_AT = (4,)
-PLAN_Q = (2, 3, 4, 5, 6, 7)
+PLAN_Q = (6, 7)
+HALVES_FROM = 5
+RUN_AT = (4,)
+LAST_RUNS = (4,)
+LAST_ROOM = 8
+LONG_RUNS = False
 V_LAG = 4
 P_LAG = 2
 G_LAG = 5
@@ -145,19 +150,39 @@ def tile_attention_pa_t_kernel(tc, x, W1, W2, W0, out):
                 nc.tensor.matmul(out=accT[hf][:, t * P : (t + 1) * P], lhsT=src[:, t * P : (t + 1) * P], rhs=ident[:],
                                  is_transpose=True, start=(first and t == 0), stop=(left[hf] == 0 and t == 3))
 
-        def pe_sums():
-            while owed and owed[0][2] <= state["units"] - P_LAG:
+        def pe_sums(room=100):
+            while room > 0 and owed and owed[0][2] <= state["units"] - P_LAG:
                 hf, z, seq = owed.pop(0)
                 pe_sum(hf, z)
+                room -= 1
             for key in sorted(last_seq):
-                if last_seq[key] <= state["units"] - (G_LAG if key[0] == "g" else V_LAG + P_LAG):
+                if room > 0 and last_seq[key] <= state["units"] - (G_LAG if key[0] == "g" else V_LAG + P_LAG):
                     last_seq.pop(key)
                     pe_sum(key[1], acc[key])
+                    room -= 1
 
         def quant_view(t):
             return t[:].bitcast(F32).rearrange("p (g i r u) -> p g i r u", g=2, i=4, u=2)
 
-        def prep(item):
+        def prep_half(item, part):
+            kind, n = item
+            words = nat[item][:].bitcast(F32)
+            if kind == "w2" and part == 0:
+                stage[item] = stg.tile([P, 4 * F], BF16, name="xg", tag="xg", align_bytes=256)
+            for i in (2 * part, 2 * part + 1):
+                bank = transposes(words[:, i * BANK : (i + 1) * BANK])
+                if kind == "w2":
+                    side.append((item, "e", quant_view(stage[item])[:, :, i], bank[:].rearrange("p (g u r) -> p g r u", g=2, u=2)))
+                else:
+                    dst = wT["w0", n][:].rearrange("p (c t r) -> p c t r", c=4, t=4)
+                    side.append((item, "e", dst[:, :, i], bank[:].rearrange("p (c r) -> p c r", c=4)))
+            if kind == "w2" and part == 1:
+                side.append((item, "q", stage[item], None))
+            if part == 1:
+                live["w"] -= 1
+                pump()
+
+        def prep(item, more=None):
             kind, n = item
             words = nat[item][:].bitcast(F32)
             banks = []
@@ -169,7 +194,8 @@ def tile_attention_pa_t_kernel(tc, x, W1, W2, W0, out):
                 order = (0, BANK, 2 * BANK, 3 * BANK)
             for o in order:
                 banks.append(transposes(words[:, o : o + BANK]))
-            pe_sums()
+            if LONG_RUNS:
+                pe_sums()
             if kind == "x" or kind == "w2":
                 xg = stg.tile([P, 4 * F], BF16, name="xg", tag="xg", align_bytes=256)
                 for i in range(4):
@@ -284,9 +310,9 @@ def tile_attention_pa_t_kernel(tc, x, W1, W2, W0, out):
                                     start=first, stop=last)
 
         arrivals = [("w1", 0), ("w1", 1), ("x", 0), ("x", 1), ("w1", 2), ("w1", 3)] + [("x", n) for n in range(2, NQ)]
-        extras = [("w0", 0), ("w0", 1), ("w2", 0), ("w2", 1), ("p", 0), ("p", 1)]
-        plan = [(PLAN_Q[i], extras[i]) for i in range(6)]
-        loads = arrivals[0:8] + [("w0", 0), ("x", 4), ("w0", 1), ("x", 5), ("w2", 0), ("x", 6), ("w2", 1), ("x", 7), ("x", 8)]
+        extras = [("p", 0), ("p", 1)]
+        plan = [(PLAN_Q[i], extras[i]) for i in range(2)]
+        loads = arrivals[0:7] + [("w0", 0), ("x", 3), ("x", 4), ("w0", 1), ("x", 5), ("w2", 0), ("x", 6), ("x", 7), ("w2", 1), ("x", 8)]
         live = {"x": 0, "w": 0}
 
         def pump():
@@ -294,8 +320,8 @@ def tile_attention_pa_t_kernel(tc, x, W1, W2, W0, out):
                 live["x" if loads[0][0] == "x" else "w"] += 1
                 load(loads.pop(0))
 
-        def prep_and_pump(item):
-            prep(item)
+        def prep_and_pump(item, more=None):
+            prep(item, more)
             live["x" if item[0] == "x" else "w"] -= 1
             pump()
 
@@ -337,6 +363,7 @@ def tile_attention_pa_t_kernel(tc, x, W1, W2, W0, out):
                               in_=bank0[:].bitcast(BF16).rearrange("p (c b s) -> p c s b", c=4, s=2))
         prep_and_pump(arrivals[0])
         evacuate(PAT_SHORT)
+        halves = [(w, part) for w in (("w0", 0), ("w0", 1), ("w2", 0), ("w2", 1)) for part in range(2)]
         for n in range(len(arrivals)):
             item = arrivals[n]
             units = events[n]
@@ -365,8 +392,14 @@ def tile_attention_pa_t_kernel(tc, x, W1, W2, W0, out):
                     else:
                         prep_and_pump(what)
                         evacuate(PAT_LONG)
-                if n == len(arrivals) - 1 and k == LAST_RUN_AT:
-                    pe_sums()
+                if k in (LAST_RUNS if n == len(arrivals) - 1 else RUN_AT) and len(units) == 8:
+                    room = 4 if n < len(arrivals) - 1 else LAST_ROOM
+                    if halves and n >= HALVES_FROM and k == RUN_AT[0]:
+                        more = halves.pop(0)
+                        prep_half(more[0], more[1])
+                        room = 2
+                    pe_sums(room)
+                    evacuate(PAT_LONG)
                     try_pool()
                 nn, hf, c = units[k]
                 z = unit(nn, hf)
@@ -374,7 +407,8 @@ def tile_attention_pa_t_kernel(tc, x, W1, W2, W0, out):
                 while vlate and vlate[0][2] <= state["units"] - V_LAG:
                     late_add()
                 if side and k % Q_MOD == Q_AT:
-                    do_side()
+                    urgent = [i for i in range(len(side)) if side[i][0][0] == "x"]
+                    do_side(urgent[0] if urgent else 0)
                 finish("g" if c == "d" else c, hf, z)
         if pooled:
             second(pooled[0], True, False)

@@ -17,8 +17,8 @@ BANK = 512
 NQ = 9
 FLOPS = 2 * 128 * 36 * 1024 * 1024 + 3 * 2 * 128 * 1024 * 1024
 
-TABLE = ("dggg....", "gggg....", "gvgpgvgp", "gvgpgvgp", "gvgpgvgp", "gvgpgvgp", "gvgpgvgp", "gvgpgpgv", "pppppppp")
-FIRST1 = "dpgpgpgv"
+TABLE = ("dggg....", "gggg....", "gvgpgvgp", "gvgpgvgp", "gvgpgvgp", "gvgpgvgp", "gvgpgvgp", "gvgpgvgp", "pppppppp")
+FIRST1 = "dvgpgvgp"
 PAT_LONG = "ssss"
 PAT_SHORT = "svsv"
 ZB = 12
@@ -33,7 +33,7 @@ RUN_AT = (4,)
 LAST_RUNS = (4,)
 LAST_ROOM = 8
 LONG_RUNS = False
-V_LAG = 4
+V_LAG = 6
 P_LAG = 2
 G_LAG = 5
 N_WARM = 6
@@ -187,7 +187,7 @@ def tile_attention_pa_t_kernel(tc, x, W1, W2, W0, out):
             words = nat[item][:].bitcast(F32)
             banks = []
             if item == ("w1", 0):
-                order = (BANK, 0, 3 * BANK, 2 * BANK)
+                order = (0, BANK, 2 * BANK, 3 * BANK)
             elif kind == "w1":
                 order = (BANK, 3 * BANK, 0, 2 * BANK)
             else:
@@ -213,7 +213,7 @@ def tile_attention_pa_t_kernel(tc, x, W1, W2, W0, out):
                         side.append((item, "e", quant_view(stage[hf])[:, :, 2 * (n % 2) + e], bank[:].rearrange("p (g u r) -> p g r u", g=2, u=2)))
                     else:
                         side.append((item, "e", dst[:, :, 2 * (n % 2) + e], bank[:].rearrange("p (c r) -> p c r", c=4)))
-                if n % 2 == 1:
+                if n % 2 == 1 or hf == 0:
                     side.append((item, "q", stage[hf], None))
             else:
                 dst = wT["w0", n][:].rearrange("p (c t r) -> p c t r", c=4, t=4)
@@ -232,8 +232,13 @@ def tile_attention_pa_t_kernel(tc, x, W1, W2, W0, out):
                 codes[n] = (xc, xs)
             elif kind == "w2":
                 nc.vector.quantize_mx(out=wc["w2", n][:].bitcast(FP8X4), scales=ws["w2", n][:], in_=a[:])
+            elif n // 2 == 1:
+                nc.vector.quantize_mx(out=wc["w1", 1][:].bitcast(FP8X4), scales=ws["w1", 1][:], in_=a[:])
             else:
-                nc.vector.quantize_mx(out=wc["w1", n // 2][:].bitcast(FP8X4), scales=ws["w1", n // 2][:], in_=a[:])
+                for g in range(2):
+                    lo = g * BANK + (n % 2) * 2 * P
+                    nc.vector.quantize_mx(out=wc["w1", 0][:, lo : lo + 2 * P].bitcast(FP8X4), scales=ws["w1", 0][:, lo : lo + 2 * P],
+                                          in_=a[:, 4 * lo : 4 * lo + 8 * P])
 
         def flush(item):
             while [s for s in side if s[0] == item]:
@@ -287,7 +292,10 @@ def tile_attention_pa_t_kernel(tc, x, W1, W2, W0, out):
                 owed.append((hf, z, state["units"]))
 
         def quantise_pooled(g):
-            nc.scalar.copy(out=pg[g][:].rearrange("p (b t) -> p b t", t=4), in_=accT[g][:].rearrange("p (t b) -> p b t", t=4))
+            dst = pg[g][:].rearrange("p (b t) -> p b t", t=4)
+            src = accT[g][:].rearrange("p (t b) -> p b t", t=4)
+            nc.scalar.copy(out=dst[:, 0:64, :], in_=src[:, 0:64, :])
+            nc.vector.tensor_copy(out=dst[:, 64:P, :], in_=src[:, 64:P, :])
             nc.vector.quantize_mx(out=pc[:, g * P : (g + 1) * P].bitcast(FP8X4), scales=pscale[:, g * P : (g + 1) * P], in_=pg[g][:])
 
         pooled = []

@@ -67,6 +67,11 @@ def tile_attention_pa_t_kernel(tc, x, W1, W2, W0, out):
             for i in range(N_WARM):
                 nc.tensor.matmul(out=wbank[:], lhsT=zeros[:, 0:P], rhs=zeros[:], start=True, stop=True)
 
+        def keep_warm(n):
+            kb = ps.tile([P, BANK], F32, name="bank", tag="bank")
+            for i in range(n):
+                nc.tensor.matmul(out=kb[:], lhsT=zeros[:, 0:P], rhs=zeros[:], start=True, stop=True)
+
         x0n = const.tile([P, F], BF16, name="x0n")
         x0T = const.tile([P, F], BF16, name="x0T")
         wc = {}
@@ -194,6 +199,10 @@ def tile_attention_pa_t_kernel(tc, x, W1, W2, W0, out):
                 order = (0, BANK, 2 * BANK, 3 * BANK)
             for o in order:
                 banks.append(transposes(words[:, o : o + BANK]))
+                if item == ("w1", 0) and o % (2 * BANK) == BANK:
+                    keep_warm(1)
+            if item == ("w1", 1):
+                keep_warm(2)
             if LONG_RUNS:
                 pe_sums()
             if kind == "x" or kind == "w2":

@@ -9,6 +9,7 @@ U32 = mybir.dt.uint32
 U8 = mybir.dt.uint8
 FP8X4 = mybir.dt.float8_e4m3fn_x4
 ADD = mybir.AluOpType.add
+AX = mybir.AxisListType.X
 TANH = mybir.ActivationFunctionType.Tanh
 
 P = 128
@@ -21,13 +22,14 @@ TABLE = ("dggg....", "gggg....", "gvgpgvgp", "gvgpgvgp", "gvgpgvgp", "gvgpgvgp",
 FIRST1 = "dvgpgvgp"
 PAT_LONG = "ssss"
 PAT_SHORT = "svsv"
-ZB = 12
+ZB = 8
+GZ = 4
 Q_AT = 3
 Q_MOD = 4
 HF_MAJOR = 0
 G_W = 512
 EXTRA_AT = (4,)
-PLAN_Q = (6, 7)
+PLAN_Q = 6
 HALVES_FROM = 5
 RUN_AT = (4,)
 LAST_RUNS = (4,)
@@ -37,6 +39,8 @@ V_LAG = 6
 P_LAG = 2
 G_LAG = 5
 N_WARM = 6
+R_W = 128
+R_TURN = 1
 LAST_RUN_AT = 5
 NBANK = 7
 
@@ -51,6 +55,9 @@ def tile_attention_pa_t_kernel(tc, x, W1, W2, W0, out):
         stg = ctx.enter_context(tc.tile_pool(name="stg", bufs=2))
         xcp = ctx.enter_context(tc.tile_pool(name="xcp", bufs=4))
         zp = ctx.enter_context(tc.tile_pool(name="zp", bufs=ZB))
+        qp = ctx.enter_context(tc.tile_pool(name="qp", bufs=3))
+        gzp = ctx.enter_context(tc.tile_pool(name="gzp", bufs=GZ))
+        rp = ctx.enter_context(tc.tile_pool(name="rp", bufs=2))
         ps = ctx.enter_context(tc.psum_pool(name="ps", bufs=NBANK))
         atp = ctx.enter_context(tc.psum_pool(name="atp", bufs=1))
 
@@ -89,7 +96,7 @@ def tile_attention_pa_t_kernel(tc, x, W1, W2, W0, out):
         acc = {}
         for e in ("g", "v"):
             for hf in range(2):
-                acc[e, hf] = const.tile([P, BANK], F32, name="acc%s%d" % (e, hf))
+                acc[e, hf] = const.tile([P, (2 if e == "g" else 1) * BANK], F32, name="acc%s%d" % (e, hf))
         pg = [const.tile([P, BANK], BF16, name="pg%d" % g, align_bytes=256) for g in range(2)]
         pc = const.tile([P, 2 * P], U32, name="pc", align_bytes=256)
         pscale = const.tile([P, 2 * P], U8, name="pscale", align_bytes=256)
@@ -163,7 +170,8 @@ def tile_attention_pa_t_kernel(tc, x, W1, W2, W0, out):
             for key in sorted(last_seq):
                 if room > 0 and last_seq[key] <= state["units"] - (G_LAG if key[0] == "g" else V_LAG + P_LAG):
                     last_seq.pop(key)
-                    pe_sum(key[1], acc[key])
+                    for j in range(2 if key[0] == "g" else 1):
+                        pe_sum(key[1], acc[key][:, j * BANK : (j + 1) * BANK])
                     room -= 1
 
         def quant_view(t):
@@ -267,7 +275,24 @@ def tile_attention_pa_t_kernel(tc, x, W1, W2, W0, out):
                                  start=(k == 0), stop=(k == 7))
             return bank
 
-        def unit(n, hf):
+        def place(hf, c):
+            if c == "g":
+                if hf not in gpair or gpair[hf][1] == 2:
+                    gpair[hf] = [acc["g", hf] if hf not in gpair else gzp.tile([P, 2 * BANK], F32, name="z2", tag="z2"), 0]
+                q2, j = gpair[hf]
+                gpair[hf][1] += 1
+                return q2[:, j * BANK : (j + 1) * BANK]
+            if c != "r":
+                z = zp.tile([P, BANK], F32, name="z", tag="z")
+                return z[:]
+            if hf not in quad or quad[hf][1] == 4:
+                q4 = qp.tile([P, 4 * BANK], F32, name="z4", tag="z4")
+                quad[hf] = [q4, 0]
+            q4, j = quad[hf]
+            quad[hf][1] += 1
+            return q4[:, j * BANK : (j + 1) * BANK]
+
+        def unit(n, hf, c):
             xc, xs = codes[n // 4]
             bank = ps.tile([P, BANK], F32, name="bank", tag="bank")
             for g in range(2):
@@ -275,23 +300,45 @@ def tile_attention_pa_t_kernel(tc, x, W1, W2, W0, out):
                 nc.tensor.matmul_mx(out=bank[:], lhsT=xc[:, lo : lo + P].bitcast(FP8X4), lhsT_scale=xs[:, lo : lo + P],
                                     rhs=wc["w1", hf][:, g * BANK : (g + 1) * BANK].bitcast(FP8X4),
                                     rhs_scale=ws["w1", hf][:, g * BANK : (g + 1) * BANK], start=(g == 0), stop=(g == 1))
-            z = zp.tile([P, BANK], F32, name="z", tag="z")
-            nc.vector.tensor_tensor(out=z[:], in0=bank[:], in1=prod["w1", hf][:], op=ADD)
+            z = place(hf, c)
+            nc.vector.tensor_tensor(out=z, in0=bank[:], in1=prod["w1", hf][:], op=ADD)
             return z
 
         vlate = []
+        quad = {}
+        gpair = {}
         started = []
 
         def late_add():
-            hf, z, seq = vlate.pop(0)
-            nc.vector.tensor_tensor(out=acc["v", hf][:], in0=acc["v", hf][:], in1=z[:], op=ADD)
+            what = vlate.pop(0)
+            if len(what) == 3:
+                hf, z, seq = what
+                nc.vector.tensor_tensor(out=acc["v", hf][:], in0=acc["v", hf][:], in1=z, op=ADD)
+            else:
+                hf, q4, seq, part, lo = what
+                nc.vector.tensor_reduce(out=part[:, lo : lo + R_W], in_=q4[:].rearrange("p (j h) -> p h j", j=4)[:, lo : lo + R_W, :], op=ADD, axis=AX)
+                if lo + R_W == BANK:
+                    owed.append((hf, part[:], state["units"]))
 
         def finish(c, hf, z):
+            if c == "r":
+                nc.scalar.activation(out=z, in_=z, func=TANH)
+                if quad[hf][1] == 4:
+                    part = rp.tile([P, BANK], F32, name="part", tag="part")
+                    for lo in range(0, BANK, R_W):
+                        vlate.append((hf, quad[hf][0], state["units"], part, lo))
+                return
+            if c == "g":
+                nc.scalar.activation(out=z, in_=z, func=TANH)
+                if gpair[hf][1] == 2 and gpair[hf][0] is not acc["g", hf]:
+                    q2 = gpair[hf][0]
+                    nc.gpsimd.tensor_tensor(out=acc["g", hf][:], in0=acc["g", hf][:], in1=q2[:], op=ADD)
+                return
             if c in "gv" and (c, hf) not in started:
                 started.append((c, hf))
-                nc.scalar.activation(out=acc[c, hf][:], in_=z[:], func=TANH)
+                nc.scalar.activation(out=acc[c, hf][:], in_=z, func=TANH)
                 return
-            nc.scalar.activation(out=z[:], in_=z[:], func=TANH)
+            nc.scalar.activation(out=z, in_=z, func=TANH)
             if c == "g":
                 for o in range(0, BANK, G_W):
                     nc.gpsimd.tensor_tensor(out=acc["g", hf][:, o : o + G_W], in0=acc["g", hf][:, o : o + G_W], in1=z[:, o : o + G_W], op=ADD)
@@ -327,8 +374,7 @@ def tile_attention_pa_t_kernel(tc, x, W1, W2, W0, out):
                                     start=first, stop=last)
 
         arrivals = [("w1", 0), ("w1", 1), ("x", 0), ("x", 1), ("w1", 2), ("w1", 3)] + [("x", n) for n in range(2, NQ)]
-        extras = [("p", 0), ("p", 1)]
-        plan = [(PLAN_Q[i], extras[i]) for i in range(2)]
+        plan = [(PLAN_Q, ("p", 0))]
         loads = arrivals[0:7] + [("w0", 0), ("x", 3), ("x", 4), ("w0", 1), ("x", 5), ("w2", 0), ("x", 6), ("x", 7), ("w2", 1), ("x", 8)]
         live = {"x": 0, "w": 0}
 
@@ -359,13 +405,19 @@ def tile_attention_pa_t_kernel(tc, x, W1, W2, W0, out):
             elif HF_MAJOR == 2 and len(units) == 8 and item[0] == "x":
                 units = [u for u in units if u[1] == 1] + [u for u in units if u[1] == 0]
             events.append(units)
+        n_r = {0: 0, 1: 0}
         for units in events:
             for n, hf, c in units:
                 if c == "p":
                     left[hf] += 1
+                elif c == "r":
+                    n_r[hf] += 1
+        for hf in range(2):
+            assert n_r[hf] % 4 == 0
+            left[hf] += n_r[hf] // 4
         used = sorted(set([(c if c != "d" else "g", hf) for units in events for n, hf, c in units if c in "dgv"]))
         for c, hf in used:
-            left[hf] += 1
+            left[hf] += 2 if c == "g" else 1
         seq = 0
         for units in events:
             for n, hf, c in units:
@@ -419,10 +471,11 @@ def tile_attention_pa_t_kernel(tc, x, W1, W2, W0, out):
                     evacuate(PAT_LONG)
                     try_pool()
                 nn, hf, c = units[k]
-                z = unit(nn, hf)
+                z = unit(nn, hf, "g" if c == "d" else c)
                 state["units"] += 1
-                while vlate and vlate[0][2] <= state["units"] - V_LAG:
-                    late_add()
+                for turn in range(R_TURN):
+                    if vlate and vlate[0][2] <= state["units"] - V_LAG:
+                        late_add()
                 if side and k % Q_MOD == Q_AT:
                     urgent = [i for i in range(len(side)) if side[i][0][0] == "x"]
                     do_side(urgent[0] if urgent else 0)
@@ -437,6 +490,8 @@ def tile_attention_pa_t_kernel(tc, x, W1, W2, W0, out):
         pe_sums()
         n_before = len(pooled)
         try_pool()
+        wb = anchors("w0", 1)
+        nc.scalar.copy(out=prod["w0", 1][:], in_=wb[:])
         assert len(pooled) == 2
         for g in pooled[n_before:]:
             second(g, g == pooled[0], g == pooled[1])

@@ -52,7 +52,7 @@ def tile_attention_pa_t_kernel(tc, x, W1, W2, W0, out):
         const = ctx.enter_context(tc.tile_pool(name="const", bufs=1))
         xin = ctx.enter_context(tc.tile_pool(name="xin", bufs=3))
         win = ctx.enter_context(tc.tile_pool(name="win", bufs=2))
-        stg = ctx.enter_context(tc.tile_pool(name="stg", bufs=2))
+        stg = ctx.enter_context(tc.tile_pool(name="stg", bufs=4))
         xcp = ctx.enter_context(tc.tile_pool(name="xcp", bufs=4))
         zp = ctx.enter_context(tc.tile_pool(name="zp", bufs=ZB))
         qp = ctx.enter_context(tc.tile_pool(name="qp", bufs=3))
@@ -142,6 +142,7 @@ def tile_attention_pa_t_kernel(tc, x, W1, W2, W0, out):
                 nc.tensor.transpose(bank[:, c * P : (c + 1) * P], words[:, c * P : (c + 1) * P], ident[:])
             return bank
 
+        w2_last = []
         side = []
         codes = {}
         stage = {}
@@ -190,7 +191,7 @@ def tile_attention_pa_t_kernel(tc, x, W1, W2, W0, out):
                     dst = wT["w0", n][:].rearrange("p (c t r) -> p c t r", c=4, t=4)
                     side.append((item, "e", dst[:, :, i], bank[:].rearrange("p (c r) -> p c r", c=4)))
             if kind == "w2" and part == 1:
-                side.append((item, "q", stage[item], None))
+                w2_last.append((item, "q", stage[item], None))
             if part == 1:
                 live["w"] -= 1
                 pump()
@@ -480,20 +481,20 @@ def tile_attention_pa_t_kernel(tc, x, W1, W2, W0, out):
                     urgent = [i for i in range(len(side)) if side[i][0][0] == "x"]
                     do_side(urgent[0] if urgent else 0)
                 finish("g" if c == "d" else c, hf, z)
-        if pooled:
-            second(pooled[0], True, False)
         while vlate:
             late_add()
+        side.extend(w2_last)
+        while side:
+            do_side()
         state["units"] += P_LAG
         pe_sums()
         state["units"] += 100
         pe_sums()
-        n_before = len(pooled)
         try_pool()
         wb = anchors("w0", 1)
         nc.scalar.copy(out=prod["w0", 1][:], in_=wb[:])
         assert len(pooled) == 2
-        for g in pooled[n_before:]:
+        for g in pooled:
             second(g, g == pooled[0], g == pooled[1])
         for o in range(2):
             s = slice(o * BANK, (o + 1) * BANK)

@@ -18,9 +18,9 @@ BANK = 512
 NQ = 9
 FLOPS = 2 * 128 * 36 * 1024 * 1024 + 3 * 2 * 128 * 1024 * 1024
 
-TABLE = ("dggg....", "gggg....", "gvgpgvgp", "gvgpgvgp", "gvgpgvgp", "gvgpgvgp", "gvgpgvgp", "gvgpgvgp", "pppppppp")
-FIRST1 = "dvgpgvgp"
-PAT_LONG = "ssss"
+TABLE = ("dggg....", "gggg....", "gvgpgvgp", "gvgpgvgp", "gvgpgvgp", "gvgpgvgp", "gvgpgvgp", "gvgpgvgp", "pvpvpppp")
+FIRST1 = "dgggggvp"
+PAT_LONG = "sssv"
 PAT_SHORT = "svsv"
 ZB = 8
 GZ = 4
@@ -28,7 +28,7 @@ Q_AT = 3
 Q_MOD = 4
 HF_MAJOR = 0
 G_W = 512
-EXTRA_AT = (4,)
+EXTRA_AT = (0,)
 PLAN_Q = 6
 HALVES_FROM = 5
 RUN_AT = (4,)

@@ -20,7 +20,7 @@ FLOPS = 2 * 128 * 36 * 1024 * 1024 + 3 * 2 * 128 * 1024 * 1024
 
 TABLE = ("dggg....", "gggg....", "gvgpgvgp", "gvgpgvgp", "gvgpgvgp", "gvgpgvgp", "gvgpgvgp", "gvgpgvgp", "pvpvpppp")
 FIRST1 = "dgggggvp"
-PAT_LONG = "sssv"
+PAT_LONG = "ssss"
 PAT_SHORT = "svsv"
 ZB = 8
 GZ = 4
@@ -31,6 +31,7 @@ G_W = 512
 EXTRA_AT = (0,)
 PLAN_Q = 6
 HALVES_FROM = 5
+OUT_SPLIT = (1, 2)
 RUN_AT = (4,)
 LAST_RUNS = (4,)
 LAST_ROOM = 8
@@ -351,8 +352,7 @@ def tile_attention_pa_t_kernel(tc, x, W1, W2, W0, out):
         def quantise_pooled(g):
             dst = pg[g][:].rearrange("p (b t) -> p b t", t=4)
             src = accT[g][:].rearrange("p (t b) -> p b t", t=4)
-            nc.scalar.copy(out=dst[:, 0:64, :], in_=src[:, 0:64, :])
-            nc.vector.tensor_copy(out=dst[:, 64:P, :], in_=src[:, 64:P, :])
+            nc.scalar.copy(out=dst, in_=src)
             nc.vector.quantize_mx(out=pc[:, g * P : (g + 1) * P].bitcast(FP8X4), scales=pscale[:, g * P : (g + 1) * P], in_=pg[g][:])
 
         pooled = []
@@ -362,17 +362,6 @@ def tile_attention_pa_t_kernel(tc, x, W1, W2, W0, out):
                 if left[g] == 0 and g not in pooled:
                     pooled.append(g)
                     quantise_pooled(g)
-
-        obs = []
-
-        def second(g, first, last):
-            for o in range(2):
-                if first:
-                    ob = ps.tile([P, BANK], F32, name="bank", tag="bank")
-                    obs.append(ob)
-                nc.tensor.matmul_mx(out=obs[o][:], lhsT=pc[:, g * P : (g + 1) * P].bitcast(FP8X4), lhsT_scale=pscale[:, g * P : (g + 1) * P],
-                                    rhs=wc["w2", o][:, g * BANK : (g + 1) * BANK].bitcast(FP8X4), rhs_scale=ws["w2", o][:, g * BANK : (g + 1) * BANK],
-                                    start=first, stop=last)
 
         arrivals = [("w1", 0), ("w1", 1), ("x", 0), ("x", 1), ("w1", 2), ("w1", 3)] + [("x", n) for n in range(2, NQ)]
         plan = [(PLAN_Q, ("p", 0))]
@@ -494,12 +483,17 @@ def tile_attention_pa_t_kernel(tc, x, W1, W2, W0, out):
         wb = anchors("w0", 1)
         nc.scalar.copy(out=prod["w0", 1][:], in_=wb[:])
         assert len(pooled) == 2
-        for g in pooled:
-            second(g, g == pooled[0], g == pooled[1])
         for o in range(2):
-            s = slice(o * BANK, (o + 1) * BANK)
-            nc.vector.tensor_tensor(out=res[:, s], in0=obs[o][:], in1=prod["w0", o][:], op=ADD)
-            if o == 0:
-                nc.sync.dma_start(out=out[:, s], in_=res[:, s])
-            else:
-                nc.scalar.dma_start(out=out[:, s], in_=res[:, s])
+            ob = ps.tile([P, BANK], F32, name="bank", tag="bank")
+            for g in pooled:
+                nc.tensor.matmul_mx(out=ob[:], lhsT=pc[:, g * P : (g + 1) * P].bitcast(FP8X4), lhsT_scale=pscale[:, g * P : (g + 1) * P],
+                                    rhs=wc["w2", o][:, g * BANK : (g + 1) * BANK].bitcast(FP8X4), rhs_scale=ws["w2", o][:, g * BANK : (g + 1) * BANK],
+                                    start=(g == pooled[0]), stop=(g == pooled[1]))
+            width = BANK // OUT_SPLIT[o]
+            for c in range(OUT_SPLIT[o]):
+                s = slice(o * BANK + c * width, o * BANK + (c + 1) * width)
+                nc.vector.tensor_tensor(out=res[:, s], in0=ob[:, c * width : (c + 1) * width], in1=prod["w0", o][:, c * width : (c + 1) * width], op=ADD)
+                if (o + c) % 2 == 0:
+                    nc.sync.dma_start(out=out[:, s], in_=res[:, s])
+                else:
+                    nc.scalar.dma_start(out=out[:, s], in_=res[:, s])

@@ -31,6 +31,8 @@ G_W = 512
 EXTRA_AT = (0,)
 PLAN_Q = 6
 HALVES_FROM = 5
+MIX_W1 = 8
+TAIL_MIX = 4
 OUT_SPLIT = (1, 2)
 RUN_AT = (4,)
 LAST_RUNS = (4,)
@@ -137,10 +139,17 @@ def tile_attention_pa_t_kernel(tc, x, W1, W2, W0, out):
                                   in_=W.rearrange("(t p) c -> p t c", p=P)[:, 4 * n : 4 * n + 4, :])
             nat[item] = t
 
+        mix = []
+
         def transposes(words):
             bank = ps.tile([P, BANK], F32, name="bank", tag="bank")
             for c in range(4):
                 nc.tensor.transpose(bank[:, c * P : (c + 1) * P], words[:, c * P : (c + 1) * P], ident[:])
+                if mix:
+                    if mix[0] > 0:
+                        mix[0] -= 1
+                    elif len(mix) > 1:
+                        mix.pop(1)()
             return bank
 
         w2_last = []
@@ -163,6 +172,8 @@ def tile_attention_pa_t_kernel(tc, x, W1, W2, W0, out):
             for t in range(4):
                 nc.tensor.matmul(out=accT[hf][:, t * P : (t + 1) * P], lhsT=src[:, t * P : (t + 1) * P], rhs=ident[:],
                                  is_transpose=True, start=(first and t == 0), stop=(left[hf] == 0 and t == 3))
+                if len(mix) > 1:
+                    mix.pop(1)()
 
         def pe_sums(room=100):
             while room > 0 and owed and owed[0][2] <= state["units"] - P_LAG:
@@ -269,13 +280,28 @@ def tile_attention_pa_t_kernel(tc, x, W1, W2, W0, out):
                 state["on_v"] = pattern[i % len(pattern)] == "v"
                 do_side([s[1] for s in side].index("e"))
 
-        def anchors(nm, hf, lo=0, width=BANK):
-            bank = ps.tile([P, BANK], F32, name="bank", tag="bank")
+        def anchors(nm, hf, lo=0, width=BANK, wait=None):
             v = wT[nm, hf][:].bitcast(BF16).rearrange("p (c r s) -> p c r s", c=4, s=2)
-            for k in range(8):
-                nc.tensor.matmul(out=bank[:, 0:width], lhsT=x0T[:, k * P : (k + 1) * P], rhs=v[:, k // 2, lo : lo + width, k % 2],
+            hold = []
+
+            def step(k):
+                if k == 0:
+                    hold.append(ps.tile([P, BANK], F32, name="bank", tag="bank"))
+                nc.tensor.matmul(out=hold[0][:, 0:width], lhsT=x0T[:, k * P : (k + 1) * P], rhs=v[:, k // 2, lo : lo + width, k % 2],
                                  start=(k == 0), stop=(k == 7))
-            return bank
+
+            steps = [lambda k=k: step(k) for k in range(8)]
+            if wait is None:
+                for s in steps:
+                    s()
+            else:
+                mix.extend([wait] + steps)
+            return hold
+
+        def mixed():
+            while len(mix) > 1:
+                mix.pop(1)()
+            mix.clear()
 
         def place(hf, c):
             if c == "g":
@@ -431,26 +457,25 @@ def tile_attention_pa_t_kernel(tc, x, W1, W2, W0, out):
             hb = None
             if n == 0:
                 hb = anchors("w1", 0, 0, 2 * P)
+            wb = None
+            if item[0] == "w1" and n > 0:
+                hb = anchors("w1", item[1] // 2, (item[1] % 2) * 2 * P, 2 * P, wait=MIX_W1)
+            elif long_event and plan and item[0] == "x" and plan[0][0] <= item[1]:
+                plan.pop(0)
+                wb = anchors("w0", 0, wait=0)
             if n + 1 < len(arrivals):
                 prep_and_pump(arrivals[n + 1])
-            if item[0] == "w1" and n > 0:
-                hb = anchors("w1", item[1] // 2, (item[1] % 2) * 2 * P, 2 * P)
+            mixed()
             evacuate(PAT_LONG if long_event else PAT_SHORT)
+            if wb is not None:
+                nc.scalar.copy(out=prod["w0", 0][:], in_=wb[0][:])
             if not long_event:
                 while side and side[0][1] == "q":
                     do_side()
             if hb is not None:
                 lo = (item[1] % 2) * 2 * P
-                nc.scalar.copy(out=prod["w1", item[1] // 2][:, lo : lo + 2 * P], in_=hb[:, 0 : 2 * P])
+                nc.scalar.copy(out=prod["w1", item[1] // 2][:, lo : lo + 2 * P], in_=hb[0][:, 0 : 2 * P])
             for k in range(len(units)):
-                if long_event and k in EXTRA_AT and plan and item[0] == "x" and plan[0][0] <= item[1]:
-                    what = plan.pop(0)[1]
-                    if what[0] == "p":
-                        wb = anchors("w0", what[1])
-                        nc.scalar.copy(out=prod["w0", what[1]][:], in_=wb[:])
-                    else:
-                        prep_and_pump(what)
-                        evacuate(PAT_LONG)
                 if k in (LAST_RUNS if n == len(arrivals) - 1 else RUN_AT) and len(units) == 8:
                     room = 4 if n < len(arrivals) - 1 else LAST_ROOM
                     if halves and n >= HALVES_FROM and k == RUN_AT[0]:
@@ -475,13 +500,20 @@ def tile_attention_pa_t_kernel(tc, x, W1, W2, W0, out):
         side.extend(w2_last)
         while side:
             do_side()
+        wb = anchors("w0", 1, wait=0)
+        rest = mix[1 + TAIL_MIX :]
+        del_from = mix[0 : 1 + TAIL_MIX]
+        mix.clear()
+        mix.extend(del_from)
         state["units"] += P_LAG
         pe_sums()
         state["units"] += 100
         pe_sums()
+        mixed()
         try_pool()
-        wb = anchors("w0", 1)
-        nc.scalar.copy(out=prod["w0", 1][:], in_=wb[:])
+        for s in rest:
+            s()
+        nc.scalar.copy(out=prod["w0", 1][:], in_=wb[0][:])
         assert len(pooled) == 2
         for o in range(2):
             ob = ps.tile([P, BANK], F32, name="bank", tag="bank")

@@ -29,9 +29,10 @@ Q_MOD = 4
 HF_MAJOR = 0
 G_W = 512
 EXTRA_AT = (0,)
-PLAN_Q = 6
+PLAN_Q = (4, 5, 6)
+MIX_W0 = 8
 HALVES_FROM = 5
-MIX_W1 = 8
+MIX_W1 = 100
 TAIL_MIX = 4
 OUT_SPLIT = (1, 2)
 RUN_AT = (4,)
@@ -390,7 +391,7 @@ def tile_attention_pa_t_kernel(tc, x, W1, W2, W0, out):
                     quantise_pooled(g)
 
         arrivals = [("w1", 0), ("w1", 1), ("x", 0), ("x", 1), ("w1", 2), ("w1", 3)] + [("x", n) for n in range(2, NQ)]
-        plan = [(PLAN_Q, ("p", 0))]
+        plan = [(PLAN_Q[i], i) for i in range(len(PLAN_Q))]
         loads = arrivals[0:7] + [("w0", 0), ("x", 3), ("x", 4), ("w0", 1), ("x", 5), ("w2", 0), ("x", 6), ("x", 7), ("w2", 1), ("x", 8)]
         live = {"x": 0, "w": 0}
 
@@ -461,14 +462,15 @@ def tile_attention_pa_t_kernel(tc, x, W1, W2, W0, out):
             if item[0] == "w1" and n > 0:
                 hb = anchors("w1", item[1] // 2, (item[1] % 2) * 2 * P, 2 * P, wait=MIX_W1)
             elif long_event and plan and item[0] == "x" and plan[0][0] <= item[1]:
-                plan.pop(0)
-                wb = anchors("w0", 0, wait=0)
+                quarter = plan.pop(0)[1]
+                wb = anchors("w0", quarter // 2, (quarter % 2) * 2 * P, 2 * P, wait=MIX_W0)
             if n + 1 < len(arrivals):
                 prep_and_pump(arrivals[n + 1])
             mixed()
             evacuate(PAT_LONG if long_event else PAT_SHORT)
             if wb is not None:
-                nc.scalar.copy(out=prod["w0", 0][:], in_=wb[0][:])
+                lo = (quarter % 2) * 2 * P
+                nc.scalar.copy(out=prod["w0", quarter // 2][:, lo : lo + 2 * P], in_=wb[0][:, 0 : 2 * P])
             if not long_event:
                 while side and side[0][1] == "q":
                     do_side()
@@ -500,7 +502,7 @@ def tile_attention_pa_t_kernel(tc, x, W1, W2, W0, out):
         side.extend(w2_last)
         while side:
             do_side()
-        wb = anchors("w0", 1, wait=0)
+        wb = anchors("w0", 1, 2 * P, 2 * P, wait=0)
         rest = mix[1 + TAIL_MIX :]
         del_from = mix[0 : 1 + TAIL_MIX]
         mix.clear()
@@ -513,7 +515,7 @@ def tile_attention_pa_t_kernel(tc, x, W1, W2, W0, out):
         try_pool()
         for s in rest:
             s()
-        nc.scalar.copy(out=prod["w0", 1][:], in_=wb[0][:])
+        nc.scalar.copy(out=prod["w0", 1][:, 2 * P : BANK], in_=wb[0][:, 0 : 2 * P])
         assert len(pooled) == 2
         for o in range(2):
             ob = ps.tile([P, BANK], F32, name="bank", tag="bank")

@@ -18,9 +18,9 @@ BANK = 512
 NQ = 9
 FLOPS = 2 * 128 * 36 * 1024 * 1024 + 3 * 2 * 128 * 1024 * 1024
 
-TABLE = ("dggg....", "gggg....", "gvgpgvgp", "gvgpgvgp", "gvgpgvgp", "gvgpgvgp", "gvgpgvgp", "gvgpgvgp", "pvpvpppp")
+TABLE = ("dggg....", "gggg....", "gvgpgvgp", "gvgpgvgp", "gvgpgvgp", "gvgpgvgp", "gvgpgvgp", "gpgggpgg", "pvpvpppp")
 FIRST1 = "dgggggvp"
-PAT_LONG = "ssss"
+PAT_LONG = "sssv"
 PAT_SHORT = "svsv"
 ZB = 8
 GZ = 4
@@ -29,24 +29,20 @@ Q_MOD = 4
 HF_MAJOR = 0
 G_W = 512
 EXTRA_AT = (0,)
-PLAN_Q = (4, 5, 6)
-MIX_W0 = 8
 HALVES_FROM = 5
-MIX_W1 = 100
-TAIL_MIX = 4
-OUT_SPLIT = (1, 2)
 RUN_AT = (4,)
 LAST_RUNS = (4,)
 LAST_ROOM = 8
 LONG_RUNS = False
 V_LAG = 6
 P_LAG = 2
-G_LAG = 5
+G_LAG = 9
 N_WARM = 6
 R_W = 128
 R_TURN = 1
 LAST_RUN_AT = 5
-NBANK = 7
+NBANK = 6
+P_FROM = 6
 
 
 def tile_attention_pa_t_kernel(tc, x, W1, W2, W0, out):
@@ -63,6 +59,7 @@ def tile_attention_pa_t_kernel(tc, x, W1, W2, W0, out):
         gzp = ctx.enter_context(tc.tile_pool(name="gzp", bufs=GZ))
         rp = ctx.enter_context(tc.tile_pool(name="rp", bufs=2))
         ps = ctx.enter_context(tc.psum_pool(name="ps", bufs=NBANK))
+        pp = ctx.enter_context(tc.psum_pool(name="pp", bufs=1))
         atp = ctx.enter_context(tc.psum_pool(name="atp", bufs=1))
 
         ident = const.tile([P, P], F32, name="ident")
@@ -140,17 +137,10 @@ def tile_attention_pa_t_kernel(tc, x, W1, W2, W0, out):
                                   in_=W.rearrange("(t p) c -> p t c", p=P)[:, 4 * n : 4 * n + 4, :])
             nat[item] = t
 
-        mix = []
-
         def transposes(words):
             bank = ps.tile([P, BANK], F32, name="bank", tag="bank")
             for c in range(4):
                 nc.tensor.transpose(bank[:, c * P : (c + 1) * P], words[:, c * P : (c + 1) * P], ident[:])
-                if mix:
-                    if mix[0] > 0:
-                        mix[0] -= 1
-                    elif len(mix) > 1:
-                        mix.pop(1)()
             return bank
 
         w2_last = []
@@ -173,8 +163,6 @@ def tile_attention_pa_t_kernel(tc, x, W1, W2, W0, out):
             for t in range(4):
                 nc.tensor.matmul(out=accT[hf][:, t * P : (t + 1) * P], lhsT=src[:, t * P : (t + 1) * P], rhs=ident[:],
                                  is_transpose=True, start=(first and t == 0), stop=(left[hf] == 0 and t == 3))
-                if len(mix) > 1:
-                    mix.pop(1)()
 
         def pe_sums(room=100):
             while room > 0 and owed and owed[0][2] <= state["units"] - P_LAG:
@@ -281,28 +269,31 @@ def tile_attention_pa_t_kernel(tc, x, W1, W2, W0, out):
                 state["on_v"] = pattern[i % len(pattern)] == "v"
                 do_side([s[1] for s in side].index("e"))
 
-        def anchors(nm, hf, lo=0, width=BANK, wait=None):
+        def anchors(nm, hf, lo):
             v = wT[nm, hf][:].bitcast(BF16).rearrange("p (c r s) -> p c r s", c=4, s=2)
             hold = []
 
             def step(k):
                 if k == 0:
-                    hold.append(ps.tile([P, BANK], F32, name="bank", tag="bank"))
-                nc.tensor.matmul(out=hold[0][:, 0:width], lhsT=x0T[:, k * P : (k + 1) * P], rhs=v[:, k // 2, lo : lo + width, k % 2],
+                    hold.append(pp.tile([P, BANK], F32, name="pbank", tag="pbank"))
+                nc.tensor.matmul(out=hold[0][:, 0 : 2 * P], lhsT=x0T[:, k * P : (k + 1) * P], rhs=v[:, k // 2, lo : lo + 2 * P, k % 2],
                                  start=(k == 0), stop=(k == 7))
+                if k == 7:
+                    pcopy.append((prod[nm, hf][:, lo : lo + 2 * P], hold[0][:, 0 : 2 * P]))
 
-            steps = [lambda k=k: step(k) for k in range(8)]
-            if wait is None:
-                for s in steps:
-                    s()
-            else:
-                mix.extend([wait] + steps)
-            return hold
+            return [lambda k=k: step(k) for k in range(8)]
 
-        def mixed():
-            while len(mix) > 1:
-                mix.pop(1)()
-            mix.clear()
+        pcopy = []
+        plain = []
+
+        def bridge():
+            if plain and plain[0][0] <= ready[0]:
+                plain.pop(0)[1]()
+
+        def copy_products():
+            while pcopy:
+                dst, src = pcopy.pop(0)
+                nc.scalar.copy(out=dst, in_=src)
 
         def place(hf, c):
             if c == "g":
@@ -391,7 +382,9 @@ def tile_attention_pa_t_kernel(tc, x, W1, W2, W0, out):
                     quantise_pooled(g)
 
         arrivals = [("w1", 0), ("w1", 1), ("x", 0), ("x", 1), ("w1", 2), ("w1", 3)] + [("x", n) for n in range(2, NQ)]
-        plan = [(PLAN_Q[i], i) for i in range(len(PLAN_Q))]
+        ready = [0]
+        for quarter in range(4):
+            plain.extend([(quarter + 1, s) for s in anchors("w0", quarter // 2, (quarter % 2) * 2 * P)])
         loads = arrivals[0:7] + [("w0", 0), ("x", 3), ("x", 4), ("w0", 1), ("x", 5), ("w2", 0), ("x", 6), ("x", 7), ("w2", 1), ("x", 8)]
         live = {"x": 0, "w": 0}
 
@@ -455,37 +448,39 @@ def tile_attention_pa_t_kernel(tc, x, W1, W2, W0, out):
             units = events[n]
             flush(item)
             long_event = len(units) == 8
-            hb = None
+            long_run = long_event and n >= P_FROM and n + 1 < len(arrivals)
             if n == 0:
-                hb = anchors("w1", 0, 0, 2 * P)
-            wb = None
-            if item[0] == "w1" and n > 0:
-                hb = anchors("w1", item[1] // 2, (item[1] % 2) * 2 * P, 2 * P, wait=MIX_W1)
-            elif long_event and plan and item[0] == "x" and plan[0][0] <= item[1]:
-                quarter = plan.pop(0)[1]
-                wb = anchors("w0", quarter // 2, (quarter % 2) * 2 * P, 2 * P, wait=MIX_W0)
+                for s in anchors("w1", 0, 0):
+                    s()
+            if long_run:
+                bridge()
             if n + 1 < len(arrivals):
                 prep_and_pump(arrivals[n + 1])
-            mixed()
+            if long_run:
+                bridge()
+            if item[0] == "w1" and n > 0:
+                for s in anchors("w1", item[1] // 2, (item[1] % 2) * 2 * P):
+                    s()
             evacuate(PAT_LONG if long_event else PAT_SHORT)
-            if wb is not None:
-                lo = (quarter % 2) * 2 * P
-                nc.scalar.copy(out=prod["w0", quarter // 2][:, lo : lo + 2 * P], in_=wb[0][:, 0 : 2 * P])
             if not long_event:
                 while side and side[0][1] == "q":
                     do_side()
-            if hb is not None:
-                lo = (item[1] % 2) * 2 * P
-                nc.scalar.copy(out=prod["w1", item[1] // 2][:, lo : lo + 2 * P], in_=hb[0][:, 0 : 2 * P])
+            copy_products()
             for k in range(len(units)):
                 if k in (LAST_RUNS if n == len(arrivals) - 1 else RUN_AT) and len(units) == 8:
                     room = 4 if n < len(arrivals) - 1 else LAST_ROOM
+                    if n >= P_FROM:
+                        bridge()
                     if halves and n >= HALVES_FROM and k == RUN_AT[0]:
                         more = halves.pop(0)
                         prep_half(more[0], more[1])
                         room = 2
                     pe_sums(room)
+                    if n >= P_FROM:
+                        bridge()
                     evacuate(PAT_LONG)
+                    ready[0] = 8 - len(halves)
+                    copy_products()
                     try_pool()
                 nn, hf, c = units[k]
                 z = unit(nn, hf, "g" if c == "d" else c)
@@ -502,32 +497,26 @@ def tile_attention_pa_t_kernel(tc, x, W1, W2, W0, out):
         side.extend(w2_last)
         while side:
             do_side()
-        wb = anchors("w0", 1, 2 * P, 2 * P, wait=0)
-        rest = mix[1 + TAIL_MIX :]
-        del_from = mix[0 : 1 + TAIL_MIX]
-        mix.clear()
-        mix.extend(del_from)
+        bridge()
         state["units"] += P_LAG
         pe_sums()
         state["units"] += 100
         pe_sums()
-        mixed()
         try_pool()
-        for s in rest:
-            s()
-        nc.scalar.copy(out=prod["w0", 1][:, 2 * P : BANK], in_=wb[0][:, 0 : 2 * P])
+        while plain:
+            bridge()
+        copy_products()
         assert len(pooled) == 2
-        for o in range(2):
+        for o, lo, width in ((0, 0, BANK), (1, 0, 2 * P), (1, 2 * P, 2 * P)):
             ob = ps.tile([P, BANK], F32, name="bank", tag="bank")
             for g in pooled:
-                nc.tensor.matmul_mx(out=ob[:], lhsT=pc[:, g * P : (g + 1) * P].bitcast(FP8X4), lhsT_scale=pscale[:, g * P : (g + 1) * P],
-                                    rhs=wc["w2", o][:, g * BANK : (g + 1) * BANK].bitcast(FP8X4), rhs_scale=ws["w2", o][:, g * BANK : (g + 1) * BANK],
+                c = slice(g * BANK + lo, g * BANK + lo + width)
+                nc.tensor.matmul_mx(out=ob[:, 0:width], lhsT=pc[:, g * P : (g + 1) * P].bitcast(FP8X4), lhsT_scale=pscale[:, g * P : (g + 1) * P],
+                                    rhs=wc["w2", o][:, c].bitcast(FP8X4), rhs_scale=ws["w2", o][:, c],
                                     start=(g == pooled[0]), stop=(g == pooled[1]))
-            width = BANK // OUT_SPLIT[o]
-            for c in range(OUT_SPLIT[o]):
-                s = slice(o * BANK + c * width, o * BANK + (c + 1) * width)
-                nc.vector.tensor_tensor(out=res[:, s], in0=ob[:, c * width : (c + 1) * width], in1=prod["w0", o][:, c * width : (c + 1) * width], op=ADD)
-                if (o + c) % 2 == 0:
-                    nc.sync.dma_start(out=out[:, s], in_=res[:, s])
-                else:
-                    nc.scalar.dma_start(out=out[:, s], in_=res[:, s])
+            s = slice(o * BANK + lo, o * BANK + lo + width)
+            nc.vector.tensor_tensor(out=res[:, s], in0=ob[:, 0:width], in1=prod["w0", o][:, lo : lo + width], op=ADD)
+            if lo == 0:
+                nc.sync.dma_start(out=out[:, s], in_=res[:, s])
+            else:
+                nc.scalar.dma_start(out=out[:, s], in_=res[:, s])

from contextlib import ExitStack

import concourse.mybir as mybir
from concourse.masks import make_identity

F32 = mybir.dt.float32
BF16 = mybir.dt.bfloat16
U32 = mybir.dt.uint32
U8 = mybir.dt.uint8
FP8X4 = mybir.dt.float8_e4m3fn_x4
ADD = mybir.AluOpType.add
AX = mybir.AxisListType.X
TANH = mybir.ActivationFunctionType.Tanh

P = 128
F = 1024
BANK = 512
NQ = 9
FLOPS = 2 * 128 * 36 * 1024 * 1024 + 3 * 2 * 128 * 1024 * 1024

TABLE = ("dggg....", "gggg....", "gvgpgvgp", "gvgpgvgp", "gvgpgvgp", "gvgpgvgp", "gvgpgvgp", "gpgggpgg", "pvpvpppp")
FIRST1 = "dgggggvp"
PAT_LONG = "sssv"
PAT_SHORT = "svsv"
ZB = 8
GZ = 4
Q_AT = 3
Q_MOD = 4
HF_MAJOR = 0
G_W = 512
EXTRA_AT = (0,)
HALVES_FROM = 5
RUN_AT = (4,)
LAST_RUNS = (4,)
LAST_ROOM = 8
LONG_RUNS = False
V_LAG = 6
P_LAG = 2
G_LAG = 9
N_WARM = 6
R_W = 128
R_TURN = 1
LAST_RUN_AT = 5
NBANK = 6
P_FROM = 6


def tile_attention_pa_t_kernel(tc, x, W1, W2, W0, out):
    nc = tc.nc
    with ExitStack() as ctx:
        ctx.enter_context(tc.manual_schedule())
        const = ctx.enter_context(tc.tile_pool(name="const", bufs=1))
        xin = ctx.enter_context(tc.tile_pool(name="xin", bufs=3))
        win = ctx.enter_context(tc.tile_pool(name="win", bufs=2))
        stg = ctx.enter_context(tc.tile_pool(name="stg", bufs=4))
        xcp = ctx.enter_context(tc.tile_pool(name="xcp", bufs=4))
        zp = ctx.enter_context(tc.tile_pool(name="zp", bufs=ZB))
        qp = ctx.enter_context(tc.tile_pool(name="qp", bufs=3))
        gzp = ctx.enter_context(tc.tile_pool(name="gzp", bufs=GZ))
        rp = ctx.enter_context(tc.tile_pool(name="rp", bufs=2))
        ps = ctx.enter_context(tc.psum_pool(name="ps", bufs=NBANK))
        pp = ctx.enter_context(tc.psum_pool(name="pp", bufs=1))
        atp = ctx.enter_context(tc.psum_pool(name="atp", bufs=1))

        ident = const.tile([P, P], F32, name="ident")
        make_identity(nc, ident[:])
        warm = const.tile([P, 1], F32, name="warm")
        nc.vector.memset(warm[:], 0.0)
        nc.scalar.activation(out=warm[:], in_=warm[:], func=TANH)

        if N_WARM:
            zeros = const.tile([P, BANK], BF16, name="zeros")
            nc.vector.memset(zeros[:], 0.0)
            wbank = ps.tile([P, BANK], F32, name="bank", tag="bank")
            for i in range(N_WARM):
                nc.tensor.matmul(out=wbank[:], lhsT=zeros[:, 0:P], rhs=zeros[:], start=True, stop=True)

        def keep_warm(n):
            kb = ps.tile([P, BANK], F32, name="bank", tag="bank")
            for i in range(n):
                nc.tensor.matmul(out=kb[:], lhsT=zeros[:, 0:P], rhs=zeros[:], start=True, stop=True)

        x0n = const.tile([P, F], BF16, name="x0n")
        x0T = const.tile([P, F], BF16, name="x0T")
        wc = {}
        ws = {}
        for nm in ("w1", "w2"):
            for hf in range(2):
                wc[nm, hf] = const.tile([P, F], U32, name="c%s%d" % (nm, hf), align_bytes=256)
                ws[nm, hf] = const.tile([P, F], U8, name="s%s%d" % (nm, hf), align_bytes=256)
        wT = {}
        prod = {}
        for nm in ("w1", "w0"):
            for hf in range(2):
                wT[nm, hf] = const.tile([P, 4 * BANK], F32, name="t%s%d" % (nm, hf))
                prod[nm, hf] = const.tile([P, BANK], F32, name="b%s%d" % (nm, hf))
        acc = {}
        for e in ("g", "v"):
            for hf in range(2):
                acc[e, hf] = const.tile([P, (2 if e == "g" else 1) * BANK], F32, name="acc%s%d" % (e, hf))
        pg = [const.tile([P, BANK], BF16, name="pg%d" % g, align_bytes=256) for g in range(2)]
        pc = const.tile([P, 2 * P], U32, name="pc", align_bytes=256)
        pscale = const.tile([P, 2 * P], U8, name="pscale", align_bytes=256)
        res = const.tile([P, F], F32, name="res")

        nat = {}
        state = {"on_v": False, "units": 0}

        def copy(dst, src):
            if state["on_v"]:
                nc.vector.tensor_copy(out=dst, in_=src)
            else:
                nc.scalar.copy(out=dst, in_=src)

        def load(item):
            kind, n = item
            if kind == "x":
                t = xin.tile([P, 4 * F], BF16, name="xn", tag="xn")
                v = t[:].rearrange("p (i f) -> p i f", i=4)
                if n == 0:
                    nc.sync.dma_start(out=v[:, 0:2, :], in_=x[:, 1:3, :])
                    nc.sync.dma_start(out=v[:, 2:4, :], in_=x[:, 3:5, :])
                else:
                    nc.sync.dma_start(out=v, in_=x[:, 1 + 4 * n : 5 + 4 * n, :])
            elif kind == "w1":
                t = win.tile([P, 4 * F], BF16, name="wn", tag="wn")
                v = t[:].rearrange("p (e c) -> p e c", e=2)
                if n == 0:
                    for e in range(2):
                        nc.sync.dma_start(out=v[:, e, :], in_=W1.rearrange("(j p e) c -> j e p c", p=P, e=2)[n, e])
                else:
                    nc.sync.dma_start(out=v, in_=W1.rearrange("(j p e) c -> j p e c", p=P, e=2)[n])
            else:
                t = win.tile([P, 4 * F], BF16, name="wn", tag="wn")
                W = W0 if kind == "w0" else W2
                nc.sync.dma_start(out=t[:].rearrange("p (t c) -> p t c", t=4),
                                  in_=W.rearrange("(t p) c -> p t c", p=P)[:, 4 * n : 4 * n + 4, :])
            nat[item] = t

        def transposes(words):
            bank = ps.tile([P, BANK], F32, name="bank", tag="bank")
            for c in range(4):
                nc.tensor.transpose(bank[:, c * P : (c + 1) * P], words[:, c * P : (c + 1) * P], ident[:])
            return bank

        w2_last = []
        side = []
        codes = {}
        stage = {}
        last_seq = {}
        owed = []
        accT = {}
        left = {0: 0, 1: 0}

        def pe_sum(hf, src):
            first = hf not in accT
            if first:
                if hf == 1:
                    accT[hf] = atp.tile([P, BANK], F32, name="at1")
                else:
                    accT[hf] = ps.tile([P, BANK], F32, name="bank", tag="bank")
            left[hf] -= 1
            for t in range(4):
                nc.tensor.matmul(out=accT[hf][:, t * P : (t + 1) * P], lhsT=src[:, t * P : (t + 1) * P], rhs=ident[:],
                                 is_transpose=True, start=(first and t == 0), stop=(left[hf] == 0 and t == 3))

        def pe_sums(room=100):
            while room > 0 and owed and owed[0][2] <= state["units"] - P_LAG:
                hf, z, seq = owed.pop(0)
                pe_sum(hf, z)
                room -= 1
            for key in sorted(last_seq):
                if room > 0 and last_seq[key] <= state["units"] - (G_LAG if key[0] == "g" else V_LAG + P_LAG):
                    last_seq.pop(key)
                    for j in range(2 if key[0] == "g" else 1):
                        pe_sum(key[1], acc[key][:, j * BANK : (j + 1) * BANK])
                    room -= 1

        def quant_view(t):
            return t[:].bitcast(F32).rearrange("p (g i r u) -> p g i r u", g=2, i=4, u=2)

        def prep_half(item, part):
            kind, n = item
            words = nat[item][:].bitcast(F32)
            if kind == "w2" and part == 0:
                stage[item] = stg.tile([P, 4 * F], BF16, name="xg", tag="xg", align_bytes=256)
            for i in (2 * part, 2 * part + 1):
                bank = transposes(words[:, i * BANK : (i + 1) * BANK])
                if kind == "w2":
                    side.append((item, "e", quant_view(stage[item])[:, :, i], bank[:].rearrange("p (g u r) -> p g r u", g=2, u=2)))
                else:
                    dst = wT["w0", n][:].rearrange("p (c t r) -> p c t r", c=4, t=4)
                    side.append((item, "e", dst[:, :, i], bank[:].rearrange("p (c r) -> p c r", c=4)))
            if kind == "w2" and part == 1:
                w2_last.append((item, "q", stage[item], None))
            if part == 1:
                live["w"] -= 1
                pump()

        def prep(item, more=None):
            kind, n = item
            words = nat[item][:].bitcast(F32)
            banks = []
            if item == ("w1", 0):
                order = (0, BANK, 2 * BANK, 3 * BANK)
            elif kind == "w1":
                order = (BANK, 3 * BANK, 0, 2 * BANK)
            else:
                order = (0, BANK, 2 * BANK, 3 * BANK)
            for o in order:
                banks.append(transposes(words[:, o : o + BANK]))
                if item == ("w1", 0) and o % (2 * BANK) == BANK:
                    keep_warm(1)
            if item == ("w1", 1):
                keep_warm(2)
            if LONG_RUNS:
                pe_sums()
            if kind == "x" or kind == "w2":
                xg = stg.tile([P, 4 * F], BF16, name="xg", tag="xg", align_bytes=256)
                for i in range(4):
                    side.append((item, "e", quant_view(xg)[:, :, i], banks[i][:].rearrange("p (g u r) -> p g r u", g=2, u=2)))
                side.append((item, "q", xg, None))
            elif kind == "w1":
                hf = n // 2
                if n % 2 == 0:
                    stage[hf] = stg.tile([P, 4 * F], BF16, name="xg", tag="xg", align_bytes=256)
                dst = wT["w1", hf][:].rearrange("p (c t r) -> p c t r", c=4, t=4)
                for o in order:
                    e = o // (2 * BANK)
                    bank = banks[order.index(o)]
                    if o % (2 * BANK) == BANK:
                        side.append((item, "e", quant_view(stage[hf])[:, :, 2 * (n % 2) + e], bank[:].rearrange("p (g u r) -> p g r u", g=2, u=2)))
                    else:
                        side.append((item, "e", dst[:, :, 2 * (n % 2) + e], bank[:].rearrange("p (c r) -> p c r", c=4)))
                if n % 2 == 1 or hf == 0:
                    side.append((item, "q", stage[hf], None))
            else:
                dst = wT["w0", n][:].rearrange("p (c t r) -> p c t r", c=4, t=4)
                for i in range(4):
                    side.append((item, "e", dst[:, :, i], banks[i][:].rearrange("p (c r) -> p c r", c=4)))

        def do_side(at=0):
            item, what, a, b = side.pop(at)
            kind, n = item
            if what == "e":
                copy(a, b)
            elif kind == "x":
                xc = xcp.tile([P, F], U32, name="xc", tag="xc", align_bytes=256)
                xs = xcp.tile([P, F], U8, name="xs", tag="xs", align_bytes=256)
                nc.vector.quantize_mx(out=xc[:].bitcast(FP8X4), scales=xs[:], in_=a[:])
                codes[n] = (xc, xs)
            elif kind == "w2":
                nc.vector.quantize_mx(out=wc["w2", n][:].bitcast(FP8X4), scales=ws["w2", n][:], in_=a[:])
            elif n // 2 == 1:
                nc.vector.quantize_mx(out=wc["w1", 1][:].bitcast(FP8X4), scales=ws["w1", 1][:], in_=a[:])
            else:
                for g in range(2):
                    lo = g * BANK + (n % 2) * 2 * P
                    nc.vector.quantize_mx(out=wc["w1", 0][:, lo : lo + 2 * P].bitcast(FP8X4), scales=ws["w1", 0][:, lo : lo + 2 * P],
                                          in_=a[:, 4 * lo : 4 * lo + 8 * P])

        def flush(item):
            while [s for s in side if s[0] == item]:
                do_side()

        def evacuate(pattern):
            n_e = len([s for s in side if s[1] == "e"])
            for i in range(n_e):
                state["on_v"] = pattern[i % len(pattern)] == "v"
                do_side([s[1] for s in side].index("e"))

        def anchors(nm, hf, lo):
            v = wT[nm, hf][:].bitcast(BF16).rearrange("p (c r s) -> p c r s", c=4, s=2)
            hold = []

            def step(k):
                if k == 0:
                    hold.append(pp.tile([P, BANK], F32, name="pbank", tag="pbank"))
                nc.tensor.matmul(out=hold[0][:, 0 : 2 * P], lhsT=x0T[:, k * P : (k + 1) * P], rhs=v[:, k // 2, lo : lo + 2 * P, k % 2],
                                 start=(k == 0), stop=(k == 7))
                if k == 7:
                    pcopy.append((prod[nm, hf][:, lo : lo + 2 * P], hold[0][:, 0 : 2 * P]))

            return [lambda k=k: step(k) for k in range(8)]

        pcopy = []
        plain = []

        def bridge():
            if plain and plain[0][0] <= ready[0]:
                plain.pop(0)[1]()

        def copy_products():
            while pcopy:
                dst, src = pcopy.pop(0)
                nc.scalar.copy(out=dst, in_=src)

        def place(hf, c):
            if c == "g":
                if hf not in gpair or gpair[hf][1] == 2:
                    gpair[hf] = [acc["g", hf] if hf not in gpair else gzp.tile([P, 2 * BANK], F32, name="z2", tag="z2"), 0]
                q2, j = gpair[hf]
                gpair[hf][1] += 1
                return q2[:, j * BANK : (j + 1) * BANK]
            if c != "r":
                z = zp.tile([P, BANK], F32, name="z", tag="z")
                return z[:]
            if hf not in quad or quad[hf][1] == 4:
                q4 = qp.tile([P, 4 * BANK], F32, name="z4", tag="z4")
                quad[hf] = [q4, 0]
            q4, j = quad[hf]
            quad[hf][1] += 1
            return q4[:, j * BANK : (j + 1) * BANK]

        def unit(n, hf, c):
            xc, xs = codes[n // 4]
            bank = ps.tile([P, BANK], F32, name="bank", tag="bank")
            for g in range(2):
                lo = g * BANK + (n % 4) * P
                nc.tensor.matmul_mx(out=bank[:], lhsT=xc[:, lo : lo + P].bitcast(FP8X4), lhsT_scale=xs[:, lo : lo + P],
                                    rhs=wc["w1", hf][:, g * BANK : (g + 1) * BANK].bitcast(FP8X4),
                                    rhs_scale=ws["w1", hf][:, g * BANK : (g + 1) * BANK], start=(g == 0), stop=(g == 1))
            z = place(hf, c)
            nc.vector.tensor_tensor(out=z, in0=bank[:], in1=prod["w1", hf][:], op=ADD)
            return z

        vlate = []
        quad = {}
        gpair = {}
        started = []

        def late_add():
            what = vlate.pop(0)
            if len(what) == 3:
                hf, z, seq = what
                nc.vector.tensor_tensor(out=acc["v", hf][:], in0=acc["v", hf][:], in1=z, op=ADD)
            else:
                hf, q4, seq, part, lo = what
                nc.vector.tensor_reduce(out=part[:, lo : lo + R_W], in_=q4[:].rearrange("p (j h) -> p h j", j=4)[:, lo : lo + R_W, :], op=ADD, axis=AX)
                if lo + R_W == BANK:
                    owed.append((hf, part[:], state["units"]))

        def finish(c, hf, z):
            if c == "r":
                nc.scalar.activation(out=z, in_=z, func=TANH)
                if quad[hf][1] == 4:
                    part = rp.tile([P, BANK], F32, name="part", tag="part")
                    for lo in range(0, BANK, R_W):
                        vlate.append((hf, quad[hf][0], state["units"], part, lo))
                return
            if c == "g":
                nc.scalar.activation(out=z, in_=z, func=TANH)
                if gpair[hf][1] == 2 and gpair[hf][0] is not acc["g", hf]:
                    q2 = gpair[hf][0]
                    nc.gpsimd.tensor_tensor(out=acc["g", hf][:], in0=acc["g", hf][:], in1=q2[:], op=ADD)
                return
            if c in "gv" and (c, hf) not in started:
                started.append((c, hf))
                nc.scalar.activation(out=acc[c, hf][:], in_=z, func=TANH)
                return
            nc.scalar.activation(out=z, in_=z, func=TANH)
            if c == "g":
                for o in range(0, BANK, G_W):
                    nc.gpsimd.tensor_tensor(out=acc["g", hf][:, o : o + G_W], in0=acc["g", hf][:, o : o + G_W], in1=z[:, o : o + G_W], op=ADD)
            elif c == "v":
                vlate.append((hf, z, state["units"]))
            else:
                owed.append((hf, z, state["units"]))

        def quantise_pooled(g):
            dst = pg[g][:].rearrange("p (b t) -> p b t", t=4)
            src = accT[g][:].rearrange("p (t b) -> p b t", t=4)
            nc.scalar.copy(out=dst, in_=src)
            nc.vector.quantize_mx(out=pc[:, g * P : (g + 1) * P].bitcast(FP8X4), scales=pscale[:, g * P : (g + 1) * P], in_=pg[g][:])

        pooled = []

        def try_pool():
            for g in range(2):
                if left[g] == 0 and g not in pooled:
                    pooled.append(g)
                    quantise_pooled(g)

        arrivals = [("w1", 0), ("w1", 1), ("x", 0), ("x", 1), ("w1", 2), ("w1", 3)] + [("x", n) for n in range(2, NQ)]
        ready = [0]
        for quarter in range(4):
            plain.extend([(quarter + 1, s) for s in anchors("w0", quarter // 2, (quarter % 2) * 2 * P)])
        loads = arrivals[0:7] + [("w0", 0), ("x", 3), ("x", 4), ("w0", 1), ("x", 5), ("w2", 0), ("x", 6), ("x", 7), ("w2", 1), ("x", 8)]
        live = {"x": 0, "w": 0}

        def pump():
            while loads and live["x" if loads[0][0] == "x" else "w"] < (3 if loads[0][0] == "x" else 2):
                live["x" if loads[0][0] == "x" else "w"] += 1
                load(loads.pop(0))

        def prep_and_pump(item, more=None):
            prep(item, more)
            live["x" if item[0] == "x" else "w"] -= 1
            pump()

        events = []
        for item in arrivals:
            units = []
            if item == ("w1", 3):
                units = [(n, 1, FIRST1[n]) for n in range(8)]
            elif item[0] == "x":
                q = item[1]
                for i in range(4):
                    for hf in range(2):
                        c = TABLE[q][2 * i + hf] if q >= 2 else (TABLE[q][i] if hf == 0 else ".")
                        if c != ".":
                            units.append((4 * q + i, hf, c))
            if item == ("x", NQ - 1) or (HF_MAJOR == 1 and len(units) == 8 and item[0] == "x"):
                units = [u for u in units if u[1] == 0] + [u for u in units if u[1] == 1]
            elif HF_MAJOR == 2 and len(units) == 8 and item[0] == "x":
                units = [u for u in units if u[1] == 1] + [u for u in units if u[1] == 0]
            events.append(units)
        n_r = {0: 0, 1: 0}
        for units in events:
            for n, hf, c in units:
                if c == "p":
                    left[hf] += 1
                elif c == "r":
                    n_r[hf] += 1
        for hf in range(2):
            assert n_r[hf] % 4 == 0
            left[hf] += n_r[hf] // 4
        used = sorted(set([(c if c != "d" else "g", hf) for units in events for n, hf, c in units if c in "dgv"]))
        for c, hf in used:
            left[hf] += 2 if c == "g" else 1
        seq = 0
        for units in events:
            for n, hf, c in units:
                seq += 1
                if c in "dgv":
                    last_seq["g" if c == "d" else c, hf] = seq

        nc.sync.dma_start(out=x0n[:], in_=x[:, 0, :])
        pump()
        bank0 = transposes(x0n[:].bitcast(F32))
        nc.vector.tensor_copy(out=x0T[:].rearrange("p (c s b) -> p c s b", c=4, s=2),
                              in_=bank0[:].bitcast(BF16).rearrange("p (c b s) -> p c s b", c=4, s=2))
        prep_and_pump(arrivals[0])
        evacuate(PAT_SHORT)
        halves = [(w, part) for w in (("w0", 0), ("w0", 1), ("w2", 0), ("w2", 1)) for part in range(2)]
        for n in range(len(arrivals)):
            item = arrivals[n]
            units = events[n]
            flush(item)
            long_event = len(units) == 8
            long_run = long_event and n >= P_FROM and n + 1 < len(arrivals)
            if n == 0:
                for s in anchors("w1", 0, 0):
                    s()
            if long_run:
                bridge()
            if n + 1 < len(arrivals):
                prep_and_pump(arrivals[n + 1])
            if long_run:
                bridge()
            if item[0] == "w1" and n > 0:
                for s in anchors("w1", item[1] // 2, (item[1] % 2) * 2 * P):
                    s()
            evacuate(PAT_LONG if long_event else PAT_SHORT)
            if not long_event:
                while side and side[0][1] == "q":
                    do_side()
            copy_products()
            for k in range(len(units)):
                if k in (LAST_RUNS if n == len(arrivals) - 1 else RUN_AT) and len(units) == 8:
                    room = 4 if n < len(arrivals) - 1 else LAST_ROOM
                    if n >= P_FROM:
                        bridge()
                    if halves and n >= HALVES_FROM and k == RUN_AT[0]:
                        more = halves.pop(0)
                        prep_half(more[0], more[1])
                        room = 2
                    pe_sums(room)
                    if n >= P_FROM:
                        bridge()
                    evacuate(PAT_LONG)
                    ready[0] = 8 - len(halves)
                    copy_products()
                    try_pool()
                nn, hf, c = units[k]
                z = unit(nn, hf, "g" if c == "d" else c)
                state["units"] += 1
                for turn in range(R_TURN):
                    if vlate and vlate[0][2] <= state["units"] - V_LAG:
                        late_add()
                if side and k % Q_MOD == Q_AT:
                    urgent = [i for i in range(len(side)) if side[i][0][0] == "x"]
                    do_side(urgent[0] if urgent else 0)
                finish("g" if c == "d" else c, hf, z)
        while vlate:
            late_add()
        side.extend(w2_last)
        while side:
            do_side()
        bridge()
        state["units"] += P_LAG
        pe_sums()
        state["units"] += 100
        pe_sums()
        try_pool()
        while plain:
            bridge()
        copy_products()
        assert len(pooled) == 2
        for o, lo, width in ((0, 0, BANK), (1, 0, 2 * P), (1, 2 * P, 2 * P)):
            ob = ps.tile([P, BANK], F32, name="bank", tag="bank")
            for g in pooled:
                c = slice(g * BANK + lo, g * BANK + lo + width)
                nc.tensor.matmul_mx(out=ob[:, 0:width], lhsT=pc[:, g * P : (g + 1) * P].bitcast(FP8X4), lhsT_scale=pscale[:, g * P : (g + 1) * P],
                                    rhs=wc["w2", o][:, c].bitcast(FP8X4), rhs_scale=ws["w2", o][:, c],
                                    start=(g == pooled[0]), stop=(g == pooled[1]))
            s = slice(o * BANK + lo, o * BANK + lo + width)
            nc.vector.tensor_tensor(out=res[:, s], in0=ob[:, 0:width], in1=prod["w0", o][:, lo : lo + width], op=ADD)
            if lo == 0:
                nc.sync.dma_start(out=out[:, s], in_=res[:, s])
            else:
                nc.scalar.dma_start(out=out[:, s], in_=res[:, s])
